import numpy as np
import ml_dtypes


def mxq(x, axis, fmt="e4m3"):
    dtype, down = {"e4m3": (ml_dtypes.float8_e4m3fn, 7), "e5m2": (ml_dtypes.float8_e5m2, 14)}[fmt]
    v = np.moveaxis(np.asarray(x, np.float32).astype(ml_dtypes.bfloat16).astype(np.float64), axis, -1)
    blocks = v.reshape(v.shape[:-1] + (-1, 32))
    amax = np.abs(blocks).max(-1, keepdims=True)
    byte = np.maximum(np.where(amax > 0, np.frexp(amax)[1] - 1 + 127, 0) - down, 1)
    scale = np.exp2(byte - 127.0)
    codes = (blocks / scale).astype(np.float32).astype(dtype).astype(np.float64)
    return np.moveaxis((codes * scale).reshape(v.shape), -1, axis)


WIDE = False


def mx_kscale(k):
    if not WIDE:
        return np.ones(k)
    levels = np.array([10, -10, 5, -5, 0])
    a = np.random.permutation(np.resize(levels, k // 512 * 4)).reshape(k // 512, 4)
    idx = np.arange(k)
    return np.exp2(a[idx // 512, idx % 128 // 32])


BF16 = ml_dtypes.bfloat16


def bf(x):
    return np.asarray(x, np.float32).astype(BF16)


def f64(x):
    return np.asarray(x).astype(np.float64)


E2M1 = np.array([0.0, 0.5, 1.0, 1.5, 2.0, 3.0, 4.0, 6.0, -0.0, -0.5, -1.0, -1.5, -2.0, -3.0, -4.0, -6.0])


def pack_weight(w, fmt):
    k, n = w.shape
    w = f64(bf(w)).reshape(k // 32, 32, n)
    amax = np.abs(w).max(1)
    if fmt == "e4m3":
        byte = np.frexp(amax)[1] - 1 + 127 - 7
    else:
        mant, ex = np.frexp(amax / 6.0)
        byte = np.where(mant > 0.5, ex, ex - 1) + 127
    byte = np.clip(np.where(amax > 0, byte, 1), 1, 254)
    scaled = (w * np.exp2(127.0 - byte)[:, None, :]).reshape(k, n).astype(np.float32)
    by_word = np.ascontiguousarray(scaled.reshape(k // 512, 128, 4, n).transpose(0, 1, 3, 2))
    if fmt == "e4m3":
        words = by_word.astype(ml_dtypes.float8_e4m3fn).view(np.uint8)
    else:
        c = by_word.astype(ml_dtypes.float4_e2m1fn).view(np.uint8) & 0xF
        words = c[..., 0::2] | (c[..., 1::2] << 4)
    return np.ascontiguousarray(words), np.ascontiguousarray(byte.astype(np.uint8).reshape(k // 512, 16, n))


def unpack_weight(words, scales, fmt):
    g, p, n, _ = words.shape
    if fmt == "e4m3":
        vals = np.ascontiguousarray(words).view(ml_dtypes.float8_e4m3fn).astype(np.float64)
    else:
        nib = np.empty((g, p, n, 4), np.uint8)
        nib[..., 0::2] = words & 0xF
        nib[..., 1::2] = words >> 4
        vals = E2M1[nib]
    vals = vals * np.repeat(np.exp2(scales.astype(np.float64) - 127.0), 8, axis=1)[..., None]
    return vals.transpose(0, 1, 3, 2).reshape(g * 512, n)

def pack4(w):
    words, scales = pack_weight(w, "e2m1")
    return words.reshape(words.shape[0], 128, -1), scales


def unpack4(words, scales):
    return unpack_weight(words.reshape(words.shape[0], 128, -1, 2), scales, "e2m1")


B, F, D, L1, L2, L3 = 320, 8, 32, 256, 256, 512
H2 = L2 // 2
K3 = H2 * F


def interact(h, x0):
    z = h.transpose(0, 2, 1)[:, :, :, None] * x0.transpose(0, 2, 1)[:, :, None, :]
    return z.reshape(z.shape[0], z.shape[1], -1)


def setup_inputs():
    a = mx_kscale(K3).reshape(H2, F)[:, 0]
    h2 = bf(np.maximum(np.random.standard_normal((B, H2, D)) * 0.75, 0.0) * a[None, :, None])
    x0 = bf(np.random.standard_normal((B, F, D)))
    W3_words, W3_scales = pack4(np.random.standard_normal((K3, L3)) / np.sqrt(K3) / np.repeat(a, F)[:, None])
    b3 = bf(np.random.standard_normal(L3) * 0.2)
    return {"h2": h2, "x0": x0, "W3_words": W3_words, "W3_scales": W3_scales, "b3": b3}


def reference(h2, x0, W3_words, W3_scales, b3):
    z = interact(f64(h2), f64(x0))
    y = np.maximum((mxq(z, 2, "e4m3") @ unpack4(W3_words, W3_scales)) + f64(b3), 0.0)
    return y.transpose(0, 2, 1).sum(axis=2)

@@ -1,0 +1,171 @@
+from contextlib import ExitStack
+
+import concourse.mybir as mybir
+from concourse.masks import make_identity
+
+BF16 = mybir.dt.bfloat16
+F32 = mybir.dt.float32
+I32 = mybir.dt.int32
+U8 = mybir.dt.uint8
+U32 = mybir.dt.uint32
+FP8X4 = mybir.dt.float8_e4m3fn_x4
+FP4X4 = mybir.dt.float4_e2m1fn_x4
+ALU = mybir.AluOpType
+
+B, H2, F, D, L3 = 320, 128, 8, 32, 512
+P = 128
+G = 2
+FL = H2 // G
+BT = P // G
+NPT = B // BT
+DCH = 8
+NCH = D // DCH
+NCOL = DCH * BT
+CT = L3 // P
+BLK = 2
+NBLK = (NPT + BLK - 1) // BLK
+
+FLOPS = 2 * B * D * H2 * F * L3
+
+
+def tile_cin_pb_t_kernel(tc, h2, x0, W3_words, W3_scales, b3, out):
+    nc = tc.nc
+    with ExitStack() as ctx:
+        const = ctx.enter_context(tc.tile_pool(name="const", bufs=1))
+        h2_pool = ctx.enter_context(tc.tile_pool(name="h2_pool", bufs=NPT))
+        work = ctx.enter_context(tc.tile_pool(name="work", bufs=3))
+        sums = ctx.enter_context(tc.tile_pool(name="sums", bufs=2))
+        t_psum = ctx.enter_context(tc.psum_pool(name="t_psum", bufs=3))
+        y_psum = ctx.enter_context(tc.psum_pool(name="y_psum", bufs=4))
+        o_psum = ctx.enter_context(tc.psum_pool(name="o_psum", bufs=1))
+
+        x0_sb = const.tile([P, NPT, F * D], BF16)
+        x0_rows = x0.rearrange("(t b) j d -> b t (j d)", b=BT)
+        for g in range(G):
+            nc.sync.dma_start(out=x0_sb[g:P:G, :, :], in_=x0_rows)
+        h2_rows = h2.rearrange("b (g fl) d -> (b g) fl d", g=G)
+        h2_sb = []
+        for pt in range(NPT):
+            h2_tile = h2_pool.tile([P, FL, D], BF16, name="h2_tile")
+            h2_sb.append(h2_tile)
+        nc.sync.dma_start(out=h2_sb[0][:], in_=h2_rows[0:P])
+        w_words = const.tile([P, G, 2 * L3], U8, align_bytes=64)
+        nc.sync.dma_start(out=w_words[:].bitcast(I32), in_=W3_words.bitcast(I32).rearrange("g p n -> p g n"))
+        w_scales = const.tile([P, G, L3], U8, align_bytes=64)
+        nc.vector.memset(w_scales[:].bitcast(I32), 0)
+        for quad in range(4):
+            nc.sync.dma_start(
+                out=w_scales[32 * quad : 32 * quad + 4].bitcast(I32),
+                in_=W3_scales[:, 4 * quad : 4 * quad + 4, :].bitcast(I32).rearrange("g r n -> r g n"),
+            )
+        b_rows = const.tile([P, P], BF16)
+        nc.vector.memset(b_rows[:].bitcast(I32), 0)
+        nc.sync.dma_start(out=b_rows[0:CT, :], in_=b3.rearrange("(r c) -> r c", c=P))
+        for pt in range(1, NPT):
+            nc.sync.dma_start(out=h2_sb[pt][:], in_=h2_rows[pt * P : (pt + 1) * P])
+
+        ident = const.tile([P, P], F32)
+        make_identity(nc, ident[:])
+
+        b_rows_f = const.tile([P, P], F32)
+        nc.vector.tensor_copy(out=b_rows_f[:], in_=b_rows[:])
+        b_cols = o_psum.tile([P, P], F32, tag="o")
+        nc.tensor.transpose(b_cols[:], b_rows_f[:], ident[:])
+        neg_b = const.tile([P, CT], F32)
+        nc.vector.tensor_scalar(out=neg_b[:], in0=b_cols[:, 0:CT], scalar1=-1.0, scalar2=None, op0=ALU.mult)
+        d_times_b = const.tile([P, CT], F32)
+        nc.vector.tensor_scalar(out=d_times_b[:], in0=b_cols[:, 0:CT], scalar1=float(D), scalar2=None, op0=ALU.mult)
+
+        x0_pairs = const.tile([P, NPT, D, 2, 2, 2], BF16)
+        x0_view = x0_sb[:].rearrange("p t (jh u e d) -> p t d u jh e", jh=2, u=2, e=2)
+        for u in range(2):
+            nc.vector.tensor_copy(out=x0_pairs[:, :, :, u], in_=x0_view[:, :, :, u])
+
+        pooled = const.tile([P, CT, NBLK * P], F32)
+        nc.vector.memset(pooled[:].bitcast(I32), 0)
+
+        for pt in range(NPT):
+            acc = sums.tile([P, CT, DCH, BT], F32)
+            for ch in range(NCH):
+                d0 = ch * DCH
+                h2_twice = work.tile([P, DCH, FL, 2], BF16)
+                nc.scalar.copy(
+                    out=h2_twice[:],
+                    in_=h2_sb[pt][:, :, d0 : d0 + DCH].rearrange("p fl d -> p d fl").unsqueeze(3).to_broadcast([P, DCH, FL, 2]),
+                )
+                z_rows = work.tile([P, DCH, 2, FL, 2, 2], BF16)
+                for u in range(2):
+                    nc.vector.tensor_tensor(
+                        out=z_rows[:, :, u],
+                        in0=h2_twice[:].unsqueeze(3).to_broadcast([P, DCH, FL, 2, 2]),
+                        in1=x0_pairs[:, pt, d0 : d0 + DCH, u].unsqueeze(2).to_broadcast([P, DCH, FL, 2, 2]),
+                        op=ALU.mult,
+                    )
+                grouped = work.tile([P, G, NCOL, 4], BF16, align_bytes=64)
+                grouped_words = grouped[:].bitcast(F32)
+                for half in range(DCH // 2):
+                    z_cols = t_psum.tile([P, 2, 2, BT, G], F32)
+                    for dd in range(2):
+                        for u in range(2):
+                            nc.tensor.transpose(
+                                z_cols[:, dd, u].rearrange("p b g -> p (b g)"),
+                                z_rows[:, 2 * half + dd, u].rearrange("p fl jh e -> p (fl jh e)").bitcast(F32),
+                                ident[:],
+                            )
+                    for g in range(G):
+                        nc.scalar.copy(
+                            out=grouped_words[:, g, 2 * BT * half : 2 * BT * (half + 1), :].rearrange(
+                                "p (dd b) u -> p dd b u", dd=2
+                            ),
+                            in_=z_cols[:, :, :, :, g].rearrange("p dd u b -> p dd b u"),
+                        )
+                z_codes = work.tile([P, G, NCOL], U32, align_bytes=64)
+                z_scales = work.tile([P, G, NCOL], U8, align_bytes=64)
+                nc.vector.quantize_mx(
+                    out=z_codes[:].rearrange("p g n -> p (g n)").bitcast(FP8X4),
+                    scales=z_scales[:].rearrange("p g n -> p (g n)"),
+                    in_=grouped[:].rearrange("p g n t -> p (g n t)"),
+                )
+                for ct in range(CT):
+                    y = y_psum.tile([P, NCOL], F32)
+                    for g in range(G):
+                        nc.tensor.matmul_mx(
+                            out=y[:],
+                            lhsT=w_words[:, g, 2 * P * ct : 2 * P * (ct + 1)].bitcast(FP4X4),
+                            lhsT_scale=w_scales[:, g, P * ct : P * (ct + 1)],
+                            rhs=z_codes[:, g, :].bitcast(FP8X4),
+                            rhs_scale=z_scales[:, g, :],
+                            start=(g == 0),
+                            stop=(g == G - 1),
+                        )
+                    acc_ct = acc[:, ct].rearrange("p d b -> p (d b)")
+                    if ch == 0:
+                        nc.vector.tensor_scalar(
+                            out=acc_ct, in0=y[:], scalar1=neg_b[:, ct : ct + 1], scalar2=None, op0=ALU.max
+                        )
+                    else:
+                        nc.vector.scalar_tensor_tensor(
+                            out=acc_ct, in0=y[:], scalar=neg_b[:, ct : ct + 1], in1=acc_ct, op0=ALU.max, op1=ALU.add
+                        )
+            fold4 = sums.tile([P, CT, 4, BT], F32)
+            nc.vector.tensor_tensor(out=fold4[:], in0=acc[:, :, 0:4, :], in1=acc[:, :, 4:8, :], op=ALU.add)
+            fold2 = sums.tile([P, CT, 2, BT], F32)
+            nc.vector.tensor_tensor(out=fold2[:], in0=fold4[:, :, 0:2, :], in1=fold4[:, :, 2:4, :], op=ALU.add)
+            for ct in range(CT):
+                nc.vector.scalar_tensor_tensor(
+                    out=pooled[:, ct, pt * BT : (pt + 1) * BT],
+                    in0=fold2[:, ct, 0, :],
+                    scalar=d_times_b[:, ct : ct + 1],
+                    in1=fold2[:, ct, 1, :],
+                    op0=ALU.add,
+                    op1=ALU.add,
+                )
+            if pt % BLK == BLK - 1 or pt == NPT - 1:
+                blk = pt // BLK
+                rows = min(P, B - blk * P)
+                out_ps = o_psum.tile([P, L3], F32, tag="o")
+                for ct in range(CT):
+                    nc.tensor.transpose(out_ps[:, ct * P : (ct + 1) * P], pooled[:, ct, blk * P : (blk + 1) * P], ident[:])
+                out_sb = sums.tile([P, L3], F32)
+                nc.scalar.copy(out=out_sb[:], in_=out_ps[:])
+                nc.sync.dma_start(out=out[blk * P : blk * P + rows, :], in_=out_sb[0:rows, :])

@@ -11,6 +11,7 @@ U32 = mybir.dt.uint32
 FP8X4 = mybir.dt.float8_e4m3fn_x4
 FP4X4 = mybir.dt.float4_e2m1fn_x4
 ALU = mybir.AluOpType
+RELU = mybir.ActivationFunctionType.Relu
 
 B, H2, F, D, L3 = 320, 128, 8, 32, 512
 P = 128
@@ -23,7 +24,6 @@ NCH = D // DCH
 NCOL = DCH * BT
 CT = L3 // P
 BLK = 2
-NBLK = (NPT + BLK - 1) // BLK
 
 FLOPS = 2 * B * D * H2 * F * L3
 
@@ -36,8 +36,8 @@ def tile_cin_pb_t_kernel(tc, h2, x0, W3_words, W3_scales, b3, out):
         work = ctx.enter_context(tc.tile_pool(name="work", bufs=3))
         sums = ctx.enter_context(tc.tile_pool(name="sums", bufs=2))
         t_psum = ctx.enter_context(tc.psum_pool(name="t_psum", bufs=3))
-        y_psum = ctx.enter_context(tc.psum_pool(name="y_psum", bufs=4))
-        o_psum = ctx.enter_context(tc.psum_pool(name="o_psum", bufs=1))
+        y_psum = ctx.enter_context(tc.psum_pool(name="y_psum", bufs=3))
+        r_psum = ctx.enter_context(tc.psum_pool(name="r_psum", bufs=1))
 
         x0_sb = const.tile([P, NPT, F * D], BF16)
         x0_rows = x0.rearrange("(t b) j d -> b t (j d)", b=BT)
@@ -69,23 +69,31 @@ def tile_cin_pb_t_kernel(tc, h2, x0, W3_words, W3_scales, b3, out):
 
         b_rows_f = const.tile([P, P], F32)
         nc.vector.tensor_copy(out=b_rows_f[:], in_=b_rows[:])
-        b_cols = o_psum.tile([P, P], F32, tag="o")
+        b_cols = y_psum.tile([P, P], F32, tag="y")
         nc.tensor.transpose(b_cols[:], b_rows_f[:], ident[:])
+        bias = const.tile([P, CT], F32)
+        nc.vector.tensor_copy(out=bias[:], in_=b_cols[:, 0:CT])
         neg_b = const.tile([P, CT], F32)
         nc.vector.tensor_scalar(out=neg_b[:], in0=b_cols[:, 0:CT], scalar1=-1.0, scalar2=None, op0=ALU.mult)
-        d_times_b = const.tile([P, CT], F32)
-        nc.vector.tensor_scalar(out=d_times_b[:], in0=b_cols[:, 0:CT], scalar1=float(D), scalar2=None, op0=ALU.mult)
+        nch_b = const.tile([P, CT], F32)
+        nc.vector.tensor_scalar(out=nch_b[:], in0=b_cols[:, 0:CT], scalar1=float(NCH), scalar2=None, op0=ALU.mult)
+
+        fold = []
+        for s in range(BLK):
+            fold_s = const.tile([P, P], F32, name="fold%d" % s)
+            nc.vector.memset(fold_s[:].bitcast(I32), 0)
+            nc.vector.tensor_tensor(out=fold_s[:, BT * s : BT * (s + 1)], in0=ident[:, 0:BT], in1=ident[:, BT:P], op=ALU.add)
+            fold.append(fold_s)
 
         x0_pairs = const.tile([P, NPT, D, 2, 2, 2], BF16)
         x0_view = x0_sb[:].rearrange("p t (jh u e d) -> p t d u jh e", jh=2, u=2, e=2)
         for u in range(2):
             nc.vector.tensor_copy(out=x0_pairs[:, :, :, u], in_=x0_view[:, :, :, u])
 
-        pooled = const.tile([P, CT, NBLK * P], F32)
-        nc.vector.memset(pooled[:].bitcast(I32), 0)
-
+        turned_sb = []
         for pt in range(NPT):
-            acc = sums.tile([P, CT, DCH, BT], F32)
+            acc = sums.tile([P, CT // 2, NCOL], F32)
+            turned = [r_psum.tile([P, 2, P], F32, name="turned%d" % j) for j in range(CT // 2)]
             for ch in range(NCH):
                 d0 = ch * DCH
                 h2_twice = work.tile([P, DCH, FL, 2], BF16)
@@ -127,7 +135,7 @@ def tile_cin_pb_t_kernel(tc, h2, x0, W3_words, W3_scales, b3, out):
                     in_=grouped[:].rearrange("p g n t -> p (g n t)"),
                 )
                 for ct in range(CT):
-                    y = y_psum.tile([P, NCOL], F32)
+                    y = y_psum.tile([P, NCOL], F32, tag="y")
                     for g in range(G):
                         nc.tensor.matmul_mx(
                             out=y[:],
@@ -138,34 +146,60 @@ def tile_cin_pb_t_kernel(tc, h2, x0, W3_words, W3_scales, b3, out):
                             start=(g == 0),
                             stop=(g == G - 1),
                         )
-                    acc_ct = acc[:, ct].rearrange("p d b -> p (d b)")
-                    if ch == 0:
-                        nc.vector.tensor_scalar(
-                            out=acc_ct, in0=y[:], scalar1=neg_b[:, ct : ct + 1], scalar2=None, op0=ALU.max
-                        )
+                    if ct % 2 == 0:
+                        acc_ct = acc[:, ct // 2, :]
+                        if ch == 0:
+                            nc.vector.tensor_scalar(
+                                out=acc_ct,
+                                in0=y[:],
+                                scalar1=neg_b[:, ct : ct + 1],
+                                scalar2=nch_b[:, ct : ct + 1],
+                                op0=ALU.max,
+                                op1=ALU.add,
+                            )
+                        else:
+                            nc.vector.scalar_tensor_tensor(
+                                out=acc_ct, in0=y[:], scalar=neg_b[:, ct : ct + 1], in1=acc_ct, op0=ALU.max, op1=ALU.add
+                            )
                     else:
-                        nc.vector.scalar_tensor_tensor(
-                            out=acc_ct, in0=y[:], scalar=neg_b[:, ct : ct + 1], in1=acc_ct, op0=ALU.max, op1=ALU.add
-                        )
-            fold4 = sums.tile([P, CT, 4, BT], F32)
-            nc.vector.tensor_tensor(out=fold4[:], in0=acc[:, :, 0:4, :], in1=acc[:, :, 4:8, :], op=ALU.add)
-            fold2 = sums.tile([P, CT, 2, BT], F32)
-            nc.vector.tensor_tensor(out=fold2[:], in0=fold4[:, :, 0:2, :], in1=fold4[:, :, 2:4, :], op=ALU.add)
-            for ct in range(CT):
-                nc.vector.scalar_tensor_tensor(
-                    out=pooled[:, ct, pt * BT : (pt + 1) * BT],
-                    in0=fold2[:, ct, 0, :],
-                    scalar=d_times_b[:, ct : ct + 1],
-                    in1=fold2[:, ct, 1, :],
-                    op0=ALU.add,
-                    op1=ALU.add,
-                )
+                        y_relu = work.tile([P, NCOL], F32)
+                        nc.scalar.activation(out=y_relu[:], in_=y[:], func=RELU, bias=bias[:, ct : ct + 1], scale=1.0)
+                        for q in range(NCOL // P):
+                            nc.tensor.matmul(
+                                out=turned[ct // 2][:, 1, :],
+                                lhsT=y_relu[:, q * P : (q + 1) * P],
+                                rhs=ident[:],
+                                is_transpose=True,
+                                start=(ch == 0 and q == 0),
+                                stop=(ch == NCH - 1 and q == NCOL // P - 1),
+                            )
+            for j in range(CT // 2):
+                for q in range(NCOL // P):
+                    nc.tensor.matmul(
+                        out=turned[j][:, 0, :],
+                        lhsT=acc[:, j, q * P : (q + 1) * P],
+                        rhs=ident[:],
+                        is_transpose=True,
+                        start=(q == 0),
+                        stop=(q == NCOL // P - 1),
+                    )
+            turned_tile = sums.tile([P, CT // 2, 2 * P], F32, name="turned_tile")
+            for j in range(CT // 2):
+                nc.vector.tensor_copy(out=turned_tile[:, j, :], in_=turned[j][:].rearrange("p h c -> p (h c)"))
+            turned_sb.append(turned_tile)
             if pt % BLK == BLK - 1 or pt == NPT - 1:
                 blk = pt // BLK
                 rows = min(P, B - blk * P)
-                out_ps = o_psum.tile([P, L3], F32, tag="o")
-                for ct in range(CT):
-                    nc.tensor.transpose(out_ps[:, ct * P : (ct + 1) * P], pooled[:, ct, blk * P : (blk + 1) * P], ident[:])
+                out_ps = y_psum.tile([P, L3], F32, tag="y")
+                for s in range(len(turned_sb)):
+                    nc.tensor.matmul(
+                        out=out_ps[:],
+                        lhsT=fold[s][:],
+                        rhs=turned_sb[s][:].rearrange("p j c -> p (j c)"),
+                        start=(s == 0),
+                        stop=(s == len(turned_sb) - 1),
+                    )
+                turned_sb = []
                 out_sb = sums.tile([P, L3], F32)
                 nc.scalar.copy(out=out_sb[:], in_=out_ps[:])
                 nc.sync.dma_start(out=out[blk * P : blk * P + rows, :], in_=out_sb[0:rows, :])

@@ -21,6 +21,7 @@ BT = P // G
 NPT = B // BT
 DCH = 8
 NCH = D // DCH
+NCHUNK = NPT * NCH
 NCOL = DCH * BT
 CT = L3 // P
 BLK = 2
@@ -67,6 +68,11 @@ def tile_cin_pb_t_kernel(tc, h2, x0, W3_words, W3_scales, b3, out):
         ident = const.tile([P, P], F32)
         make_identity(nc, ident[:])
 
+        x0_pairs = const.tile([P, NPT, D, 2, 2, 2], BF16)
+        x0_view = x0_sb[:].rearrange("p t (jh u e d) -> p t d u jh e", jh=2, u=2, e=2)
+        for u in range(2):
+            nc.vector.tensor_copy(out=x0_pairs[:, :, :, u], in_=x0_view[:, :, :, u])
+
         b_rows_f = const.tile([P, P], F32)
         nc.vector.tensor_copy(out=b_rows_f[:], in_=b_rows[:])
         b_cols = y_psum.tile([P, P], F32, tag="y")
@@ -85,121 +91,187 @@ def tile_cin_pb_t_kernel(tc, h2, x0, W3_words, W3_scales, b3, out):
             nc.vector.tensor_tensor(out=fold_s[:, BT * s : BT * (s + 1)], in0=ident[:, 0:BT], in1=ident[:, BT:P], op=ALU.add)
             fold.append(fold_s)
 
-        x0_pairs = const.tile([P, NPT, D, 2, 2, 2], BF16)
-        x0_view = x0_sb[:].rearrange("p t (jh u e d) -> p t d u jh e", jh=2, u=2, e=2)
-        for u in range(2):
-            nc.vector.tensor_copy(out=x0_pairs[:, :, :, u], in_=x0_view[:, :, :, u])
+        h2_twice = {}
+        z_rows = {}
+        z_cols = {}
+        grouped = {}
+        z_codes = {}
+        z_scales = {}
+        y = {}
+        y_relu = {}
+        acc = {}
+        turned = {}
+        turned_sb = {}
 
-        turned_sb = []
-        for pt in range(NPT):
-            acc = sums.tile([P, CT // 2, NCOL], F32)
-            turned = [r_psum.tile([P, 2, P], F32, name="turned%d" % j) for j in range(CT // 2)]
-            for ch in range(NCH):
-                d0 = ch * DCH
-                h2_twice = work.tile([P, DCH, FL, 2], BF16)
-                nc.scalar.copy(
-                    out=h2_twice[:],
-                    in_=h2_sb[pt][:, :, d0 : d0 + DCH].rearrange("p fl d -> p d fl").unsqueeze(3).to_broadcast([P, DCH, FL, 2]),
-                )
-                z_rows = work.tile([P, DCH, 2, FL, 2, 2], BF16)
+        def double_h2(c):
+            d0 = (c % NCH) * DCH
+            h2_twice[c] = work.tile([P, DCH, FL, 2], BF16, name="h2_twice")
+            nc.scalar.copy(
+                out=h2_twice[c][:],
+                in_=h2_sb[c // NCH][:, :, d0 : d0 + DCH]
+                .rearrange("p fl d -> p d fl")
+                .unsqueeze(3)
+                .to_broadcast([P, DCH, FL, 2]),
+            )
+
+        def multiply(c, u):
+            d0 = (c % NCH) * DCH
+            if u == 0:
+                z_rows[c] = work.tile([P, DCH, 2, FL, 2, 2], BF16, name="z_rows")
+            nc.vector.tensor_tensor(
+                out=z_rows[c][:, :, u],
+                in0=h2_twice[c][:].unsqueeze(3).to_broadcast([P, DCH, FL, 2, 2]),
+                in1=x0_pairs[:, c // NCH, d0 : d0 + DCH, u].unsqueeze(2).to_broadcast([P, DCH, FL, 2, 2]),
+                op=ALU.mult,
+            )
+
+        def turn_z(c, half):
+            for pair in (2 * half, 2 * half + 1):
+                z_cols[c, pair] = t_psum.tile([P, 2, 2, BT, G], F32, name="z_cols")
                 for u in range(2):
-                    nc.vector.tensor_tensor(
-                        out=z_rows[:, :, u],
-                        in0=h2_twice[:].unsqueeze(3).to_broadcast([P, DCH, FL, 2, 2]),
-                        in1=x0_pairs[:, pt, d0 : d0 + DCH, u].unsqueeze(2).to_broadcast([P, DCH, FL, 2, 2]),
-                        op=ALU.mult,
-                    )
-                grouped = work.tile([P, G, NCOL, 4], BF16, align_bytes=64)
-                grouped_words = grouped[:].bitcast(F32)
-                for half in range(DCH // 2):
-                    z_cols = t_psum.tile([P, 2, 2, BT, G], F32)
                     for dd in range(2):
-                        for u in range(2):
-                            nc.tensor.transpose(
-                                z_cols[:, dd, u].rearrange("p b g -> p (b g)"),
-                                z_rows[:, 2 * half + dd, u].rearrange("p fl jh e -> p (fl jh e)").bitcast(F32),
-                                ident[:],
-                            )
-                    for g in range(G):
-                        nc.scalar.copy(
-                            out=grouped_words[:, g, 2 * BT * half : 2 * BT * (half + 1), :].rearrange(
-                                "p (dd b) u -> p dd b u", dd=2
-                            ),
-                            in_=z_cols[:, :, :, :, g].rearrange("p dd u b -> p dd b u"),
+                        nc.tensor.transpose(
+                            z_cols[c, pair][:, u, dd].rearrange("p b g -> p (b g)"),
+                            z_rows[c][:, 2 * pair + dd, u].rearrange("p fl jh e -> p (fl jh e)").bitcast(F32),
+                            ident[:],
                         )
-                z_codes = work.tile([P, G, NCOL], U32, align_bytes=64)
-                z_scales = work.tile([P, G, NCOL], U8, align_bytes=64)
-                nc.vector.quantize_mx(
-                    out=z_codes[:].rearrange("p g n -> p (g n)").bitcast(FP8X4),
-                    scales=z_scales[:].rearrange("p g n -> p (g n)"),
-                    in_=grouped[:].rearrange("p g n t -> p (g n t)"),
+
+        def regroup(c, half):
+            if half == 0:
+                grouped[c] = work.tile([P, G, NCOL, 4], BF16, name="grouped", align_bytes=64)
+            words = grouped[c][:].bitcast(F32)
+            for pair in (2 * half, 2 * half + 1):
+                nc.scalar.copy(
+                    out=words[:, :, 2 * BT * pair : 2 * BT * (pair + 1), :],
+                    in_=z_cols[c, pair][:].rearrange("p u dd b g -> p g (dd b) u"),
                 )
-                for ct in range(CT):
-                    y = y_psum.tile([P, NCOL], F32, tag="y")
-                    for g in range(G):
-                        nc.tensor.matmul_mx(
-                            out=y[:],
-                            lhsT=w_words[:, g, 2 * P * ct : 2 * P * (ct + 1)].bitcast(FP4X4),
-                            lhsT_scale=w_scales[:, g, P * ct : P * (ct + 1)],
-                            rhs=z_codes[:, g, :].bitcast(FP8X4),
-                            rhs_scale=z_scales[:, g, :],
-                            start=(g == 0),
-                            stop=(g == G - 1),
-                        )
-                    if ct % 2 == 0:
-                        acc_ct = acc[:, ct // 2, :]
-                        if ch == 0:
-                            nc.vector.tensor_scalar(
-                                out=acc_ct,
-                                in0=y[:],
-                                scalar1=neg_b[:, ct : ct + 1],
-                                scalar2=nch_b[:, ct : ct + 1],
-                                op0=ALU.max,
-                                op1=ALU.add,
-                            )
-                        else:
-                            nc.vector.scalar_tensor_tensor(
-                                out=acc_ct, in0=y[:], scalar=neg_b[:, ct : ct + 1], in1=acc_ct, op0=ALU.max, op1=ALU.add
-                            )
-                    else:
-                        y_relu = work.tile([P, NCOL], F32)
-                        nc.scalar.activation(out=y_relu[:], in_=y[:], func=RELU, bias=bias[:, ct : ct + 1], scale=1.0)
-                        for q in range(NCOL // P):
-                            nc.tensor.matmul(
-                                out=turned[ct // 2][:, 1, :],
-                                lhsT=y_relu[:, q * P : (q + 1) * P],
-                                rhs=ident[:],
-                                is_transpose=True,
-                                start=(ch == 0 and q == 0),
-                                stop=(ch == NCH - 1 and q == NCOL // P - 1),
-                            )
+
+        def quantise(c):
+            z_codes[c] = work.tile([P, G, NCOL], U32, name="z_codes", align_bytes=64)
+            z_scales[c] = work.tile([P, G, NCOL], U8, name="z_scales", align_bytes=64)
+            nc.vector.quantize_mx(
+                out=z_codes[c][:].rearrange("p g n -> p (g n)").bitcast(FP8X4),
+                scales=z_scales[c][:].rearrange("p g n -> p (g n)"),
+                in_=grouped[c][:].rearrange("p g n t -> p (g n t)"),
+            )
+
+        def multiply_mx(c, ct):
+            y[c, ct] = y_psum.tile([P, NCOL], F32, name="y", tag="y")
+            for g in range(G):
+                nc.tensor.matmul_mx(
+                    out=y[c, ct][:],
+                    lhsT=w_words[:, g, 2 * P * ct : 2 * P * (ct + 1)].bitcast(FP4X4),
+                    lhsT_scale=w_scales[:, g, P * ct : P * (ct + 1)],
+                    rhs=z_codes[c][:, g, :].bitcast(FP8X4),
+                    rhs_scale=z_scales[c][:, g, :],
+                    start=(g == 0),
+                    stop=(g == G - 1),
+                )
+
+        def relu_add_vector(c, ct):
+            pt = c // NCH
+            if c % NCH == 0 and ct == 0:
+                acc[pt] = sums.tile([P, CT // 2, NCOL], F32, name="acc")
+            acc_ct = acc[pt][:, ct // 2, :]
+            if c % NCH == 0:
+                nc.vector.tensor_scalar(
+                    out=acc_ct,
+                    in0=y[c, ct][:],
+                    scalar1=neg_b[:, ct : ct + 1],
+                    scalar2=nch_b[:, ct : ct + 1],
+                    op0=ALU.max,
+                    op1=ALU.add,
+                )
+            else:
+                nc.vector.scalar_tensor_tensor(
+                    out=acc_ct, in0=y[c, ct][:], scalar=neg_b[:, ct : ct + 1], in1=acc_ct, op0=ALU.max, op1=ALU.add
+                )
+
+        def relu_scalar(c, ct):
+            y_relu[c, ct] = work.tile([P, NCOL], F32, name="y_relu")
+            nc.scalar.activation(out=y_relu[c, ct][:], in_=y[c, ct][:], func=RELU, bias=bias[:, ct : ct + 1], scale=1.0)
+
+        def turn_and_add(dest, columns, first, last):
+            for q in range(NCOL // P):
+                nc.tensor.matmul(
+                    out=dest,
+                    lhsT=columns[:, q * P : (q + 1) * P],
+                    rhs=ident[:],
+                    is_transpose=True,
+                    start=(first and q == 0),
+                    stop=(last and q == NCOL // P - 1),
+                )
+
+        def turn_and_add_scalar(c, ct):
+            pt = c // NCH
+            if c % NCH == 0:
+                turned[pt, ct // 2] = r_psum.tile([P, 2, P], F32, name="turned%d" % (ct // 2))
+            turn_and_add(turned[pt, ct // 2][:, 1, :], y_relu[c, ct], c % NCH == 0, c % NCH == NCH - 1)
+
+        def turn_and_add_vector(pt):
             for j in range(CT // 2):
-                for q in range(NCOL // P):
-                    nc.tensor.matmul(
-                        out=turned[j][:, 0, :],
-                        lhsT=acc[:, j, q * P : (q + 1) * P],
-                        rhs=ident[:],
-                        is_transpose=True,
-                        start=(q == 0),
-                        stop=(q == NCOL // P - 1),
-                    )
-            turned_tile = sums.tile([P, CT // 2, 2 * P], F32, name="turned_tile")
+                turn_and_add(turned[pt, j][:, 0, :], acc[pt][:, j, :], True, True)
+
+        def save_turned(pt):
+            turned_sb[pt] = sums.tile([P, CT // 2, 2 * P], F32, name="turned_sb")
             for j in range(CT // 2):
-                nc.vector.tensor_copy(out=turned_tile[:, j, :], in_=turned[j][:].rearrange("p h c -> p (h c)"))
-            turned_sb.append(turned_tile)
-            if pt % BLK == BLK - 1 or pt == NPT - 1:
-                blk = pt // BLK
-                rows = min(P, B - blk * P)
-                out_ps = y_psum.tile([P, L3], F32, tag="y")
-                for s in range(len(turned_sb)):
-                    nc.tensor.matmul(
-                        out=out_ps[:],
-                        lhsT=fold[s][:],
-                        rhs=turned_sb[s][:].rearrange("p j c -> p (j c)"),
-                        start=(s == 0),
-                        stop=(s == len(turned_sb) - 1),
-                    )
-                turned_sb = []
-                out_sb = sums.tile([P, L3], F32)
-                nc.scalar.copy(out=out_sb[:], in_=out_ps[:])
-                nc.sync.dma_start(out=out[blk * P : blk * P + rows, :], in_=out_sb[0:rows, :])
+                nc.vector.tensor_copy(out=turned_sb[pt][:, j, :], in_=turned[pt, j][:].rearrange("p h c -> p (h c)"))
+
+        def store_block(blk):
+            tiles = list(range(blk * BLK, min((blk + 1) * BLK, NPT)))
+            out_ps = y_psum.tile([P, L3], F32, name="out_ps", tag="y")
+            for s in range(len(tiles)):
+                nc.tensor.matmul(
+                    out=out_ps[:],
+                    lhsT=fold[s][:],
+                    rhs=turned_sb[tiles[s]][:].rearrange("p j c -> p (j c)"),
+                    start=(s == 0),
+                    stop=(s == len(tiles) - 1),
+                )
+            out_sb = sums.tile([P, L3], F32, name="out_sb")
+            nc.scalar.copy(out=out_sb[:], in_=out_ps[:])
+            rows = BT * len(tiles)
+            nc.sync.dma_start(out=out[blk * P : blk * P + rows, :], in_=out_sb[0:rows, :])
+
+        def live(c):
+            return 0 <= c < NCHUNK
+
+        with tc.manual_schedule():
+            for s in range(-4, NCHUNK + 1):
+                tile_done = live(s - 1) and s % NCH == 0
+                if live(s + 2):
+                    turn_z(s + 2, 0)
+                if live(s - 1):
+                    turn_and_add_scalar(s - 1, 3)
+                if tile_done:
+                    turn_and_add_vector((s - 1) // NCH)
+                if live(s + 2):
+                    regroup(s + 2, 0)
+                if live(s + 1):
+                    quantise(s + 1)
+                if live(s + 3):
+                    multiply(s + 3, 0)
+                if tile_done:
+                    save_turned((s - 1) // NCH)
+                if live(s):
+                    multiply_mx(s, 0)
+                    multiply_mx(s, 1)
+                    relu_add_vector(s, 0)
+                    relu_scalar(s, 1)
+                if live(s + 2):
+                    turn_z(s + 2, 1)
+                if live(s):
+                    turn_and_add_scalar(s, 1)
+                if tile_done and ((s - 1) // NCH % BLK == BLK - 1 or s == NCHUNK):
+                    store_block((s - 1) // NCH // BLK)
+                if live(s + 2):
+                    regroup(s + 2, 1)
+                if live(s + 3):
+                    multiply(s + 3, 1)
+                if live(s):
+                    multiply_mx(s, 2)
+                    multiply_mx(s, 3)
+                    relu_add_vector(s, 2)
+                    relu_scalar(s, 3)
+                if live(s + 4):
+                    double_h2(s + 4)

@@ -188,7 +188,7 @@ def tile_cin_pb_t_kernel(tc, h2, x0, W3_words, W3_scales, b3, out):
                 )
 
         def relu_scalar(c, ct):
-            y_relu[c, ct] = work.tile([P, NCOL], F32, name="y_relu")
+            y_relu[c, ct] = work.tile([P, NCOL], F32, name="y_relu", bufs=4)
             nc.scalar.activation(out=y_relu[c, ct][:], in_=y[c, ct][:], func=RELU, bias=bias[:, ct : ct + 1], scale=1.0)
 
         def turn_and_add(dest, columns, first, last):
@@ -242,6 +242,7 @@ def tile_cin_pb_t_kernel(tc, h2, x0, W3_words, W3_scales, b3, out):
                 if live(s + 2):
                     turn_z(s + 2, 0)
                 if live(s - 1):
+                    turn_and_add_scalar(s - 1, 1)
                     turn_and_add_scalar(s - 1, 3)
                 if tile_done:
                     turn_and_add_vector((s - 1) // NCH)
@@ -260,8 +261,6 @@ def tile_cin_pb_t_kernel(tc, h2, x0, W3_words, W3_scales, b3, out):
                     relu_scalar(s, 1)
                 if live(s + 2):
                     turn_z(s + 2, 1)
-                if live(s):
-                    turn_and_add_scalar(s, 1)
                 if tile_done and ((s - 1) // NCH % BLK == BLK - 1 or s == NCHUNK):
                     store_block((s - 1) // NCH // BLK)
                 if live(s + 2):

@@ -40,18 +40,21 @@ def tile_cin_pb_t_kernel(tc, h2, x0, W3_words, W3_scales, b3, out):
         y_psum = ctx.enter_context(tc.psum_pool(name="y_psum", bufs=3))
         r_psum = ctx.enter_context(tc.psum_pool(name="r_psum", bufs=1))
 
-        x0_sb = const.tile([P, NPT, F * D], BF16)
-        x0_rows = x0.rearrange("(t b) j d -> b t (j d)", b=BT)
-        for g in range(G):
-            nc.sync.dma_start(out=x0_sb[g:P:G, :, :], in_=x0_rows)
+        ctx.enter_context(tc.manual_schedule())
+
         h2_rows = h2.rearrange("b (g fl) d -> (b g) fl d", g=G)
         h2_sb = []
         for pt in range(NPT):
             h2_tile = h2_pool.tile([P, FL, D], BF16, name="h2_tile")
             h2_sb.append(h2_tile)
         nc.sync.dma_start(out=h2_sb[0][:], in_=h2_rows[0:P])
+        x0_sb = const.tile([P, NPT, F * D], BF16)
+        x0_rows = x0.rearrange("(t b) j d -> b t (j d)", b=BT)
+        for g in range(G):
+            nc.scalar.dma_start(out=x0_sb[g:P:G, :, :], in_=x0_rows)
         w_words = const.tile([P, G, 2 * L3], U8, align_bytes=64)
         nc.sync.dma_start(out=w_words[:].bitcast(I32), in_=W3_words.bitcast(I32).rearrange("g p n -> p g n"))
+        nc.sync.dma_start(out=h2_sb[1][:], in_=h2_rows[P : 2 * P])
         w_scales = const.tile([P, G, L3], U8, align_bytes=64)
         nc.vector.memset(w_scales[:].bitcast(I32), 0)
         for quad in range(4):
@@ -62,7 +65,7 @@ def tile_cin_pb_t_kernel(tc, h2, x0, W3_words, W3_scales, b3, out):
         b_rows = const.tile([P, P], BF16)
         nc.vector.memset(b_rows[:].bitcast(I32), 0)
         nc.sync.dma_start(out=b_rows[0:CT, :], in_=b3.rearrange("(r c) -> r c", c=P))
-        for pt in range(1, NPT):
+        for pt in range(2, NPT):
             nc.sync.dma_start(out=h2_sb[pt][:], in_=h2_rows[pt * P : (pt + 1) * P])
 
         ident = const.tile([P, P], F32)
@@ -74,15 +77,19 @@ def tile_cin_pb_t_kernel(tc, h2, x0, W3_words, W3_scales, b3, out):
             nc.vector.tensor_copy(out=x0_pairs[:, :, :, u], in_=x0_view[:, :, :, u])
 
         b_rows_f = const.tile([P, P], F32)
-        nc.vector.tensor_copy(out=b_rows_f[:], in_=b_rows[:])
         b_cols = y_psum.tile([P, P], F32, tag="y")
-        nc.tensor.transpose(b_cols[:], b_rows_f[:], ident[:])
         bias = const.tile([P, CT], F32)
-        nc.vector.tensor_copy(out=bias[:], in_=b_cols[:, 0:CT])
         neg_b = const.tile([P, CT], F32)
-        nc.vector.tensor_scalar(out=neg_b[:], in0=b_cols[:, 0:CT], scalar1=-1.0, scalar2=None, op0=ALU.mult)
         nch_b = const.tile([P, CT], F32)
-        nc.vector.tensor_scalar(out=nch_b[:], in0=b_cols[:, 0:CT], scalar1=float(NCH), scalar2=None, op0=ALU.mult)
+
+        def turn_bias():
+            nc.vector.tensor_copy(out=b_rows_f[:], in_=b_rows[:])
+            nc.tensor.transpose(b_cols[:], b_rows_f[:], ident[:])
+
+        def save_bias():
+            nc.vector.tensor_copy(out=bias[:], in_=b_cols[:, 0:CT])
+            nc.vector.tensor_scalar(out=neg_b[:], in0=b_cols[:, 0:CT], scalar1=-1.0, scalar2=None, op0=ALU.mult)
+            nc.vector.tensor_scalar(out=nch_b[:], in0=b_cols[:, 0:CT], scalar1=float(NCH), scalar2=None, op0=ALU.mult)
 
         fold = []
         for s in range(BLK):
@@ -105,7 +112,7 @@ def tile_cin_pb_t_kernel(tc, h2, x0, W3_words, W3_scales, b3, out):
 
         def double_h2(c):
             d0 = (c % NCH) * DCH
-            h2_twice[c] = work.tile([P, DCH, FL, 2], BF16, name="h2_twice")
+            h2_twice[c] = work.tile([P, DCH, FL, 2], BF16, name="h2_twice", bufs=4)
             nc.scalar.copy(
                 out=h2_twice[c][:],
                 in_=h2_sb[c // NCH][:, :, d0 : d0 + DCH]
@@ -117,7 +124,7 @@ def tile_cin_pb_t_kernel(tc, h2, x0, W3_words, W3_scales, b3, out):
         def multiply(c, u):
             d0 = (c % NCH) * DCH
             if u == 0:
-                z_rows[c] = work.tile([P, DCH, 2, FL, 2, 2], BF16, name="z_rows")
+                z_rows[c] = work.tile([P, DCH, 2, FL, 2, 2], BF16, name="z_rows", bufs=4)
             nc.vector.tensor_tensor(
                 out=z_rows[c][:, :, u],
                 in0=h2_twice[c][:].unsqueeze(3).to_broadcast([P, DCH, FL, 2, 2]),
@@ -236,41 +243,44 @@ def tile_cin_pb_t_kernel(tc, h2, x0, W3_words, W3_scales, b3, out):
         def live(c):
             return 0 <= c < NCHUNK
 
-        with tc.manual_schedule():
-            for s in range(-4, NCHUNK + 1):
-                tile_done = live(s - 1) and s % NCH == 0
-                if live(s + 2):
-                    turn_z(s + 2, 0)
-                if live(s - 1):
-                    turn_and_add_scalar(s - 1, 1)
-                    turn_and_add_scalar(s - 1, 3)
-                if tile_done:
-                    turn_and_add_vector((s - 1) // NCH)
-                if live(s + 2):
-                    regroup(s + 2, 0)
-                if live(s + 1):
-                    quantise(s + 1)
-                if live(s + 3):
-                    multiply(s + 3, 0)
-                if tile_done:
-                    save_turned((s - 1) // NCH)
-                if live(s):
-                    multiply_mx(s, 0)
-                    multiply_mx(s, 1)
-                    relu_add_vector(s, 0)
-                    relu_scalar(s, 1)
-                if live(s + 2):
-                    turn_z(s + 2, 1)
-                if tile_done and ((s - 1) // NCH % BLK == BLK - 1 or s == NCHUNK):
-                    store_block((s - 1) // NCH // BLK)
-                if live(s + 2):
-                    regroup(s + 2, 1)
-                if live(s + 3):
-                    multiply(s + 3, 1)
-                if live(s):
-                    multiply_mx(s, 2)
-                    multiply_mx(s, 3)
-                    relu_add_vector(s, 2)
-                    relu_scalar(s, 3)
-                if live(s + 4):
-                    double_h2(s + 4)
+        for s in range(-6, NCHUNK + 1):
+            tile_done = live(s - 1) and s % NCH == 0
+            if live(s + 2):
+                turn_z(s + 2, 0)
+            if live(s - 1):
+                turn_and_add_scalar(s - 1, 1)
+                turn_and_add_scalar(s - 1, 3)
+            if tile_done:
+                turn_and_add_vector((s - 1) // NCH)
+            if live(s + 2):
+                regroup(s + 2, 0)
+            if live(s + 1):
+                quantise(s + 1)
+            if live(s + 4):
+                multiply(s + 4, 0)
+            if tile_done:
+                save_turned((s - 1) // NCH)
+            if live(s):
+                multiply_mx(s, 0)
+                multiply_mx(s, 1)
+                relu_add_vector(s, 0)
+                relu_scalar(s, 1)
+            if live(s + 2):
+                turn_z(s + 2, 1)
+            if tile_done and ((s - 1) // NCH % BLK == BLK - 1 or s == NCHUNK):
+                store_block((s - 1) // NCH // BLK)
+            if live(s + 2):
+                regroup(s + 2, 1)
+            if live(s + 4):
+                multiply(s + 4, 1)
+            if s == -4:
+                turn_bias()
+            if s == -3:
+                save_bias()
+            if live(s):
+                multiply_mx(s, 2)
+                multiply_mx(s, 3)
+                relu_add_vector(s, 2)
+                relu_scalar(s, 3)
+            if live(s + 6):
+                double_h2(s + 6)

@@ -24,7 +24,13 @@ NCH = D // DCH
 NCHUNK = NPT * NCH
 NCOL = DCH * BT
 CT = L3 // P
-BLK = 2
+NBANK = CT // 2
+BLK = P // BT
+
+H2_AHEAD = 6
+PRODUCT_AHEAD = 4
+TURN_AHEAD = 2
+QUANTISE_AHEAD = 1
 
 FLOPS = 2 * B * D * H2 * F * L3
 
@@ -39,7 +45,6 @@ def tile_cin_pb_t_kernel(tc, h2, x0, W3_words, W3_scales, b3, out):
         t_psum = ctx.enter_context(tc.psum_pool(name="t_psum", bufs=3))
         y_psum = ctx.enter_context(tc.psum_pool(name="y_psum", bufs=3))
         r_psum = ctx.enter_context(tc.psum_pool(name="r_psum", bufs=1))
-
         ctx.enter_context(tc.manual_schedule())
 
         h2_rows = h2.rearrange("b (g fl) d -> (b g) fl d", g=G)
@@ -76,6 +81,13 @@ def tile_cin_pb_t_kernel(tc, h2, x0, W3_words, W3_scales, b3, out):
         for u in range(2):
             nc.vector.tensor_copy(out=x0_pairs[:, :, :, u], in_=x0_view[:, :, :, u])
 
+        fold = []
+        for s in range(BLK):
+            fold_s = const.tile([P, P], F32, name="fold%d" % s)
+            nc.vector.memset(fold_s[:].bitcast(I32), 0)
+            nc.vector.tensor_tensor(out=fold_s[:, BT * s : BT * (s + 1)], in0=ident[:, 0:BT], in1=ident[:, BT:P], op=ALU.add)
+            fold.append(fold_s)
+
         b_rows_f = const.tile([P, P], F32)
         b_cols = y_psum.tile([P, P], F32, tag="y")
         bias = const.tile([P, CT], F32)
@@ -91,13 +103,6 @@ def tile_cin_pb_t_kernel(tc, h2, x0, W3_words, W3_scales, b3, out):
             nc.vector.tensor_scalar(out=neg_b[:], in0=b_cols[:, 0:CT], scalar1=-1.0, scalar2=None, op0=ALU.mult)
             nc.vector.tensor_scalar(out=nch_b[:], in0=b_cols[:, 0:CT], scalar1=float(NCH), scalar2=None, op0=ALU.mult)
 
-        fold = []
-        for s in range(BLK):
-            fold_s = const.tile([P, P], F32, name="fold%d" % s)
-            nc.vector.memset(fold_s[:].bitcast(I32), 0)
-            nc.vector.tensor_tensor(out=fold_s[:, BT * s : BT * (s + 1)], in0=ident[:, 0:BT], in1=ident[:, BT:P], op=ALU.add)
-            fold.append(fold_s)
-
         h2_twice = {}
         z_rows = {}
         z_cols = {}
@@ -112,7 +117,7 @@ def tile_cin_pb_t_kernel(tc, h2, x0, W3_words, W3_scales, b3, out):
 
         def double_h2(c):
             d0 = (c % NCH) * DCH
-            h2_twice[c] = work.tile([P, DCH, FL, 2], BF16, name="h2_twice", bufs=4)
+            h2_twice[c] = work.tile([P, DCH, FL, 2], BF16, name="h2_twice", bufs=H2_AHEAD - PRODUCT_AHEAD + 2)
             nc.scalar.copy(
                 out=h2_twice[c][:],
                 in_=h2_sb[c // NCH][:, :, d0 : d0 + DCH]
@@ -124,7 +129,7 @@ def tile_cin_pb_t_kernel(tc, h2, x0, W3_words, W3_scales, b3, out):
         def multiply(c, u):
             d0 = (c % NCH) * DCH
             if u == 0:
-                z_rows[c] = work.tile([P, DCH, 2, FL, 2, 2], BF16, name="z_rows", bufs=4)
+                z_rows[c] = work.tile([P, DCH, 2, FL, 2, 2], BF16, name="z_rows", bufs=PRODUCT_AHEAD - TURN_AHEAD + 2)
             nc.vector.tensor_tensor(
                 out=z_rows[c][:, :, u],
                 in0=h2_twice[c][:].unsqueeze(3).to_broadcast([P, DCH, FL, 2, 2]),
@@ -145,7 +150,9 @@ def tile_cin_pb_t_kernel(tc, h2, x0, W3_words, W3_scales, b3, out):
 
         def regroup(c, half):
             if half == 0:
-                grouped[c] = work.tile([P, G, NCOL, 4], BF16, name="grouped", align_bytes=64)
+                grouped[c] = work.tile(
+                    [P, G, NCOL, 4], BF16, name="grouped", bufs=TURN_AHEAD - QUANTISE_AHEAD + 2, align_bytes=64
+                )
             words = grouped[c][:].bitcast(F32)
             for pair in (2 * half, 2 * half + 1):
                 nc.scalar.copy(
@@ -154,8 +161,8 @@ def tile_cin_pb_t_kernel(tc, h2, x0, W3_words, W3_scales, b3, out):
                 )
 
         def quantise(c):
-            z_codes[c] = work.tile([P, G, NCOL], U32, name="z_codes", align_bytes=64)
-            z_scales[c] = work.tile([P, G, NCOL], U8, name="z_scales", align_bytes=64)
+            z_codes[c] = work.tile([P, G, NCOL], U32, name="z_codes", bufs=QUANTISE_AHEAD + 2, align_bytes=64)
+            z_scales[c] = work.tile([P, G, NCOL], U8, name="z_scales", bufs=QUANTISE_AHEAD + 2, align_bytes=64)
             nc.vector.quantize_mx(
                 out=z_codes[c][:].rearrange("p g n -> p (g n)").bitcast(FP8X4),
                 scales=z_scales[c][:].rearrange("p g n -> p (g n)"),
@@ -178,7 +185,7 @@ def tile_cin_pb_t_kernel(tc, h2, x0, W3_words, W3_scales, b3, out):
         def relu_add_vector(c, ct):
             pt = c // NCH
             if c % NCH == 0 and ct == 0:
-                acc[pt] = sums.tile([P, CT // 2, NCOL], F32, name="acc")
+                acc[pt] = sums.tile([P, NBANK, NCOL], F32, name="acc")
             acc_ct = acc[pt][:, ct // 2, :]
             if c % NCH == 0:
                 nc.vector.tensor_scalar(
@@ -215,72 +222,65 @@ def tile_cin_pb_t_kernel(tc, h2, x0, W3_words, W3_scales, b3, out):
                 turned[pt, ct // 2] = r_psum.tile([P, 2, P], F32, name="turned%d" % (ct // 2))
             turn_and_add(turned[pt, ct // 2][:, 1, :], y_relu[c, ct], c % NCH == 0, c % NCH == NCH - 1)
 
-        def turn_and_add_vector(pt):
-            for j in range(CT // 2):
-                turn_and_add(turned[pt, j][:, 0, :], acc[pt][:, j, :], True, True)
+        def finish_bank(pt, j):
+            turn_and_add(turned[pt, j][:, 0, :], acc[pt][:, j, :], True, True)
+            turned_sb[pt, j] = sums.tile([P, 2 * P], F32, name="turned_sb%d" % j)
+            nc.vector.tensor_copy(out=turned_sb[pt, j][:], in_=turned[pt, j][:].rearrange("p h c -> p (h c)"))
 
-        def save_turned(pt):
-            turned_sb[pt] = sums.tile([P, CT // 2, 2 * P], F32, name="turned_sb")
-            for j in range(CT // 2):
-                nc.vector.tensor_copy(out=turned_sb[pt][:, j, :], in_=turned[pt, j][:].rearrange("p h c -> p (h c)"))
-
-        def store_block(blk):
+        def store_block(blk, j):
             tiles = list(range(blk * BLK, min((blk + 1) * BLK, NPT)))
-            out_ps = y_psum.tile([P, L3], F32, name="out_ps", tag="y")
+            out_ps = y_psum.tile([P, 2 * P], F32, name="out_ps", tag="y")
             for s in range(len(tiles)):
                 nc.tensor.matmul(
-                    out=out_ps[:],
-                    lhsT=fold[s][:],
-                    rhs=turned_sb[tiles[s]][:].rearrange("p j c -> p (j c)"),
-                    start=(s == 0),
-                    stop=(s == len(tiles) - 1),
+                    out=out_ps[:], lhsT=fold[s][:], rhs=turned_sb[tiles[s], j][:], start=(s == 0), stop=(s == len(tiles) - 1)
                 )
-            out_sb = sums.tile([P, L3], F32, name="out_sb")
+            out_sb = sums.tile([P, 2 * P], F32, name="out_sb")
             nc.scalar.copy(out=out_sb[:], in_=out_ps[:])
             rows = BT * len(tiles)
-            nc.sync.dma_start(out=out[blk * P : blk * P + rows, :], in_=out_sb[0:rows, :])
+            nc.sync.dma_start(out=out[blk * P : blk * P + rows, 2 * P * j : 2 * P * (j + 1)], in_=out_sb[0:rows, :])
 
         def live(c):
             return 0 <= c < NCHUNK
 
-        for s in range(-6, NCHUNK + 1):
+        for s in range(-H2_AHEAD, NCHUNK + 1):
             tile_done = live(s - 1) and s % NCH == 0
-            if live(s + 2):
-                turn_z(s + 2, 0)
+            pt_done = (s - 1) // NCH
             if live(s - 1):
                 turn_and_add_scalar(s - 1, 1)
-                turn_and_add_scalar(s - 1, 3)
             if tile_done:
-                turn_and_add_vector((s - 1) // NCH)
-            if live(s + 2):
-                regroup(s + 2, 0)
-            if live(s + 1):
-                quantise(s + 1)
-            if live(s + 4):
-                multiply(s + 4, 0)
-            if tile_done:
-                save_turned((s - 1) // NCH)
+                finish_bank(pt_done, 0)
+            if live(s + TURN_AHEAD):
+                turn_z(s + TURN_AHEAD, 0)
+                regroup(s + TURN_AHEAD, 0)
+            if live(s + QUANTISE_AHEAD):
+                quantise(s + QUANTISE_AHEAD)
+            if live(s + PRODUCT_AHEAD):
+                multiply(s + PRODUCT_AHEAD, 0)
             if live(s):
                 multiply_mx(s, 0)
                 multiply_mx(s, 1)
                 relu_add_vector(s, 0)
                 relu_scalar(s, 1)
-            if live(s + 2):
-                turn_z(s + 2, 1)
-            if tile_done and ((s - 1) // NCH % BLK == BLK - 1 or s == NCHUNK):
-                store_block((s - 1) // NCH // BLK)
-            if live(s + 2):
-                regroup(s + 2, 1)
-            if live(s + 4):
-                multiply(s + 4, 1)
-            if s == -4:
+            if live(s - 1):
+                turn_and_add_scalar(s - 1, 3)
+            if tile_done:
+                finish_bank(pt_done, 1)
+            if live(s + TURN_AHEAD):
+                turn_z(s + TURN_AHEAD, 1)
+                regroup(s + TURN_AHEAD, 1)
+            if live(s + PRODUCT_AHEAD):
+                multiply(s + PRODUCT_AHEAD, 1)
+            if s == -PRODUCT_AHEAD:
                 turn_bias()
-            if s == -3:
+            if s == -PRODUCT_AHEAD + 1:
                 save_bias()
             if live(s):
                 multiply_mx(s, 2)
                 multiply_mx(s, 3)
                 relu_add_vector(s, 2)
                 relu_scalar(s, 3)
-            if live(s + 6):
-                double_h2(s + 6)
+            if tile_done and (pt_done % BLK == BLK - 1 or pt_done == NPT - 1):
+                for j in range(NBANK):
+                    store_block(pt_done // BLK, j)
+            if live(s + H2_AHEAD):
+                double_h2(s + H2_AHEAD)

@@ -17,82 +17,129 @@ B, H2, F, D, L3 = 320, 128, 8, 32, 512
 P = 128
 G = 2
 FL = H2 // G
-BT = P // G
-NPT = B // BT
-DCH = 8
-NCH = D // DCH
-NCHUNK = NPT * NCH
-NCOL = DCH * BT
+NCOL = 512
 CT = L3 // P
-NBANK = CT // 2
-BLK = P // BT
+NW = D // 2
+DQ = 4
+TILES = ((0, 128), (256, 64), (128, 128))
+NCHUNK = B * D // NCOL
+PARK_ROW = 128
 
-H2_AHEAD = 6
-PRODUCT_AHEAD = 4
-TURN_AHEAD = 2
-QUANTISE_AHEAD = 1
+T_AHEAD = 5
+E_AHEAD = 4
+M_AHEAD = 2
+Q_AHEAD = 1
+X_AHEAD = 6
+V_EVERY = 2
 
 FLOPS = 2 * B * D * H2 * F * L3
+
+
+def on_vector(k, ct):
+    return V_EVERY > 0 and ct == 0 and k % V_EVERY == 0
 
 
 def tile_cin_pb_t_kernel(tc, h2, x0, W3_words, W3_scales, b3, out):
     nc = tc.nc
     with ExitStack() as ctx:
         const = ctx.enter_context(tc.tile_pool(name="const", bufs=1))
-        h2_pool = ctx.enter_context(tc.tile_pool(name="h2_pool", bufs=NPT))
         work = ctx.enter_context(tc.tile_pool(name="work", bufs=3))
-        sums = ctx.enter_context(tc.tile_pool(name="sums", bufs=2))
-        t_psum = ctx.enter_context(tc.psum_pool(name="t_psum", bufs=3))
-        y_psum = ctx.enter_context(tc.psum_pool(name="y_psum", bufs=3))
-        r_psum = ctx.enter_context(tc.psum_pool(name="r_psum", bufs=1))
+        t_psum = ctx.enter_context(tc.psum_pool(name="t_psum", bufs=2))
+        y_psum = ctx.enter_context(tc.psum_pool(name="y_psum", bufs=4))
+        a_psum = ctx.enter_context(tc.psum_pool(name="a_psum", bufs=2))
         ctx.enter_context(tc.manual_schedule())
 
-        h2_rows = h2.rearrange("b (g fl) d -> (b g) fl d", g=G)
+        ntile = len(TILES)
+        CHUNKS = [(ti, k) for ti in range(ntile) for k in range(D * TILES[ti][1] // NCOL)]
+        row0 = [b0 + nb - P for (b0, nb) in TILES]
+        skip = [P - nb for (b0, nb) in TILES]
+        nwc = [NCOL // (2 * nb) for (b0, nb) in TILES]
+        nchunk = [NW // n for n in nwc]
+        park_rows = [DQ * nb * 16 // L3 for (b0, nb) in TILES]
+        park0 = {}
+        row = PARK_ROW
+        for ti in range(ntile):
+            for jh in range(2):
+                park0[ti, jh] = row
+                row += park_rows[ti]
+
+        x1 = const.tile([P, ntile, F * D], BF16, name="x1")
+        for ti in range(ntile):
+            nc.scalar.dma_start(out=x1[:, ti, :], in_=x0[row0[ti] : row0[ti] + P].rearrange("b j d -> b (j d)"))
         h2_sb = []
-        for pt in range(NPT):
-            h2_tile = h2_pool.tile([P, FL, D], BF16, name="h2_tile")
+        for ti in range(ntile):
+            h2_tile = const.tile([P, H2 * D], BF16, name="h2_tile%d" % ti)
             h2_sb.append(h2_tile)
-        nc.sync.dma_start(out=h2_sb[0][:], in_=h2_rows[0:P])
-        x0_sb = const.tile([P, NPT, F * D], BF16)
-        x0_rows = x0.rearrange("(t b) j d -> b t (j d)", b=BT)
-        for g in range(G):
-            nc.scalar.dma_start(out=x0_sb[g:P:G, :, :], in_=x0_rows)
+
+        def load_h2(ti):
+            nc.sync.dma_start(out=h2_sb[ti][:], in_=h2[row0[ti] : row0[ti] + P].rearrange("b f d -> b (f d)"))
+
+        load_h2(0)
         w_words = const.tile([P, G, 2 * L3], U8, align_bytes=64)
         nc.sync.dma_start(out=w_words[:].bitcast(I32), in_=W3_words.bitcast(I32).rearrange("g p n -> p g n"))
-        nc.sync.dma_start(out=h2_sb[1][:], in_=h2_rows[P : 2 * P])
         w_scales = const.tile([P, G, L3], U8, align_bytes=64)
         nc.vector.memset(w_scales[:].bitcast(I32), 0)
+        b_rows = const.tile([P, P], BF16)
+        nc.vector.memset(b_rows[:].bitcast(I32), 0)
+
+        ident = const.tile([P, P], F32)
+        make_identity(nc, ident[:])
+
+        x2 = const.tile([P, ntile, 2, D, 4], BF16, name="x2")
+        nc.vector.tensor_copy(
+            out=x2[:].rearrange("p i jh d t -> p (i jh) d t"),
+            in_=x1[:].rearrange("p i (jh t d) -> p (i jh) d t", jh=2, t=4),
+        )
+
+        def park_x0(ti):
+            for jh in range(2):
+                rows = out[park0[ti, jh] : park0[ti, jh] + park_rows[ti], :].rearrange("r c -> (r c)")
+                nc.sync.dma_start(
+                    out=rows.rearrange("(dq b w) -> b dq w", dq=DQ, w=16),
+                    in_=x2[skip[ti] : P, ti, jh].rearrange("p (dq d8) t -> p dq (d8 t)", dq=DQ).bitcast(F32),
+                )
+
+        xq = {}
+
+        def spread_x0(ti, dq):
+            nb = TILES[ti][1]
+            xq[ti, dq] = work.tile([P, P * 32], BF16, name="xq", bufs=4)
+            nrow = park_rows[ti] // DQ
+            for jh in range(2):
+                r = park0[ti, jh] + nrow * dq
+                nc.sync.dma_start(
+                    out=xq[ti, dq][jh:P:2, 0 : nb * 32].bitcast(F32),
+                    in_=out[r : r + nrow, :].rearrange("r c -> (r c)").partition_broadcast(P // 2),
+                )
+
+        units = [(ti, dq) for ti in range(ntile) for dq in range(DQ)]
+
+        def first_use(ti, dq):
+            return CHUNKS.index((ti, dq * nchunk[ti] // DQ))
+
         for quad in range(4):
             nc.sync.dma_start(
                 out=w_scales[32 * quad : 32 * quad + 4].bitcast(I32),
                 in_=W3_scales[:, 4 * quad : 4 * quad + 4, :].bitcast(I32).rearrange("g r n -> r g n"),
             )
-        b_rows = const.tile([P, P], BF16)
-        nc.vector.memset(b_rows[:].bitcast(I32), 0)
         nc.sync.dma_start(out=b_rows[0:CT, :], in_=b3.rearrange("(r c) -> r c", c=P))
-        for pt in range(2, NPT):
-            nc.sync.dma_start(out=h2_sb[pt][:], in_=h2_rows[pt * P : (pt + 1) * P])
+        park_x0(0)
+        spread_x0(0, 0)
+        for ti in range(1, ntile):
+            park_x0(ti)
+        for ti in range(1, ntile):
+            load_h2(ti)
 
-        ident = const.tile([P, P], F32)
-        make_identity(nc, ident[:])
-
-        x0_pairs = const.tile([P, NPT, D, 2, 2, 2], BF16)
-        x0_view = x0_sb[:].rearrange("p t (jh u e d) -> p t d u jh e", jh=2, u=2, e=2)
-        for u in range(2):
-            nc.vector.tensor_copy(out=x0_pairs[:, :, :, u], in_=x0_view[:, :, :, u])
-
-        fold = []
-        for s in range(BLK):
-            fold_s = const.tile([P, P], F32, name="fold%d" % s)
-            nc.vector.memset(fold_s[:].bitcast(I32), 0)
-            nc.vector.tensor_tensor(out=fold_s[:, BT * s : BT * (s + 1)], in0=ident[:, 0:BT], in1=ident[:, BT:P], op=ALU.add)
-            fold.append(fold_s)
+        fold = const.tile([P, P], F32, name="fold")
+        nc.vector.memset(fold[:].bitcast(I32), 0)
+        nc.vector.tensor_tensor(out=fold[:, 0 : P // 2], in0=ident[:, 0:P:2], in1=ident[:, 1:P:2], op=ALU.add)
 
         b_rows_f = const.tile([P, P], F32)
-        b_cols = y_psum.tile([P, P], F32, tag="y")
+        b_cols = y_psum.tile([P, P], F32, tag="y", name="b_cols")
         bias = const.tile([P, CT], F32)
         neg_b = const.tile([P, CT], F32)
-        nch_b = const.tile([P, CT], F32)
+        nv_b = {}
+        nv = [len([k for k in range(n) if on_vector(k, 0)]) for n in nchunk]
 
         def turn_bias():
             nc.vector.tensor_copy(out=b_rows_f[:], in_=b_rows[:])
@@ -101,72 +148,70 @@ def tile_cin_pb_t_kernel(tc, h2, x0, W3_words, W3_scales, b3, out):
         def save_bias():
             nc.vector.tensor_copy(out=bias[:], in_=b_cols[:, 0:CT])
             nc.vector.tensor_scalar(out=neg_b[:], in0=b_cols[:, 0:CT], scalar1=-1.0, scalar2=None, op0=ALU.mult)
-            nc.vector.tensor_scalar(out=nch_b[:], in0=b_cols[:, 0:CT], scalar1=float(NCH), scalar2=None, op0=ALU.mult)
+            for n in sorted(set(nv)):
+                if n > 0:
+                    nv_b[n] = const.tile([P, CT], F32, name="nv_b%d" % n)
+                    nc.vector.tensor_scalar(out=nv_b[n][:], in0=b_cols[:, 0:CT], scalar1=float(n), scalar2=None, op0=ALU.mult)
 
-        h2_twice = {}
-        z_rows = {}
-        z_cols = {}
-        grouped = {}
+        h_t = {}
+        h2e = {}
+        h2p = {}
+        z = {}
         z_codes = {}
         z_scales = {}
         y = {}
         y_relu = {}
         acc = {}
-        turned = {}
-        turned_sb = {}
+        acc_v = {}
+        acc_sb = {}
+        done = {}
+
+        def turn_h2(c):
+            ti, k = CHUNKS[c]
+            h_t[c] = t_psum.tile([P, 4, P], F32, name="h_t")
+            words = h2_sb[ti][:].bitcast(F32)
+            for wl in range(nwc[ti]):
+                nc.tensor.transpose(h_t[c][:, wl, :], words[:, k * nwc[ti] + wl : H2 * NW : NW], ident[:])
 
         def double_h2(c):
-            d0 = (c % NCH) * DCH
-            h2_twice[c] = work.tile([P, DCH, FL, 2], BF16, name="h2_twice", bufs=H2_AHEAD - PRODUCT_AHEAD + 2)
+            ti, k = CHUNKS[c]
+            nb = TILES[ti][1]
+            h2e[c] = work.tile([P, NCOL, 2], BF16, name="h2e", bufs=3)
             nc.scalar.copy(
-                out=h2_twice[c][:],
-                in_=h2_sb[c // NCH][:, :, d0 : d0 + DCH]
-                .rearrange("p fl d -> p d fl")
-                .unsqueeze(3)
-                .to_broadcast([P, DCH, FL, 2]),
+                out=h2e[c][:].rearrange("p (wl x) e -> p wl x e", wl=nwc[ti]),
+                in_=h_t[c][:, 0 : nwc[ti], skip[ti] : P].bitcast(BF16).unsqueeze(3).to_broadcast([P, nwc[ti], 2 * nb, 2]),
             )
+            h2p[c] = work.tile([P, G, NCOL, 2], BF16, name="h2p", bufs=4)
+            for g in range(G):
+                for r in range(2):
+                    nc.sync.dma_start(out=h2p[c][r:P:2, g], in_=h2e[c][FL * g : FL * (g + 1)])
 
-        def multiply(c, u):
-            d0 = (c % NCH) * DCH
-            if u == 0:
-                z_rows[c] = work.tile([P, DCH, 2, FL, 2, 2], BF16, name="z_rows", bufs=PRODUCT_AHEAD - TURN_AHEAD + 2)
+        def multiply(c, g):
+            ti, k = CHUNKS[c]
+            nb = TILES[ti][1]
+            n = nwc[ti]
+            if g == 0:
+                z[c] = work.tile([P, G, NCOL, 4], BF16, name="z", bufs=3, align_bytes=64)
+            w0 = k * n
             nc.vector.tensor_tensor(
-                out=z_rows[c][:, :, u],
-                in0=h2_twice[c][:].unsqueeze(3).to_broadcast([P, DCH, FL, 2, 2]),
-                in1=x0_pairs[:, c // NCH, d0 : d0 + DCH, u].unsqueeze(2).to_broadcast([P, DCH, FL, 2, 2]),
+                out=z[c][:, g].rearrange("p (wl b d2) (tp e) -> p wl b d2 tp e", wl=n, d2=2, tp=2),
+                in0=h2p[c][:, g]
+                .rearrange("p (wl b d2) e -> p wl b d2 e", wl=n, d2=2)
+                .unsqueeze(4)
+                .to_broadcast([P, n, nb, 2, 2, 2]),
+                in1=xq[ti, w0 // 4][:, 0 : nb * 32].rearrange("p (b wq d2 tp e) -> p wq b d2 tp e", b=nb, wq=4, d2=2, tp=2)[
+                    :, w0 % 4 : w0 % 4 + n
+                ],
                 op=ALU.mult,
             )
 
-        def turn_z(c, half):
-            for pair in (2 * half, 2 * half + 1):
-                z_cols[c, pair] = t_psum.tile([P, 2, 2, BT, G], F32, name="z_cols")
-                for u in range(2):
-                    for dd in range(2):
-                        nc.tensor.transpose(
-                            z_cols[c, pair][:, u, dd].rearrange("p b g -> p (b g)"),
-                            z_rows[c][:, 2 * pair + dd, u].rearrange("p fl jh e -> p (fl jh e)").bitcast(F32),
-                            ident[:],
-                        )
-
-        def regroup(c, half):
-            if half == 0:
-                grouped[c] = work.tile(
-                    [P, G, NCOL, 4], BF16, name="grouped", bufs=TURN_AHEAD - QUANTISE_AHEAD + 2, align_bytes=64
-                )
-            words = grouped[c][:].bitcast(F32)
-            for pair in (2 * half, 2 * half + 1):
-                nc.scalar.copy(
-                    out=words[:, :, 2 * BT * pair : 2 * BT * (pair + 1), :],
-                    in_=z_cols[c, pair][:].rearrange("p u dd b g -> p g (dd b) u"),
-                )
-
         def quantise(c):
-            z_codes[c] = work.tile([P, G, NCOL], U32, name="z_codes", bufs=QUANTISE_AHEAD + 2, align_bytes=64)
-            z_scales[c] = work.tile([P, G, NCOL], U8, name="z_scales", bufs=QUANTISE_AHEAD + 2, align_bytes=64)
+            z_codes[c] = work.tile([P, G, NCOL], U32, name="z_codes", bufs=3, align_bytes=64)
+            z_scales[c] = work.tile([P, G, NCOL], U8, name="z_scales", bufs=3, align_bytes=64)
             nc.vector.quantize_mx(
                 out=z_codes[c][:].rearrange("p g n -> p (g n)").bitcast(FP8X4),
                 scales=z_scales[c][:].rearrange("p g n -> p (g n)"),
-                in_=grouped[c][:].rearrange("p g n t -> p (g n t)"),
+                in_=z[c][:].rearrange("p g n t -> p (g n t)"),
             )
 
         def multiply_mx(c, ct):
@@ -183,104 +228,129 @@ def tile_cin_pb_t_kernel(tc, h2, x0, W3_words, W3_scales, b3, out):
                 )
 
         def relu_add_vector(c, ct):
-            pt = c // NCH
-            if c % NCH == 0 and ct == 0:
-                acc[pt] = sums.tile([P, NBANK, NCOL], F32, name="acc")
-            acc_ct = acc[pt][:, ct // 2, :]
-            if c % NCH == 0:
+            ti, k = CHUNKS[c]
+            if ti not in acc_v:
+                acc_v[ti] = work.tile([P, NCOL], F32, name="acc_v", bufs=2)
                 nc.vector.tensor_scalar(
-                    out=acc_ct,
+                    out=acc_v[ti][:],
                     in0=y[c, ct][:],
                     scalar1=neg_b[:, ct : ct + 1],
-                    scalar2=nch_b[:, ct : ct + 1],
+                    scalar2=nv_b[nv[ti]][:, ct : ct + 1],
                     op0=ALU.max,
                     op1=ALU.add,
                 )
             else:
                 nc.vector.scalar_tensor_tensor(
-                    out=acc_ct, in0=y[c, ct][:], scalar=neg_b[:, ct : ct + 1], in1=acc_ct, op0=ALU.max, op1=ALU.add
+                    out=acc_v[ti][:], in0=y[c, ct][:], scalar=neg_b[:, ct : ct + 1], in1=acc_v[ti][:], op0=ALU.max, op1=ALU.add
                 )
 
         def relu_scalar(c, ct):
-            y_relu[c, ct] = work.tile([P, NCOL], F32, name="y_relu", bufs=4)
-            nc.scalar.activation(out=y_relu[c, ct][:], in_=y[c, ct][:], func=RELU, bias=bias[:, ct : ct + 1], scale=1.0)
-
-        def turn_and_add(dest, columns, first, last):
-            for q in range(NCOL // P):
-                nc.tensor.matmul(
-                    out=dest,
-                    lhsT=columns[:, q * P : (q + 1) * P],
-                    rhs=ident[:],
-                    is_transpose=True,
-                    start=(first and q == 0),
-                    stop=(last and q == NCOL // P - 1),
+            ti, k = CHUNKS[c]
+            y_relu[c, ct] = work.tile([P, NCOL], F32, name="y_relu", bufs=8)
+            if TILES[ti][1] == P:
+                nc.scalar.activation(
+                    out=y_relu[c, ct][:].rearrange("p (wl d2 b) -> p wl d2 b", wl=2, d2=2),
+                    in_=y[c, ct][:].rearrange("p (wl b d2) -> p wl d2 b", wl=2, d2=2),
+                    func=RELU,
+                    bias=bias[:, ct : ct + 1],
+                    scale=1.0,
                 )
+            else:
+                nc.scalar.activation(out=y_relu[c, ct][:], in_=y[c, ct][:], func=RELU, bias=bias[:, ct : ct + 1], scale=1.0)
 
-        def turn_and_add_scalar(c, ct):
-            pt = c // NCH
-            if c % NCH == 0:
-                turned[pt, ct // 2] = r_psum.tile([P, 2, P], F32, name="turned%d" % (ct // 2))
-            turn_and_add(turned[pt, ct // 2][:, 1, :], y_relu[c, ct], c % NCH == 0, c % NCH == NCH - 1)
+        def n_adds(ti):
+            n = len([1 for k in range(nchunk[ti]) for ct in range(CT) if not on_vector(k, ct)])
+            return (NCOL // P) * (n + (1 if nv[ti] > 0 else 0))
 
-        def finish_bank(pt, j):
-            turn_and_add(turned[pt, j][:, 0, :], acc[pt][:, j, :], True, True)
-            turned_sb[pt, j] = sums.tile([P, 2 * P], F32, name="turned_sb%d" % j)
-            nc.vector.tensor_copy(out=turned_sb[pt, j][:], in_=turned[pt, j][:].rearrange("p h c -> p (h c)"))
+        def add_up(ti, ct, columns):
+            if ti not in acc:
+                acc[ti] = a_psum.tile([P, CT, P], F32, name="acc")
+                done[ti] = 0
+            nc.tensor.matmul(
+                out=acc[ti][:, ct, :],
+                lhsT=columns,
+                rhs=ident[:],
+                is_transpose=True,
+                start=(done[ti] == 0),
+                stop=(done[ti] == n_adds(ti) - 1),
+            )
+            done[ti] += 1
 
-        def store_block(blk, j):
-            tiles = list(range(blk * BLK, min((blk + 1) * BLK, NPT)))
-            out_ps = y_psum.tile([P, 2 * P], F32, name="out_ps", tag="y")
-            for s in range(len(tiles)):
-                nc.tensor.matmul(
-                    out=out_ps[:], lhsT=fold[s][:], rhs=turned_sb[tiles[s], j][:], start=(s == 0), stop=(s == len(tiles) - 1)
-                )
-            out_sb = sums.tile([P, 2 * P], F32, name="out_sb")
-            nc.scalar.copy(out=out_sb[:], in_=out_ps[:])
-            rows = BT * len(tiles)
-            nc.sync.dma_start(out=out[blk * P : blk * P + rows, 2 * P * j : 2 * P * (j + 1)], in_=out_sb[0:rows, :])
+        def add_scalar(c):
+            ti, k = CHUNKS[c]
+            for ct in range(CT):
+                if not on_vector(k, ct):
+                    for q in range(NCOL // P):
+                        add_up(ti, ct, y_relu[c, ct][:, q * P : (q + 1) * P])
+
+        def add_vector(ti):
+            if TILES[ti][1] == P:
+                for wl in range(2):
+                    for d2 in range(2):
+                        add_up(ti, 0, acc_v[ti][:, 2 * P * wl + d2 : 2 * P * (wl + 1) : 2])
+            else:
+                for q in range(NCOL // P):
+                    add_up(ti, 0, acc_v[ti][:, q * P : (q + 1) * P])
+
+        def save_sums(ti):
+            acc_sb[ti] = work.tile([P, L3], F32, name="acc_sb", bufs=2)
+            nc.scalar.copy(out=acc_sb[ti][:], in_=acc[ti][:].rearrange("p ct c -> p (ct c)"))
+            b0, nb = TILES[ti]
+            if nb == P:
+                nc.sync.dma_start(out=out[b0 : b0 + nb, :], in_=acc_sb[ti][:])
+
+        folded = {}
+
+        def fold_sums(ti):
+            folded[ti] = y_psum.tile([P, L3], F32, name="folded", tag="y")
+            nc.tensor.matmul(out=folded[ti][:], lhsT=fold[:], rhs=acc_sb[ti][:], start=True, stop=True)
+
+        def save_folded(ti):
+            b0, nb = TILES[ti]
+            out_sb = work.tile([P, L3], F32, name="out_sb", bufs=1)
+            nc.scalar.copy(out=out_sb[:], in_=folded[ti][:])
+            nc.sync.dma_start(out=out[b0 : b0 + nb, :], in_=out_sb[0:nb, :])
 
         def live(c):
             return 0 <= c < NCHUNK
 
-        for s in range(-H2_AHEAD, NCHUNK + 1):
-            tile_done = live(s - 1) and s % NCH == 0
-            pt_done = (s - 1) // NCH
-            if live(s - 1):
-                turn_and_add_scalar(s - 1, 1)
-            if tile_done:
-                finish_bank(pt_done, 0)
-            if live(s + TURN_AHEAD):
-                turn_z(s + TURN_AHEAD, 0)
-                regroup(s + TURN_AHEAD, 0)
-            if live(s + QUANTISE_AHEAD):
-                quantise(s + QUANTISE_AHEAD)
-            if live(s + PRODUCT_AHEAD):
-                multiply(s + PRODUCT_AHEAD, 0)
-            if live(s):
-                multiply_mx(s, 0)
-                multiply_mx(s, 1)
-                relu_add_vector(s, 0)
-                relu_scalar(s, 1)
-            if live(s - 1):
-                turn_and_add_scalar(s - 1, 3)
-            if tile_done:
-                finish_bank(pt_done, 1)
-            if live(s + TURN_AHEAD):
-                turn_z(s + TURN_AHEAD, 1)
-                regroup(s + TURN_AHEAD, 1)
-            if live(s + PRODUCT_AHEAD):
-                multiply(s + PRODUCT_AHEAD, 1)
-            if s == -PRODUCT_AHEAD:
+        def last_of_tile(c):
+            return live(c) and CHUNKS[c][1] == nchunk[CHUNKS[c][0]] - 1
+
+        for s in range(-X_AHEAD, NCHUNK + 3):
+            for (ti, dq) in units:
+                if first_use(ti, dq) - X_AHEAD == s and (ti, dq) not in xq:
+                    spread_x0(ti, dq)
+            if live(s + T_AHEAD):
+                turn_h2(s + T_AHEAD)
+            if live(s + E_AHEAD):
+                double_h2(s + E_AHEAD)
+            if s == -T_AHEAD:
                 turn_bias()
-            if s == -PRODUCT_AHEAD + 1:
+            if s == -T_AHEAD + 1:
                 save_bias()
+            if live(s - 1):
+                add_scalar(s - 1)
+            if last_of_tile(s - 1):
+                ti = CHUNKS[s - 1][0]
+                if nv[ti] > 0:
+                    add_vector(ti)
+                save_sums(ti)
+            if last_of_tile(s - 2) and TILES[CHUNKS[s - 2][0]][1] < P:
+                fold_sums(CHUNKS[s - 2][0])
+                save_folded(CHUNKS[s - 2][0])
+            if live(s + Q_AHEAD):
+                quantise(s + Q_AHEAD)
+            if live(s + M_AHEAD):
+                multiply(s + M_AHEAD, 0)
             if live(s):
-                multiply_mx(s, 2)
-                multiply_mx(s, 3)
-                relu_add_vector(s, 2)
-                relu_scalar(s, 3)
-            if tile_done and (pt_done % BLK == BLK - 1 or pt_done == NPT - 1):
-                for j in range(NBANK):
-                    store_block(pt_done // BLK, j)
-            if live(s + H2_AHEAD):
-                double_h2(s + H2_AHEAD)
+                k = CHUNKS[s][1]
+                for ct in range(CT):
+                    multiply_mx(s, ct)
+                for ct in range(CT):
+                    if on_vector(k, ct):
+                        relu_add_vector(s, ct)
+                    else:
+                        relu_scalar(s, ct)
+            if live(s + M_AHEAD):
+                multiply(s + M_AHEAD, 1)

@@ -18,25 +18,26 @@ P = 128
 G = 2
 FL = H2 // G
 NCOL = 512
+DC = NCOL // P
 CT = L3 // P
-NW = D // 2
-DQ = 4
+US = 8
 TILES = ((0, 128), (256, 64), (128, 128))
 NCHUNK = B * D // NCOL
 PARK_ROW = 128
+SHIFT = D // 2
 
-T_AHEAD = 5
-E_AHEAD = 4
+H_AHEAD = 5
+T_AHEAD = 3
 M_AHEAD = 2
 Q_AHEAD = 1
-X_AHEAD = 6
-V_EVERY = 2
+V_CT = 3
+V_EVERY = 1
 
 FLOPS = 2 * B * D * H2 * F * L3
 
 
 def on_vector(k, ct):
-    return V_EVERY > 0 and ct == 0 and k % V_EVERY == 0
+    return V_EVERY > 0 and ct == V_CT and k % V_EVERY == 0
 
 
 def tile_cin_pb_t_kernel(tc, h2, x0, W3_words, W3_scales, b3, out):
@@ -44,18 +45,19 @@ def tile_cin_pb_t_kernel(tc, h2, x0, W3_words, W3_scales, b3, out):
     with ExitStack() as ctx:
         const = ctx.enter_context(tc.tile_pool(name="const", bufs=1))
         work = ctx.enter_context(tc.tile_pool(name="work", bufs=3))
-        t_psum = ctx.enter_context(tc.psum_pool(name="t_psum", bufs=2))
-        y_psum = ctx.enter_context(tc.psum_pool(name="y_psum", bufs=4))
+        t_psum = ctx.enter_context(tc.psum_pool(name="t_psum", bufs=3))
+        y_psum = ctx.enter_context(tc.psum_pool(name="y_psum", bufs=3))
         a_psum = ctx.enter_context(tc.psum_pool(name="a_psum", bufs=2))
         ctx.enter_context(tc.manual_schedule())
 
         ntile = len(TILES)
-        CHUNKS = [(ti, k) for ti in range(ntile) for k in range(D * TILES[ti][1] // NCOL)]
+        nchunk = [D * nb // NCOL for (b0, nb) in TILES]
+        nunit = [n * DC // US for n in nchunk]
+        CHUNKS = [(ti, k) for ti in range(ntile) for k in range(nchunk[ti])]
         row0 = [b0 + nb - P for (b0, nb) in TILES]
         skip = [P - nb for (b0, nb) in TILES]
-        nwc = [NCOL // (2 * nb) for (b0, nb) in TILES]
-        nchunk = [NW // n for n in nwc]
-        park_rows = [DQ * nb * 16 // L3 for (b0, nb) in TILES]
+        UROWS = P * US * 2 // L3
+        park_rows = [n * UROWS for n in nunit]
         park0 = {}
         row = PARK_ROW
         for ti in range(ntile):
@@ -64,15 +66,24 @@ def tile_cin_pb_t_kernel(tc, h2, x0, W3_words, W3_scales, b3, out):
                 row += park_rows[ti]
 
         x1 = const.tile([P, ntile, F * D], BF16, name="x1")
-        for ti in range(ntile):
-            nc.scalar.dma_start(out=x1[:, ti, :], in_=x0[row0[ti] : row0[ti] + P].rearrange("b j d -> b (j d)"))
+
+        def load_x0(ti):
+            nc.sync.dma_start(out=x1[:, ti, :], in_=x0[row0[ti] : row0[ti] + P].rearrange("b j d -> b (j d)"))
+
+        load_x0(0)
         h2_sb = []
         for ti in range(ntile):
-            h2_tile = const.tile([P, H2 * D], BF16, name="h2_tile%d" % ti)
+            h2_tile = const.tile([P, H2 * D + SHIFT], BF16, name="h2_tile%d" % ti)
             h2_sb.append(h2_tile)
 
         def load_h2(ti):
-            nc.sync.dma_start(out=h2_sb[ti][:], in_=h2[row0[ti] : row0[ti] + P].rearrange("b f d -> b (f d)"))
+            b0, nb = TILES[ti]
+            rows = h2[b0 : b0 + nb].rearrange("b f d -> b (f d)")
+            if nb == P:
+                nc.scalar.dma_start(out=h2_sb[ti][:, SHIFT : SHIFT + H2 * D], in_=rows)
+            else:
+                nc.scalar.dma_start(out=h2_sb[ti][0:nb, SHIFT : SHIFT + H2 * D], in_=rows)
+                nc.scalar.dma_start(out=h2_sb[ti][nb:P, 0 : H2 * D], in_=rows)
 
         load_h2(0)
         w_words = const.tile([P, G, 2 * L3], U8, align_bytes=64)
@@ -81,65 +92,71 @@ def tile_cin_pb_t_kernel(tc, h2, x0, W3_words, W3_scales, b3, out):
         nc.vector.memset(w_scales[:].bitcast(I32), 0)
         b_rows = const.tile([P, P], BF16)
         nc.vector.memset(b_rows[:].bitcast(I32), 0)
-
-        ident = const.tile([P, P], F32)
-        make_identity(nc, ident[:])
-
-        x2 = const.tile([P, ntile, 2, D, 4], BF16, name="x2")
-        nc.vector.tensor_copy(
-            out=x2[:].rearrange("p i jh d t -> p (i jh) d t"),
-            in_=x1[:].rearrange("p i (jh t d) -> p (i jh) d t", jh=2, t=4),
-        )
-
-        def park_x0(ti):
-            for jh in range(2):
-                rows = out[park0[ti, jh] : park0[ti, jh] + park_rows[ti], :].rearrange("r c -> (r c)")
-                nc.sync.dma_start(
-                    out=rows.rearrange("(dq b w) -> b dq w", dq=DQ, w=16),
-                    in_=x2[skip[ti] : P, ti, jh].rearrange("p (dq d8) t -> p dq (d8 t)", dq=DQ).bitcast(F32),
-                )
-
-        xq = {}
-
-        def spread_x0(ti, dq):
-            nb = TILES[ti][1]
-            xq[ti, dq] = work.tile([P, P * 32], BF16, name="xq", bufs=4)
-            nrow = park_rows[ti] // DQ
-            for jh in range(2):
-                r = park0[ti, jh] + nrow * dq
-                nc.sync.dma_start(
-                    out=xq[ti, dq][jh:P:2, 0 : nb * 32].bitcast(F32),
-                    in_=out[r : r + nrow, :].rearrange("r c -> (r c)").partition_broadcast(P // 2),
-                )
-
-        units = [(ti, dq) for ti in range(ntile) for dq in range(DQ)]
-
-        def first_use(ti, dq):
-            return CHUNKS.index((ti, dq * nchunk[ti] // DQ))
-
         for quad in range(4):
             nc.sync.dma_start(
                 out=w_scales[32 * quad : 32 * quad + 4].bitcast(I32),
                 in_=W3_scales[:, 4 * quad : 4 * quad + 4, :].bitcast(I32).rearrange("g r n -> r g n"),
             )
         nc.sync.dma_start(out=b_rows[0:CT, :], in_=b3.rearrange("(r c) -> r c", c=P))
-        park_x0(0)
-        spread_x0(0, 0)
         for ti in range(1, ntile):
-            park_x0(ti)
+            load_x0(ti)
+
+        ident = const.tile([P, P], F32)
+        make_identity(nc, ident[:])
+
+        x2 = const.tile([P, ntile, 2, D, 4], BF16, name="x2")
+
+        def interleave_x0(ti):
+            nc.vector.tensor_copy(out=x2[:, ti], in_=x1[:, ti, :].rearrange("p (jh t d) -> p jh d t", jh=2, t=4))
+
+        def park_x0(ti):
+            nh = P // TILES[ti][1]
+            for jh in range(2):
+                rows = out[park0[ti, jh] : park0[ti, jh] + park_rows[ti], :].rearrange("r c -> (r c)")
+                for dh in range(nh):
+                    nc.sync.dma_start(
+                        out=rows.rearrange("(u dh b w) -> dh b u w", u=nunit[ti], dh=nh, w=2 * US)[dh],
+                        in_=x2[skip[ti] : P, ti, jh]
+                        .rearrange("p (dh u d8) t -> p dh u (d8 t)", dh=nh, u=nunit[ti])[:, dh]
+                        .bitcast(F32),
+                    )
+
+        xs = []
+        for ti in range(ntile):
+            xs_tile = const.tile([P, nunit[ti], P * US * 4], BF16, name="xs%d" % ti)
+            xs.append(xs_tile)
+
+        def spread_x0(ti, u):
+            for jh in range(2):
+                r = park0[ti, jh] + UROWS * u
+                nc.sync.dma_start(
+                    out=xs[ti][jh:P:2, u, :].bitcast(F32),
+                    in_=out[r : r + UROWS, :].rearrange("r c -> (r c)").partition_broadcast(P // 2),
+                )
+
+        interleave_x0(0)
+        park_x0(0)
+        for u in range(nunit[0]):
+            spread_x0(0, u)
         for ti in range(1, ntile):
             load_h2(ti)
+        for ti in range(1, ntile):
+            interleave_x0(ti)
+            park_x0(ti)
+        for ti in range(1, ntile):
+            for u in range(nunit[ti]):
+                spread_x0(ti, u)
 
         fold = const.tile([P, P], F32, name="fold")
         nc.vector.memset(fold[:].bitcast(I32), 0)
-        nc.vector.tensor_tensor(out=fold[:, 0 : P // 2], in0=ident[:, 0:P:2], in1=ident[:, 1:P:2], op=ALU.add)
+        nc.vector.tensor_tensor(out=fold[:, 0 : P // 2], in0=ident[:, 0 : P // 2], in1=ident[:, P // 2 : P], op=ALU.add)
 
         b_rows_f = const.tile([P, P], F32)
         b_cols = y_psum.tile([P, P], F32, tag="y", name="b_cols")
         bias = const.tile([P, CT], F32)
         neg_b = const.tile([P, CT], F32)
         nv_b = {}
-        nv = [len([k for k in range(n) if on_vector(k, 0)]) for n in nchunk]
+        nv = [len([k for k in range(n) if on_vector(k, V_CT)]) for n in nchunk]
 
         def turn_bias():
             nc.vector.tensor_copy(out=b_rows_f[:], in_=b_rows[:])
@@ -153,9 +170,8 @@ def tile_cin_pb_t_kernel(tc, h2, x0, W3_words, W3_scales, b3, out):
                     nv_b[n] = const.tile([P, CT], F32, name="nv_b%d" % n)
                     nc.vector.tensor_scalar(out=nv_b[n][:], in0=b_cols[:, 0:CT], scalar1=float(n), scalar2=None, op0=ALU.mult)
 
+        h4 = {}
         h_t = {}
-        h2e = {}
-        h2p = {}
         z = {}
         z_codes = {}
         z_scales = {}
@@ -166,42 +182,37 @@ def tile_cin_pb_t_kernel(tc, h2, x0, W3_words, W3_scales, b3, out):
         acc_sb = {}
         done = {}
 
-        def turn_h2(c):
+        def fourfold_h2(c, i):
             ti, k = CHUNKS[c]
-            h_t[c] = t_psum.tile([P, 4, P], F32, name="h_t")
-            words = h2_sb[ti][:].bitcast(F32)
-            for wl in range(nwc[ti]):
-                nc.tensor.transpose(h_t[c][:, wl, :], words[:, k * nwc[ti] + wl : H2 * NW : NW], ident[:])
-
-        def double_h2(c):
-            ti, k = CHUNKS[c]
-            nb = TILES[ti][1]
-            h2e[c] = work.tile([P, NCOL, 2], BF16, name="h2e", bufs=3)
+            if i == 0:
+                h4[c] = work.tile([P, DC, 4 * H2], BF16, name="h4", bufs=H_AHEAD - T_AHEAD + 2)
             nc.scalar.copy(
-                out=h2e[c][:].rearrange("p (wl x) e -> p wl x e", wl=nwc[ti]),
-                in_=h_t[c][:, 0 : nwc[ti], skip[ti] : P].bitcast(BF16).unsqueeze(3).to_broadcast([P, nwc[ti], 2 * nb, 2]),
+                out=h4[c][:, i, :].rearrange("p (f q) -> p f q", q=4),
+                in_=h2_sb[ti][:, SHIFT : SHIFT + H2 * D]
+                .rearrange("p (f d) -> p d f", d=D)[:, DC * k + i, :]
+                .unsqueeze(2)
+                .to_broadcast([P, H2, 4]),
             )
-            h2p[c] = work.tile([P, G, NCOL, 2], BF16, name="h2p", bufs=4)
-            for g in range(G):
-                for r in range(2):
-                    nc.sync.dma_start(out=h2p[c][r:P:2, g], in_=h2e[c][FL * g : FL * (g + 1)])
+
+        def turn_h2(c, g):
+            h_t[c, g] = t_psum.tile([P, DC, P], F32, name="h_t")
+            for i in range(DC):
+                nc.tensor.transpose(h_t[c, g][:, i, :], h4[c][:, i, 2 * H2 * g : 2 * H2 * (g + 1)].bitcast(F32), ident[:])
 
         def multiply(c, g):
             ti, k = CHUNKS[c]
-            nb = TILES[ti][1]
-            n = nwc[ti]
             if g == 0:
                 z[c] = work.tile([P, G, NCOL, 4], BF16, name="z", bufs=3, align_bytes=64)
-            w0 = k * n
+            first = DC * k % US
             nc.vector.tensor_tensor(
-                out=z[c][:, g].rearrange("p (wl b d2) (tp e) -> p wl b d2 tp e", wl=n, d2=2, tp=2),
-                in0=h2p[c][:, g]
-                .rearrange("p (wl b d2) e -> p wl b d2 e", wl=n, d2=2)
-                .unsqueeze(4)
-                .to_broadcast([P, n, nb, 2, 2, 2]),
-                in1=xq[ti, w0 // 4][:, 0 : nb * 32].rearrange("p (b wq d2 tp e) -> p wq b d2 tp e", b=nb, wq=4, d2=2, tp=2)[
-                    :, w0 % 4 : w0 % 4 + n
-                ],
+                out=z[c][:, g].rearrange("p (i r) (tp e) -> p i r tp e", i=DC, tp=2),
+                in0=h_t[c, g][:]
+                .rearrange("p i r -> p (i r)")
+                .bitcast(BF16)
+                .rearrange("p (i r e) -> p i r e", i=DC, e=2)
+                .unsqueeze(3)
+                .to_broadcast([P, DC, P, 2, 2]),
+                in1=xs[ti][:, DC * k // US, :].rearrange("p (r d8 tp e) -> p d8 r tp e", d8=US, tp=2, e=2)[:, first : first + DC],
                 op=ALU.mult,
             )
 
@@ -245,22 +256,12 @@ def tile_cin_pb_t_kernel(tc, h2, x0, W3_words, W3_scales, b3, out):
                 )
 
         def relu_scalar(c, ct):
-            ti, k = CHUNKS[c]
             y_relu[c, ct] = work.tile([P, NCOL], F32, name="y_relu", bufs=8)
-            if TILES[ti][1] == P:
-                nc.scalar.activation(
-                    out=y_relu[c, ct][:].rearrange("p (wl d2 b) -> p wl d2 b", wl=2, d2=2),
-                    in_=y[c, ct][:].rearrange("p (wl b d2) -> p wl d2 b", wl=2, d2=2),
-                    func=RELU,
-                    bias=bias[:, ct : ct + 1],
-                    scale=1.0,
-                )
-            else:
-                nc.scalar.activation(out=y_relu[c, ct][:], in_=y[c, ct][:], func=RELU, bias=bias[:, ct : ct + 1], scale=1.0)
+            nc.scalar.activation(out=y_relu[c, ct][:], in_=y[c, ct][:], func=RELU, bias=bias[:, ct : ct + 1], scale=1.0)
 
         def n_adds(ti):
             n = len([1 for k in range(nchunk[ti]) for ct in range(CT) if not on_vector(k, ct)])
-            return (NCOL // P) * (n + (1 if nv[ti] > 0 else 0))
+            return DC * (n + (1 if nv[ti] > 0 else 0))
 
         def add_up(ti, ct, columns):
             if ti not in acc:
@@ -276,21 +277,16 @@ def tile_cin_pb_t_kernel(tc, h2, x0, W3_words, W3_scales, b3, out):
             )
             done[ti] += 1
 
-        def add_scalar(c):
+        def add_scalar(c, cts):
             ti, k = CHUNKS[c]
-            for ct in range(CT):
+            for ct in cts:
                 if not on_vector(k, ct):
-                    for q in range(NCOL // P):
-                        add_up(ti, ct, y_relu[c, ct][:, q * P : (q + 1) * P])
+                    for i in range(DC):
+                        add_up(ti, ct, y_relu[c, ct][:, i * P : (i + 1) * P])
 
         def add_vector(ti):
-            if TILES[ti][1] == P:
-                for wl in range(2):
-                    for d2 in range(2):
-                        add_up(ti, 0, acc_v[ti][:, 2 * P * wl + d2 : 2 * P * (wl + 1) : 2])
-            else:
-                for q in range(NCOL // P):
-                    add_up(ti, 0, acc_v[ti][:, q * P : (q + 1) * P])
+            for i in range(DC):
+                add_up(ti, V_CT, acc_v[ti][:, i * P : (i + 1) * P])
 
         def save_sums(ti):
             acc_sb[ti] = work.tile([P, L3], F32, name="acc_sb", bufs=2)
@@ -317,40 +313,35 @@ def tile_cin_pb_t_kernel(tc, h2, x0, W3_words, W3_scales, b3, out):
         def last_of_tile(c):
             return live(c) and CHUNKS[c][1] == nchunk[CHUNKS[c][0]] - 1
 
-        for s in range(-X_AHEAD, NCHUNK + 3):
-            for (ti, dq) in units:
-                if first_use(ti, dq) - X_AHEAD == s and (ti, dq) not in xq:
-                    spread_x0(ti, dq)
-            if live(s + T_AHEAD):
-                turn_h2(s + T_AHEAD)
-            if live(s + E_AHEAD):
-                double_h2(s + E_AHEAD)
-            if s == -T_AHEAD:
-                turn_bias()
-            if s == -T_AHEAD + 1:
-                save_bias()
-            if live(s - 1):
-                add_scalar(s - 1)
-            if last_of_tile(s - 1):
-                ti = CHUNKS[s - 1][0]
-                if nv[ti] > 0:
-                    add_vector(ti)
-                save_sums(ti)
-            if last_of_tile(s - 2) and TILES[CHUNKS[s - 2][0]][1] < P:
-                fold_sums(CHUNKS[s - 2][0])
-                save_folded(CHUNKS[s - 2][0])
-            if live(s + Q_AHEAD):
-                quantise(s + Q_AHEAD)
-            if live(s + M_AHEAD):
-                multiply(s + M_AHEAD, 0)
-            if live(s):
-                k = CHUNKS[s][1]
-                for ct in range(CT):
-                    multiply_mx(s, ct)
-                for ct in range(CT):
-                    if on_vector(k, ct):
-                        relu_add_vector(s, ct)
-                    else:
-                        relu_scalar(s, ct)
-            if live(s + M_AHEAD):
-                multiply(s + M_AHEAD, 1)
+        for s in range(-H_AHEAD, NCHUNK + 3):
+            if live(s - 1) and on_vector(CHUNKS[s - 1][1], V_CT):
+                relu_add_vector(s - 1, V_CT)
+            for half in range(2):
+                cts = (2 * half, 2 * half + 1)
+                if live(s - 1):
+                    add_scalar(s - 1, cts)
+                if half == 1 and last_of_tile(s - 1):
+                    ti = CHUNKS[s - 1][0]
+                    if nv[ti] > 0:
+                        add_vector(ti)
+                    save_sums(ti)
+                if half == 0 and last_of_tile(s - 2) and TILES[CHUNKS[s - 2][0]][1] < P:
+                    fold_sums(CHUNKS[s - 2][0])
+                    save_folded(CHUNKS[s - 2][0])
+                if live(s + T_AHEAD):
+                    turn_h2(s + T_AHEAD, half)
+                if half == 0 and s == -T_AHEAD - 1:
+                    turn_bias()
+                if half == 1 and s == -T_AHEAD - 1:
+                    save_bias()
+                if live(s + M_AHEAD):
+                    multiply(s + M_AHEAD, half)
+                if half == 0 and live(s + Q_AHEAD):
+                    quantise(s + Q_AHEAD)
+                for ct in cts:
+                    if live(s + H_AHEAD):
+                        fourfold_h2(s + H_AHEAD, ct)
+                    if live(s):
+                        multiply_mx(s, ct)
+                        if not on_vector(CHUNKS[s][1], ct):
+                            relu_scalar(s, ct)

@@ -31,13 +31,13 @@ T_AHEAD = 3
 M_AHEAD = 2
 Q_AHEAD = 1
 V_CT = 3
-V_EVERY = 1
+P_CTS = (1, 2)
 
 FLOPS = 2 * B * D * H2 * F * L3
 
 
 def on_vector(k, ct):
-    return V_EVERY > 0 and ct == V_CT and k % V_EVERY == 0
+    return ct == V_CT
 
 
 def tile_cin_pb_t_kernel(tc, h2, x0, W3_words, W3_scales, b3, out):
@@ -54,6 +54,10 @@ def tile_cin_pb_t_kernel(tc, h2, x0, W3_words, W3_scales, b3, out):
         nchunk = [D * nb // NCOL for (b0, nb) in TILES]
         nunit = [n * DC // US for n in nchunk]
         CHUNKS = [(ti, k) for ti in range(ntile) for k in range(nchunk[ti])]
+
+        def on_pool(ti, k, ct):
+            return ct in P_CTS and not (ti == ntile - 1 and k == nchunk[ti] - 1)
+
         row0 = [b0 + nb - P for (b0, nb) in TILES]
         skip = [P - nb for (b0, nb) in TILES]
         UROWS = P * US * 2 // L3
@@ -179,6 +183,7 @@ def tile_cin_pb_t_kernel(tc, h2, x0, W3_words, W3_scales, b3, out):
         y_relu = {}
         acc = {}
         acc_v = {}
+        acc_p = {}
         acc_sb = {}
         done = {}
 
@@ -256,12 +261,25 @@ def tile_cin_pb_t_kernel(tc, h2, x0, W3_words, W3_scales, b3, out):
                 )
 
         def relu_scalar(c, ct):
-            y_relu[c, ct] = work.tile([P, NCOL], F32, name="y_relu", bufs=8)
+            ti, k = CHUNKS[c]
+            if on_pool(ti, k, ct) and k == 0:
+                acc_p[ti, ct] = work.tile([P, NCOL], F32, name="acc_p%d" % ct, bufs=2)
+                y_relu[c, ct] = acc_p[ti, ct]
+            elif on_pool(ti, k, ct):
+                y_relu[c, ct] = work.tile([P, NCOL], F32, name="y_relu_p", bufs=6)
+            else:
+                y_relu[c, ct] = work.tile([P, NCOL], F32, name="y_relu", bufs=4)
             nc.scalar.activation(out=y_relu[c, ct][:], in_=y[c, ct][:], func=RELU, bias=bias[:, ct : ct + 1], scale=1.0)
 
+        def add_pool(c):
+            ti, k = CHUNKS[c]
+            for ct in P_CTS:
+                if on_pool(ti, k, ct) and k > 0:
+                    nc.gpsimd.tensor_tensor(out=acc_p[ti, ct][:], in0=acc_p[ti, ct][:], in1=y_relu[c, ct][:], op=ALU.add)
+
         def n_adds(ti):
-            n = len([1 for k in range(nchunk[ti]) for ct in range(CT) if not on_vector(k, ct)])
-            return DC * (n + (1 if nv[ti] > 0 else 0))
+            n = len([1 for k in range(nchunk[ti]) for ct in range(CT) if not on_vector(k, ct) and not on_pool(ti, k, ct)])
+            return DC * (n + 1 + len(P_CTS))
 
         def add_up(ti, ct, columns):
             if ti not in acc:
@@ -280,13 +298,16 @@ def tile_cin_pb_t_kernel(tc, h2, x0, W3_words, W3_scales, b3, out):
         def add_scalar(c, cts):
             ti, k = CHUNKS[c]
             for ct in cts:
-                if not on_vector(k, ct):
+                if not on_vector(k, ct) and not on_pool(ti, k, ct):
                     for i in range(DC):
                         add_up(ti, ct, y_relu[c, ct][:, i * P : (i + 1) * P])
 
-        def add_vector(ti):
+        def add_sums(ti):
             for i in range(DC):
                 add_up(ti, V_CT, acc_v[ti][:, i * P : (i + 1) * P])
+            for ct in P_CTS:
+                for i in range(DC):
+                    add_up(ti, ct, acc_p[ti, ct][:, i * P : (i + 1) * P])
 
         def save_sums(ti):
             acc_sb[ti] = work.tile([P, L3], F32, name="acc_sb", bufs=2)
@@ -313,21 +334,27 @@ def tile_cin_pb_t_kernel(tc, h2, x0, W3_words, W3_scales, b3, out):
         def last_of_tile(c):
             return live(c) and CHUNKS[c][1] == nchunk[CHUNKS[c][0]] - 1
 
+        def finished(s):
+            for ti in range(ntile):
+                last = CHUNKS.index((ti, nchunk[ti] - 1))
+                if s == last + (1 if ti == ntile - 1 else 2):
+                    return ti
+            return None
+
         for s in range(-H_AHEAD, NCHUNK + 3):
-            if live(s - 1) and on_vector(CHUNKS[s - 1][1], V_CT):
+            if live(s - 1):
                 relu_add_vector(s - 1, V_CT)
+                add_pool(s - 1)
             for half in range(2):
                 cts = (2 * half, 2 * half + 1)
                 if live(s - 1):
                     add_scalar(s - 1, cts)
-                if half == 1 and last_of_tile(s - 1):
-                    ti = CHUNKS[s - 1][0]
-                    if nv[ti] > 0:
-                        add_vector(ti)
-                    save_sums(ti)
-                if half == 0 and last_of_tile(s - 2) and TILES[CHUNKS[s - 2][0]][1] < P:
-                    fold_sums(CHUNKS[s - 2][0])
-                    save_folded(CHUNKS[s - 2][0])
+                if half == 1 and finished(s) is not None:
+                    add_sums(finished(s))
+                    save_sums(finished(s))
+                if half == 0 and finished(s - 1) is not None and TILES[finished(s - 1)][1] < P:
+                    fold_sums(finished(s - 1))
+                    save_folded(finished(s - 1))
                 if live(s + T_AHEAD):
                     turn_h2(s + T_AHEAD, half)
                 if half == 0 and s == -T_AHEAD - 1:

@@ -26,12 +26,13 @@ NCHUNK = B * D // NCOL
 PARK_ROW = 128
 SHIFT = D // 2
 
+E_AHEAD = 7
 H_AHEAD = 5
 T_AHEAD = 3
 M_AHEAD = 2
 Q_AHEAD = 1
 V_CT = 3
-P_CTS = (1, 2)
+P_CTS = (1,)
 
 FLOPS = 2 * B * D * H2 * F * L3
 
@@ -174,6 +175,7 @@ def tile_cin_pb_t_kernel(tc, h2, x0, W3_words, W3_scales, b3, out):
                     nv_b[n] = const.tile([P, CT], F32, name="nv_b%d" % n)
                     nc.vector.tensor_scalar(out=nv_b[n][:], in0=b_cols[:, 0:CT], scalar1=float(n), scalar2=None, op0=ALU.mult)
 
+        h2e = {}
         h4 = {}
         h_t = {}
         z = {}
@@ -187,16 +189,29 @@ def tile_cin_pb_t_kernel(tc, h2, x0, W3_words, W3_scales, b3, out):
         acc_sb = {}
         done = {}
 
-        def fourfold_h2(c, i):
+        def double_values(c, half):
             ti, k = CHUNKS[c]
+            if half == 0:
+                h2e[c] = work.tile([P, DC, 2 * H2], BF16, name="h2e", bufs=E_AHEAD - H_AHEAD + 2)
+            i0 = half * DC // 2
+            nc.gpsimd.tensor_scalar(
+                out=h2e[c][:, i0 : i0 + DC // 2, :].rearrange("p i (f e) -> p i f e", e=2),
+                in0=h2_sb[ti][:, SHIFT : SHIFT + H2 * D]
+                .rearrange("p (f d) -> p d f", d=D)[:, DC * k + i0 : DC * k + i0 + DC // 2, :]
+                .unsqueeze(3)
+                .to_broadcast([P, DC // 2, H2, 2]),
+                scalar1=1.0,
+                scalar2=0.0,
+                op0=ALU.mult,
+                op1=ALU.add,
+            )
+
+        def double_words(c, i):
             if i == 0:
                 h4[c] = work.tile([P, DC, 4 * H2], BF16, name="h4", bufs=H_AHEAD - T_AHEAD + 2)
             nc.scalar.copy(
-                out=h4[c][:, i, :].rearrange("p (f q) -> p f q", q=4),
-                in_=h2_sb[ti][:, SHIFT : SHIFT + H2 * D]
-                .rearrange("p (f d) -> p d f", d=D)[:, DC * k + i, :]
-                .unsqueeze(2)
-                .to_broadcast([P, H2, 4]),
+                out=h4[c][:, i, :].bitcast(F32).rearrange("p (f r) -> p f r", r=2),
+                in_=h2e[c][:, i, :].bitcast(F32).unsqueeze(2).to_broadcast([P, H2, 2]),
             )
 
         def turn_h2(c, g):
@@ -341,34 +356,42 @@ def tile_cin_pb_t_kernel(tc, h2, x0, W3_words, W3_scales, b3, out):
                     return ti
             return None
 
-        for s in range(-H_AHEAD, NCHUNK + 3):
+        for s in range(-E_AHEAD, NCHUNK + 3):
+            if live(s + M_AHEAD):
+                multiply(s + M_AHEAD, 0)
             if live(s - 1):
-                relu_add_vector(s - 1, V_CT)
                 add_pool(s - 1)
             for half in range(2):
-                cts = (2 * half, 2 * half + 1)
-                if live(s - 1):
-                    add_scalar(s - 1, cts)
-                if half == 1 and finished(s) is not None:
-                    add_sums(finished(s))
-                    save_sums(finished(s))
-                if half == 0 and finished(s - 1) is not None and TILES[finished(s - 1)][1] < P:
-                    fold_sums(finished(s - 1))
-                    save_folded(finished(s - 1))
-                if live(s + T_AHEAD):
-                    turn_h2(s + T_AHEAD, half)
-                if half == 0 and s == -T_AHEAD - 1:
-                    turn_bias()
-                if half == 1 and s == -T_AHEAD - 1:
-                    save_bias()
-                if live(s + M_AHEAD):
-                    multiply(s + M_AHEAD, half)
-                if half == 0 and live(s + Q_AHEAD):
-                    quantise(s + Q_AHEAD)
-                for ct in cts:
-                    if live(s + H_AHEAD):
-                        fourfold_h2(s + H_AHEAD, ct)
-                    if live(s):
-                        multiply_mx(s, ct)
-                        if not on_vector(CHUNKS[s][1], ct):
-                            relu_scalar(s, ct)
+                if live(s + E_AHEAD):
+                    double_values(s + E_AHEAD, half)
+            if live(s):
+                for ct in (0, 1):
+                    multiply_mx(s, ct)
+                    relu_scalar(s, ct)
+            if live(s - 1):
+                relu_add_vector(s - 1, V_CT)
+            if live(s + Q_AHEAD):
+                quantise(s + Q_AHEAD)
+            if live(s + H_AHEAD):
+                for i in range(DC):
+                    double_words(s + H_AHEAD, i)
+            if finished(s - 1) is not None and TILES[finished(s - 1)][1] < P:
+                fold_sums(finished(s - 1))
+                save_folded(finished(s - 1))
+            if live(s - 1):
+                add_scalar(s - 1, range(CT))
+            if finished(s) is not None:
+                add_sums(finished(s))
+                save_sums(finished(s))
+            if live(s + T_AHEAD):
+                for g in range(G):
+                    turn_h2(s + T_AHEAD, g)
+            if s == -T_AHEAD - 1:
+                turn_bias()
+                save_bias()
+            if live(s + M_AHEAD):
+                multiply(s + M_AHEAD, 1)
+            if live(s):
+                multiply_mx(s, 2)
+                relu_scalar(s, 2)
+                multiply_mx(s, 3)

@@ -31,14 +31,8 @@ H_AHEAD = 5
 T_AHEAD = 3
 M_AHEAD = 2
 Q_AHEAD = 1
-V_CT = 3
-P_CTS = (1,)
 
 FLOPS = 2 * B * D * H2 * F * L3
-
-
-def on_vector(k, ct):
-    return ct == V_CT
 
 
 def tile_cin_pb_t_kernel(tc, h2, x0, W3_words, W3_scales, b3, out):
@@ -55,10 +49,6 @@ def tile_cin_pb_t_kernel(tc, h2, x0, W3_words, W3_scales, b3, out):
         nchunk = [D * nb // NCOL for (b0, nb) in TILES]
         nunit = [n * DC // US for n in nchunk]
         CHUNKS = [(ti, k) for ti in range(ntile) for k in range(nchunk[ti])]
-
-        def on_pool(ti, k, ct):
-            return ct in P_CTS and not (ti == ntile - 1 and k == nchunk[ti] - 1)
-
         row0 = [b0 + nb - P for (b0, nb) in TILES]
         skip = [P - nb for (b0, nb) in TILES]
         UROWS = P * US * 2 // L3
@@ -70,6 +60,24 @@ def tile_cin_pb_t_kernel(tc, h2, x0, W3_words, W3_scales, b3, out):
                 park0[ti, jh] = row
                 row += park_rows[ti]
 
+        def owner(c, ct):
+            if ct == 3:
+                return "V" if CHUNKS[c][1] % 2 == 0 or c == NCHUNK - 1 else "G"
+            if ct == 1 and c != NCHUNK - 1:
+                return "G"
+            return "T"
+
+        SUMS = (("V", 3), ("G", 1), ("G", 3))
+
+        def users(ti, who, ct):
+            return [c for c in range(NCHUNK) if CHUNKS[c][0] == ti and owner(c, ct) == who]
+
+        def flush_step(ti, who, ct):
+            return users(ti, who, ct)[-1] + (1 if who == "V" else 2)
+
+        def finish_step(ti):
+            return max([CHUNKS.index((ti, nchunk[ti] - 1)) + 1] + [flush_step(ti, who, ct) for (who, ct) in SUMS])
+
         x1 = const.tile([P, ntile, F * D], BF16, name="x1")
 
         def load_x0(ti):
@@ -80,32 +88,26 @@ def tile_cin_pb_t_kernel(tc, h2, x0, W3_words, W3_scales, b3, out):
         for ti in range(ntile):
             h2_tile = const.tile([P, H2 * D + SHIFT], BF16, name="h2_tile%d" % ti)
             h2_sb.append(h2_tile)
+        for g in range(G):
+            nc.scalar.dma_start(
+                out=h2_sb[0][:, SHIFT + FL * D * g : SHIFT + FL * D * (g + 1)],
+                in_=h2[0:P, FL * g : FL * (g + 1), :].rearrange("b f d -> b (f d)"),
+            )
 
         def load_h2(ti):
             b0, nb = TILES[ti]
             rows = h2[b0 : b0 + nb].rearrange("b f d -> b (f d)")
             if nb == P:
-                nc.scalar.dma_start(out=h2_sb[ti][:, SHIFT : SHIFT + H2 * D], in_=rows)
+                nc.sync.dma_start(out=h2_sb[ti][:, SHIFT : SHIFT + H2 * D], in_=rows)
             else:
-                nc.scalar.dma_start(out=h2_sb[ti][0:nb, SHIFT : SHIFT + H2 * D], in_=rows)
-                nc.scalar.dma_start(out=h2_sb[ti][nb:P, 0 : H2 * D], in_=rows)
+                nc.sync.dma_start(out=h2_sb[ti][0:nb, SHIFT : SHIFT + H2 * D], in_=rows)
+                nc.sync.dma_start(out=h2_sb[ti][nb:P, 0 : H2 * D], in_=rows)
 
-        load_h2(0)
         w_words = const.tile([P, G, 2 * L3], U8, align_bytes=64)
-        nc.sync.dma_start(out=w_words[:].bitcast(I32), in_=W3_words.bitcast(I32).rearrange("g p n -> p g n"))
         w_scales = const.tile([P, G, L3], U8, align_bytes=64)
         nc.vector.memset(w_scales[:].bitcast(I32), 0)
         b_rows = const.tile([P, P], BF16)
         nc.vector.memset(b_rows[:].bitcast(I32), 0)
-        for quad in range(4):
-            nc.sync.dma_start(
-                out=w_scales[32 * quad : 32 * quad + 4].bitcast(I32),
-                in_=W3_scales[:, 4 * quad : 4 * quad + 4, :].bitcast(I32).rearrange("g r n -> r g n"),
-            )
-        nc.sync.dma_start(out=b_rows[0:CT, :], in_=b3.rearrange("(r c) -> r c", c=P))
-        for ti in range(1, ntile):
-            load_x0(ti)
-
         ident = const.tile([P, P], F32)
         make_identity(nc, ident[:])
 
@@ -131,37 +133,54 @@ def tile_cin_pb_t_kernel(tc, h2, x0, W3_words, W3_scales, b3, out):
             xs_tile = const.tile([P, nunit[ti], P * US * 4], BF16, name="xs%d" % ti)
             xs.append(xs_tile)
 
-        def spread_x0(ti, u):
-            for jh in range(2):
-                r = park0[ti, jh] + UROWS * u
-                nc.sync.dma_start(
-                    out=xs[ti][jh:P:2, u, :].bitcast(F32),
-                    in_=out[r : r + UROWS, :].rearrange("r c -> (r c)").partition_broadcast(P // 2),
-                )
+        def spread_x0(ti):
+            for u in range(nunit[ti]):
+                for jh in range(2):
+                    r = park0[ti, jh] + UROWS * u
+                    nc.sync.dma_start(
+                        out=xs[ti][jh:P:2, u, :].bitcast(F32),
+                        in_=out[r : r + UROWS, :].rearrange("r c -> (r c)").partition_broadcast(P // 2),
+                    )
 
         interleave_x0(0)
         park_x0(0)
-        for u in range(nunit[0]):
-            spread_x0(0, u)
-        for ti in range(1, ntile):
-            load_h2(ti)
-        for ti in range(1, ntile):
-            interleave_x0(ti)
-            park_x0(ti)
-        for ti in range(1, ntile):
-            for u in range(nunit[ti]):
-                spread_x0(ti, u)
 
-        fold = const.tile([P, P], F32, name="fold")
-        nc.vector.memset(fold[:].bitcast(I32), 0)
-        nc.vector.tensor_tensor(out=fold[:, 0 : P // 2], in0=ident[:, 0 : P // 2], in1=ident[:, P // 2 : P], op=ALU.add)
+        x_rows = const.tile([P, 2 * DC, P], F32, name="x_rows")
+        nc.vector.tensor_copy(
+            out=x_rows[:].rearrange("p a (fl jh) -> p a fl jh", jh=2),
+            in_=x2[:, 0]
+            .rearrange("p jh d t -> p jh (d t)")
+            .bitcast(F32)[:, :, 0 : 2 * DC]
+            .rearrange("p jh a -> p a jh")
+            .unsqueeze(2)
+            .to_broadcast([P, 2 * DC, P // 2, 2]),
+        )
+        nc.sync.dma_start(out=w_words[:].bitcast(I32), in_=W3_words.bitcast(I32).rearrange("g p n -> p g n"))
+        for quad in range(4):
+            nc.sync.dma_start(
+                out=w_scales[32 * quad : 32 * quad + 4].bitcast(I32),
+                in_=W3_scales[:, 4 * quad : 4 * quad + 4, :].bitcast(I32).rearrange("g r n -> r g n"),
+            )
+        nc.sync.dma_start(out=b_rows[0:CT, :], in_=b3.rearrange("(r c) -> r c", c=P))
+        for ti in range(1, ntile):
+            load_x0(ti)
+        spread_x0(0)
+        load_h2(1)
+
+        def late_loads():
+            for ti in range(1, ntile):
+                interleave_x0(ti)
+                park_x0(ti)
+            spread_x0(1)
+            load_h2(2)
+            spread_x0(2)
 
         b_rows_f = const.tile([P, P], F32)
         b_cols = y_psum.tile([P, P], F32, tag="y", name="b_cols")
         bias = const.tile([P, CT], F32)
         neg_b = const.tile([P, CT], F32)
         nv_b = {}
-        nv = [len([k for k in range(n) if on_vector(k, V_CT)]) for n in nchunk]
+        nv = [len(users(ti, "V", 3)) for ti in range(ntile)]
 
         def turn_bias():
             nc.vector.tensor_copy(out=b_rows_f[:], in_=b_rows[:])
@@ -171,9 +190,29 @@ def tile_cin_pb_t_kernel(tc, h2, x0, W3_words, W3_scales, b3, out):
             nc.vector.tensor_copy(out=bias[:], in_=b_cols[:, 0:CT])
             nc.vector.tensor_scalar(out=neg_b[:], in0=b_cols[:, 0:CT], scalar1=-1.0, scalar2=None, op0=ALU.mult)
             for n in sorted(set(nv)):
-                if n > 0:
-                    nv_b[n] = const.tile([P, CT], F32, name="nv_b%d" % n)
-                    nc.vector.tensor_scalar(out=nv_b[n][:], in0=b_cols[:, 0:CT], scalar1=float(n), scalar2=None, op0=ALU.mult)
+                nv_b[n] = const.tile([P, CT], F32, name="nv_b%d" % n)
+                nc.vector.tensor_scalar(out=nv_b[n][:], in0=b_cols[:, 0:CT], scalar1=float(n), scalar2=None, op0=ALU.mult)
+
+        x_first = const.tile([P, DC, P, 4], BF16, name="x_first")
+        x_cols = []
+        for h in range(2):
+            x_cols_h = y_psum.tile([P, DC, P], F32, tag="y", name="x_cols%d" % h)
+            x_cols.append(x_cols_h)
+            for a in range(DC):
+                nc.tensor.transpose(x_cols_h[:, a, :], x_rows[:, DC * h + a, :], ident[:])
+
+        def save_first(h, copy):
+            copy(
+                out=x_first[:, 2 * h : 2 * h + 2].rearrange("p i r t -> p i (r t)").bitcast(F32).rearrange("p i (r tp) -> p i r tp", tp=2),
+                in_=x_cols[h][:].rearrange("p (i tp) r -> p i r tp", tp=2),
+            )
+
+        save_first(0, nc.scalar.copy)
+        save_first(1, nc.vector.tensor_copy)
+
+        fold = const.tile([P, P], F32, name="fold")
+        nc.vector.memset(fold[:].bitcast(I32), 0)
+        nc.vector.tensor_tensor(out=fold[:, 0 : P // 2], in0=ident[:, 0 : P // 2], in1=ident[:, P // 2 : P], op=ALU.add)
 
         h2e = {}
         h4 = {}
@@ -184,22 +223,27 @@ def tile_cin_pb_t_kernel(tc, h2, x0, W3_words, W3_scales, b3, out):
         y = {}
         y_relu = {}
         acc = {}
-        acc_v = {}
-        acc_p = {}
+        sums = {}
         acc_sb = {}
         done = {}
+        folded = {}
+
+        def h2_slots(c, i0, n, f0, nf):
+            ti, k = CHUNKS[c]
+            return h2_sb[ti][:, SHIFT : SHIFT + H2 * D].rearrange("p (f d) -> p d f", d=D)[
+                :, DC * k + i0 : DC * k + i0 + n, f0 : f0 + nf
+            ]
+
+        def new_h4(c):
+            h4[c] = work.tile([P, DC, 4 * H2], BF16, name="h4", bufs=H_AHEAD - T_AHEAD + 2)
 
         def double_values(c, half):
-            ti, k = CHUNKS[c]
             if half == 0:
                 h2e[c] = work.tile([P, DC, 2 * H2], BF16, name="h2e", bufs=E_AHEAD - H_AHEAD + 2)
             i0 = half * DC // 2
             nc.gpsimd.tensor_scalar(
                 out=h2e[c][:, i0 : i0 + DC // 2, :].rearrange("p i (f e) -> p i f e", e=2),
-                in0=h2_sb[ti][:, SHIFT : SHIFT + H2 * D]
-                .rearrange("p (f d) -> p d f", d=D)[:, DC * k + i0 : DC * k + i0 + DC // 2, :]
-                .unsqueeze(3)
-                .to_broadcast([P, DC // 2, H2, 2]),
+                in0=h2_slots(c, i0, DC // 2, 0, H2).unsqueeze(3).to_broadcast([P, DC // 2, H2, 2]),
                 scalar1=1.0,
                 scalar2=0.0,
                 op0=ALU.mult,
@@ -207,11 +251,15 @@ def tile_cin_pb_t_kernel(tc, h2, x0, W3_words, W3_scales, b3, out):
             )
 
         def double_words(c, i):
-            if i == 0:
-                h4[c] = work.tile([P, DC, 4 * H2], BF16, name="h4", bufs=H_AHEAD - T_AHEAD + 2)
             nc.scalar.copy(
                 out=h4[c][:, i, :].bitcast(F32).rearrange("p (f r) -> p f r", r=2),
                 in_=h2e[c][:, i, :].bitcast(F32).unsqueeze(2).to_broadcast([P, H2, 2]),
+            )
+
+        def fourfold_first(g):
+            nc.vector.tensor_copy(
+                out=h4[0][:, :, 4 * FL * g : 4 * FL * (g + 1)].rearrange("p i (f q) -> p i f q", q=4),
+                in_=h2_slots(0, 0, DC, FL * g, FL).unsqueeze(3).to_broadcast([P, DC, FL, 4]),
             )
 
         def turn_h2(c, g):
@@ -232,7 +280,11 @@ def tile_cin_pb_t_kernel(tc, h2, x0, W3_words, W3_scales, b3, out):
                 .rearrange("p (i r e) -> p i r e", i=DC, e=2)
                 .unsqueeze(3)
                 .to_broadcast([P, DC, P, 2, 2]),
-                in1=xs[ti][:, DC * k // US, :].rearrange("p (r d8 tp e) -> p d8 r tp e", d8=US, tp=2, e=2)[:, first : first + DC],
+                in1=(
+                    x_first[:].rearrange("p i r (tp e) -> p i r tp e", tp=2)
+                    if c == 0
+                    else xs[ti][:, DC * k // US, :].rearrange("p (r d8 tp e) -> p d8 r tp e", d8=US, tp=2, e=2)[:, first : first + DC]
+                ),
                 op=ALU.mult,
             )
 
@@ -259,11 +311,11 @@ def tile_cin_pb_t_kernel(tc, h2, x0, W3_words, W3_scales, b3, out):
                 )
 
         def relu_add_vector(c, ct):
-            ti, k = CHUNKS[c]
-            if ti not in acc_v:
-                acc_v[ti] = work.tile([P, NCOL], F32, name="acc_v", bufs=2)
+            ti = CHUNKS[c][0]
+            if c == users(ti, "V", ct)[0]:
+                sums[ti, "V", ct] = work.tile([P, NCOL], F32, name="sum_v", bufs=2)
                 nc.vector.tensor_scalar(
-                    out=acc_v[ti][:],
+                    out=sums[ti, "V", ct][:],
                     in0=y[c, ct][:],
                     scalar1=neg_b[:, ct : ct + 1],
                     scalar2=nv_b[nv[ti]][:, ct : ct + 1],
@@ -272,57 +324,48 @@ def tile_cin_pb_t_kernel(tc, h2, x0, W3_words, W3_scales, b3, out):
                 )
             else:
                 nc.vector.scalar_tensor_tensor(
-                    out=acc_v[ti][:], in0=y[c, ct][:], scalar=neg_b[:, ct : ct + 1], in1=acc_v[ti][:], op0=ALU.max, op1=ALU.add
+                    out=sums[ti, "V", ct][:],
+                    in0=y[c, ct][:],
+                    scalar=neg_b[:, ct : ct + 1],
+                    in1=sums[ti, "V", ct][:],
+                    op0=ALU.max,
+                    op1=ALU.add,
                 )
 
         def relu_scalar(c, ct):
-            ti, k = CHUNKS[c]
-            if on_pool(ti, k, ct) and k == 0:
-                acc_p[ti, ct] = work.tile([P, NCOL], F32, name="acc_p%d" % ct, bufs=2)
-                y_relu[c, ct] = acc_p[ti, ct]
-            elif on_pool(ti, k, ct):
-                y_relu[c, ct] = work.tile([P, NCOL], F32, name="y_relu_p", bufs=6)
+            ti = CHUNKS[c][0]
+            if owner(c, ct) == "G" and c == users(ti, "G", ct)[0]:
+                sums[ti, "G", ct] = work.tile([P, NCOL], F32, name="sum_g%d" % ct, bufs=2)
+                y_relu[c, ct] = sums[ti, "G", ct]
+            elif owner(c, ct) == "G":
+                y_relu[c, ct] = work.tile([P, NCOL], F32, name="y_relu_g", bufs=6)
             else:
                 y_relu[c, ct] = work.tile([P, NCOL], F32, name="y_relu", bufs=4)
             nc.scalar.activation(out=y_relu[c, ct][:], in_=y[c, ct][:], func=RELU, bias=bias[:, ct : ct + 1], scale=1.0)
 
-        def add_pool(c):
-            ti, k = CHUNKS[c]
-            for ct in P_CTS:
-                if on_pool(ti, k, ct) and k > 0:
-                    nc.gpsimd.tensor_tensor(out=acc_p[ti, ct][:], in0=acc_p[ti, ct][:], in1=y_relu[c, ct][:], op=ALU.add)
+        def add_gpsimd(c):
+            ti = CHUNKS[c][0]
+            for ct in range(CT):
+                if owner(c, ct) == "G" and c != users(ti, "G", ct)[0]:
+                    nc.gpsimd.tensor_tensor(out=sums[ti, "G", ct][:], in0=sums[ti, "G", ct][:], in1=y_relu[c, ct][:], op=ALU.add)
 
         def n_adds(ti):
-            n = len([1 for k in range(nchunk[ti]) for ct in range(CT) if not on_vector(k, ct) and not on_pool(ti, k, ct)])
-            return DC * (n + 1 + len(P_CTS))
+            return DC * (sum([len(users(ti, "T", ct)) for ct in range(CT)]) + len(SUMS))
 
         def add_up(ti, ct, columns):
             if ti not in acc:
                 acc[ti] = a_psum.tile([P, CT, P], F32, name="acc")
                 done[ti] = 0
-            nc.tensor.matmul(
-                out=acc[ti][:, ct, :],
-                lhsT=columns,
-                rhs=ident[:],
-                is_transpose=True,
-                start=(done[ti] == 0),
-                stop=(done[ti] == n_adds(ti) - 1),
-            )
-            done[ti] += 1
-
-        def add_scalar(c, cts):
-            ti, k = CHUNKS[c]
-            for ct in cts:
-                if not on_vector(k, ct) and not on_pool(ti, k, ct):
-                    for i in range(DC):
-                        add_up(ti, ct, y_relu[c, ct][:, i * P : (i + 1) * P])
-
-        def add_sums(ti):
             for i in range(DC):
-                add_up(ti, V_CT, acc_v[ti][:, i * P : (i + 1) * P])
-            for ct in P_CTS:
-                for i in range(DC):
-                    add_up(ti, ct, acc_p[ti, ct][:, i * P : (i + 1) * P])
+                nc.tensor.matmul(
+                    out=acc[ti][:, ct, :],
+                    lhsT=columns[:, i * P : (i + 1) * P],
+                    rhs=ident[:],
+                    is_transpose=True,
+                    start=(done[ti] == 0),
+                    stop=(done[ti] == n_adds(ti) - 1),
+                )
+                done[ti] += 1
 
         def save_sums(ti):
             acc_sb[ti] = work.tile([P, L3], F32, name="acc_sb", bufs=2)
@@ -331,13 +374,9 @@ def tile_cin_pb_t_kernel(tc, h2, x0, W3_words, W3_scales, b3, out):
             if nb == P:
                 nc.sync.dma_start(out=out[b0 : b0 + nb, :], in_=acc_sb[ti][:])
 
-        folded = {}
-
         def fold_sums(ti):
             folded[ti] = y_psum.tile([P, L3], F32, name="folded", tag="y")
             nc.tensor.matmul(out=folded[ti][:], lhsT=fold[:], rhs=acc_sb[ti][:], start=True, stop=True)
-
-        def save_folded(ti):
             b0, nb = TILES[ti]
             out_sb = work.tile([P, L3], F32, name="out_sb", bufs=1)
             nc.scalar.copy(out=out_sb[:], in_=folded[ti][:])
@@ -346,52 +385,56 @@ def tile_cin_pb_t_kernel(tc, h2, x0, W3_words, W3_scales, b3, out):
         def live(c):
             return 0 <= c < NCHUNK
 
-        def last_of_tile(c):
-            return live(c) and CHUNKS[c][1] == nchunk[CHUNKS[c][0]] - 1
-
-        def finished(s):
-            for ti in range(ntile):
-                last = CHUNKS.index((ti, nchunk[ti] - 1))
-                if s == last + (1 if ti == ntile - 1 else 2):
-                    return ti
-            return None
-
         for s in range(-E_AHEAD, NCHUNK + 3):
             if live(s + M_AHEAD):
                 multiply(s + M_AHEAD, 0)
             if live(s - 1):
-                add_pool(s - 1)
-            for half in range(2):
-                if live(s + E_AHEAD):
+                add_gpsimd(s - 1)
+            if live(s + E_AHEAD) and s + E_AHEAD > 0:
+                for half in range(2):
                     double_values(s + E_AHEAD, half)
             if live(s):
                 for ct in (0, 1):
                     multiply_mx(s, ct)
                     relu_scalar(s, ct)
-            if live(s - 1):
-                relu_add_vector(s - 1, V_CT)
+            if live(s - 1) and owner(s - 1, 3) == "V":
+                relu_add_vector(s - 1, 3)
             if live(s + Q_AHEAD):
                 quantise(s + Q_AHEAD)
+            if s == -Q_AHEAD:
+                save_bias()
             if live(s + H_AHEAD):
-                for i in range(DC):
-                    double_words(s + H_AHEAD, i)
-            if finished(s - 1) is not None and TILES[finished(s - 1)][1] < P:
-                fold_sums(finished(s - 1))
-                save_folded(finished(s - 1))
+                new_h4(s + H_AHEAD)
+                if s + H_AHEAD == 0:
+                    for g in range(G):
+                        fourfold_first(g)
+                else:
+                    for i in range(DC):
+                        double_words(s + H_AHEAD, i)
+            for ti in range(ntile):
+                if s == finish_step(ti) + 1 and TILES[ti][1] < P:
+                    fold_sums(ti)
             if live(s - 1):
-                add_scalar(s - 1, range(CT))
-            if finished(s) is not None:
-                add_sums(finished(s))
-                save_sums(finished(s))
+                for ct in range(CT):
+                    if owner(s - 1, ct) == "T":
+                        add_up(CHUNKS[s - 1][0], ct, y_relu[s - 1, ct])
+            for ti in range(ntile):
+                for (who, ct) in SUMS:
+                    if s == flush_step(ti, who, ct):
+                        add_up(ti, ct, sums[ti, who, ct])
+                if s == finish_step(ti):
+                    save_sums(ti)
             if live(s + T_AHEAD):
                 for g in range(G):
                     turn_h2(s + T_AHEAD, g)
-            if s == -T_AHEAD - 1:
-                turn_bias()
-                save_bias()
             if live(s + M_AHEAD):
                 multiply(s + M_AHEAD, 1)
+            if s == -M_AHEAD:
+                turn_bias()
+                late_loads()
             if live(s):
                 multiply_mx(s, 2)
                 relu_scalar(s, 2)
                 multiply_mx(s, 3)
+                if owner(s, 3) != "V":
+                    relu_scalar(s, 3)

@@ -32,6 +32,12 @@ T_AHEAD = 3
 M_AHEAD = 2
 Q_AHEAD = 1
 
+OWNERS = (("T", "G", "G", "V"), ("T", "G", "G", "V"))
+G_LAST = 1
+G_FLUSH = 3
+S_SLOTS = 2
+E_SLOTS = 1
+
 FLOPS = 2 * B * D * H2 * F * L3
 
 
@@ -61,22 +67,21 @@ def tile_cin_pb_t_kernel(tc, h2, x0, W3_words, W3_scales, b3, out):
                 row += park_rows[ti]
 
         def owner(c, ct):
-            if ct == 3:
-                return "V" if CHUNKS[c][1] % 2 == 0 or c == NCHUNK - 1 else "G"
-            if ct == 1 and c != NCHUNK - 1:
-                return "G"
-            return "T"
-
-        SUMS = (("V", 3), ("G", 1), ("G", 3))
+            who = OWNERS[CHUNKS[c][1] % 2][ct]
+            if who == "G" and c >= NCHUNK - G_LAST:
+                return "T" if c % 2 else "V"
+            return who
 
         def users(ti, who, ct):
             return [c for c in range(NCHUNK) if CHUNKS[c][0] == ti and owner(c, ct) == who]
 
         def flush_step(ti, who, ct):
-            return users(ti, who, ct)[-1] + (1 if who == "V" else 2)
+            return users(ti, who, ct)[-1] + (1 if who == "V" else G_FLUSH)
+
+        SUMS = {ti: [(who, ct) for who in "VG" for ct in range(CT) if users(ti, who, ct)] for ti in range(ntile)}
 
         def finish_step(ti):
-            return max([CHUNKS.index((ti, nchunk[ti] - 1)) + 1] + [flush_step(ti, who, ct) for (who, ct) in SUMS])
+            return max([CHUNKS.index((ti, nchunk[ti] - 1)) + 1] + [flush_step(ti, who, ct) for (who, ct) in SUMS[ti]])
 
         x1 = const.tile([P, ntile, F * D], BF16, name="x1")
 
@@ -180,7 +185,7 @@ def tile_cin_pb_t_kernel(tc, h2, x0, W3_words, W3_scales, b3, out):
         bias = const.tile([P, CT], F32)
         neg_b = const.tile([P, CT], F32)
         nv_b = {}
-        nv = [len(users(ti, "V", 3)) for ti in range(ntile)]
+        nv = {(ti, ct): len(users(ti, "V", ct)) for ti in range(ntile) for ct in range(CT)}
 
         def turn_bias():
             nc.vector.tensor_copy(out=b_rows_f[:], in_=b_rows[:])
@@ -189,10 +194,30 @@ def tile_cin_pb_t_kernel(tc, h2, x0, W3_words, W3_scales, b3, out):
         def save_bias():
             nc.vector.tensor_copy(out=bias[:], in_=b_cols[:, 0:CT])
             nc.vector.tensor_scalar(out=neg_b[:], in0=b_cols[:, 0:CT], scalar1=-1.0, scalar2=None, op0=ALU.mult)
-            for n in sorted(set(nv)):
+            for n in sorted(set(nv.values()) - {0}):
                 nv_b[n] = const.tile([P, CT], F32, name="nv_b%d" % n)
                 nc.vector.tensor_scalar(out=nv_b[n][:], in0=b_cols[:, 0:CT], scalar1=float(n), scalar2=None, op0=ALU.mult)
 
+        h2e = {}
+        h4 = {}
+
+        def h2_slots(c, i0, n, f0, nf):
+            ti, k = CHUNKS[c]
+            return h2_sb[ti][:, SHIFT : SHIFT + H2 * D].rearrange("p (f d) -> p d f", d=D)[
+                :, DC * k + i0 : DC * k + i0 + n, f0 : f0 + nf
+            ]
+
+        def new_h4(c):
+            h4[c] = work.tile([P, DC, 4 * H2], BF16, name="h4", bufs=H_AHEAD - T_AHEAD + 2)
+
+        def fourfold_first(g):
+            nc.vector.tensor_copy(
+                out=h4[0][:, :, 4 * FL * g : 4 * FL * (g + 1)].rearrange("p i (f q) -> p i f q", q=4),
+                in_=h2_slots(0, 0, DC, FL * g, FL).unsqueeze(3).to_broadcast([P, DC, FL, 4]),
+            )
+
+        new_h4(0)
+        fourfold_first(0)
         x_first = const.tile([P, DC, P, 4], BF16, name="x_first")
         x_cols = []
         for h in range(2):
@@ -209,13 +234,14 @@ def tile_cin_pb_t_kernel(tc, h2, x0, W3_words, W3_scales, b3, out):
 
         save_first(0, nc.scalar.copy)
         save_first(1, nc.vector.tensor_copy)
+        fourfold_first(1)
 
         fold = const.tile([P, P], F32, name="fold")
-        nc.vector.memset(fold[:].bitcast(I32), 0)
-        nc.vector.tensor_tensor(out=fold[:, 0 : P // 2], in0=ident[:, 0 : P // 2], in1=ident[:, P // 2 : P], op=ALU.add)
 
-        h2e = {}
-        h4 = {}
+        def fill_fold():
+            nc.vector.memset(fold[:].bitcast(I32), 0)
+            nc.vector.tensor_tensor(out=fold[:, 0 : P // 2], in0=ident[:, 0 : P // 2], in1=ident[:, P // 2 : P], op=ALU.add)
+
         h_t = {}
         z = {}
         z_codes = {}
@@ -228,22 +254,13 @@ def tile_cin_pb_t_kernel(tc, h2, x0, W3_words, W3_scales, b3, out):
         done = {}
         folded = {}
 
-        def h2_slots(c, i0, n, f0, nf):
-            ti, k = CHUNKS[c]
-            return h2_sb[ti][:, SHIFT : SHIFT + H2 * D].rearrange("p (f d) -> p d f", d=D)[
-                :, DC * k + i0 : DC * k + i0 + n, f0 : f0 + nf
-            ]
+        def new_h2e(c):
+            h2e[c] = work.tile([P, DC - S_SLOTS, 2 * H2], BF16, name="h2e", bufs=E_AHEAD - H_AHEAD + 2)
 
-        def new_h4(c):
-            h4[c] = work.tile([P, DC, 4 * H2], BF16, name="h4", bufs=H_AHEAD - T_AHEAD + 2)
-
-        def double_values(c, half):
-            if half == 0:
-                h2e[c] = work.tile([P, DC, 2 * H2], BF16, name="h2e", bufs=E_AHEAD - H_AHEAD + 2)
-            i0 = half * DC // 2
+        def double_values(c, i0, n):
             nc.gpsimd.tensor_scalar(
-                out=h2e[c][:, i0 : i0 + DC // 2, :].rearrange("p i (f e) -> p i f e", e=2),
-                in0=h2_slots(c, i0, DC // 2, 0, H2).unsqueeze(3).to_broadcast([P, DC // 2, H2, 2]),
+                out=h2e[c][:, i0 : i0 + n, :].rearrange("p i (f e) -> p i f e", e=2),
+                in0=h2_slots(c, i0, n, 0, H2).unsqueeze(3).to_broadcast([P, n, H2, 2]),
                 scalar1=1.0,
                 scalar2=0.0,
                 op0=ALU.mult,
@@ -256,10 +273,10 @@ def tile_cin_pb_t_kernel(tc, h2, x0, W3_words, W3_scales, b3, out):
                 in_=h2e[c][:, i, :].bitcast(F32).unsqueeze(2).to_broadcast([P, H2, 2]),
             )
 
-        def fourfold_first(g):
-            nc.vector.tensor_copy(
-                out=h4[0][:, :, 4 * FL * g : 4 * FL * (g + 1)].rearrange("p i (f q) -> p i f q", q=4),
-                in_=h2_slots(0, 0, DC, FL * g, FL).unsqueeze(3).to_broadcast([P, DC, FL, 4]),
+        def fourfold_scalar(c, i):
+            nc.scalar.copy(
+                out=h4[c][:, i, :].rearrange("p (f q) -> p f q", q=4),
+                in_=h2_slots(c, i, 1, 0, H2).rearrange("p i f -> p (i f)").unsqueeze(2).to_broadcast([P, H2, 4]),
             )
 
         def turn_h2(c, g):
@@ -313,12 +330,12 @@ def tile_cin_pb_t_kernel(tc, h2, x0, W3_words, W3_scales, b3, out):
         def relu_add_vector(c, ct):
             ti = CHUNKS[c][0]
             if c == users(ti, "V", ct)[0]:
-                sums[ti, "V", ct] = work.tile([P, NCOL], F32, name="sum_v", bufs=2)
+                sums[ti, "V", ct] = work.tile([P, NCOL], F32, name="sum_v%d" % ct, bufs=2)
                 nc.vector.tensor_scalar(
                     out=sums[ti, "V", ct][:],
                     in0=y[c, ct][:],
                     scalar1=neg_b[:, ct : ct + 1],
-                    scalar2=nv_b[nv[ti]][:, ct : ct + 1],
+                    scalar2=nv_b[nv[ti, ct]][:, ct : ct + 1],
                     op0=ALU.max,
                     op1=ALU.add,
                 )
@@ -350,7 +367,7 @@ def tile_cin_pb_t_kernel(tc, h2, x0, W3_words, W3_scales, b3, out):
                     nc.gpsimd.tensor_tensor(out=sums[ti, "G", ct][:], in0=sums[ti, "G", ct][:], in1=y_relu[c, ct][:], op=ALU.add)
 
         def n_adds(ti):
-            return DC * (sum([len(users(ti, "T", ct)) for ct in range(CT)]) + len(SUMS))
+            return DC * (sum([len(users(ti, "T", ct)) for ct in range(CT)]) + len(SUMS[ti]))
 
         def add_up(ti, ct, columns):
             if ti not in acc:
@@ -385,32 +402,45 @@ def tile_cin_pb_t_kernel(tc, h2, x0, W3_words, W3_scales, b3, out):
         def live(c):
             return 0 <= c < NCHUNK
 
-        for s in range(-E_AHEAD, NCHUNK + 3):
+        for s in range(-E_AHEAD, NCHUNK + 1 + G_FLUSH):
+            if s + Q_AHEAD == 0:
+                quantise(0)
+                turn_bias()
+                save_bias()
+                for ct in (0, 1):
+                    multiply_mx(0, ct)
+                    if owner(0, ct) != "V":
+                        relu_scalar(0, ct)
             if live(s + M_AHEAD):
                 multiply(s + M_AHEAD, 0)
+            if s + Q_AHEAD == 0:
+                late_loads()
+            if s == 2:
+                fill_fold()
             if live(s - 1):
                 add_gpsimd(s - 1)
             if live(s + E_AHEAD) and s + E_AHEAD > 0:
-                for half in range(2):
-                    double_values(s + E_AHEAD, half)
-            if live(s):
+                new_h2e(s + E_AHEAD)
+                for i in range(0, DC - S_SLOTS, E_SLOTS):
+                    double_values(s + E_AHEAD, i, min(E_SLOTS, DC - S_SLOTS - i))
+            if live(s) and s > 0:
                 for ct in (0, 1):
                     multiply_mx(s, ct)
-                    relu_scalar(s, ct)
-            if live(s - 1) and owner(s - 1, 3) == "V":
-                relu_add_vector(s - 1, 3)
-            if live(s + Q_AHEAD):
+                    if owner(s, ct) != "V":
+                        relu_scalar(s, ct)
+            if live(s - 1):
+                for ct in range(CT):
+                    if owner(s - 1, ct) == "V":
+                        relu_add_vector(s - 1, ct)
+            if live(s + Q_AHEAD) and s + Q_AHEAD > 0:
                 quantise(s + Q_AHEAD)
-            if s == -Q_AHEAD:
-                save_bias()
-            if live(s + H_AHEAD):
+            if live(s + H_AHEAD) and s + H_AHEAD > 0:
                 new_h4(s + H_AHEAD)
-                if s + H_AHEAD == 0:
-                    for g in range(G):
-                        fourfold_first(g)
-                else:
-                    for i in range(DC):
+                for i in range(DC):
+                    if i < DC - S_SLOTS:
                         double_words(s + H_AHEAD, i)
+                    else:
+                        fourfold_scalar(s + H_AHEAD, i)
             for ti in range(ntile):
                 if s == finish_step(ti) + 1 and TILES[ti][1] < P:
                     fold_sums(ti)
@@ -419,7 +449,7 @@ def tile_cin_pb_t_kernel(tc, h2, x0, W3_words, W3_scales, b3, out):
                     if owner(s - 1, ct) == "T":
                         add_up(CHUNKS[s - 1][0], ct, y_relu[s - 1, ct])
             for ti in range(ntile):
-                for (who, ct) in SUMS:
+                for (who, ct) in SUMS[ti]:
                     if s == flush_step(ti, who, ct):
                         add_up(ti, ct, sums[ti, who, ct])
                 if s == finish_step(ti):
@@ -429,12 +459,8 @@ def tile_cin_pb_t_kernel(tc, h2, x0, W3_words, W3_scales, b3, out):
                     turn_h2(s + T_AHEAD, g)
             if live(s + M_AHEAD):
                 multiply(s + M_AHEAD, 1)
-            if s == -M_AHEAD:
-                turn_bias()
-                late_loads()
             if live(s):
-                multiply_mx(s, 2)
-                relu_scalar(s, 2)
-                multiply_mx(s, 3)
-                if owner(s, 3) != "V":
-                    relu_scalar(s, 3)
+                for ct in (2, 3):
+                    multiply_mx(s, ct)
+                    if owner(s, ct) != "V":
+                        relu_scalar(s, ct)

@@ -26,17 +26,26 @@ NCHUNK = B * D // NCOL
 PARK_ROW = 128
 SHIFT = D // 2
 
-E_AHEAD = 7
-H_AHEAD = 5
+E_AHEAD = 5
+H_AHEAD = 4
 T_AHEAD = 3
 M_AHEAD = 2
 Q_AHEAD = 1
 
-OWNERS = (("T", "G", "G", "V"), ("T", "G", "G", "V"))
+OWNERS = (("G", "T", "T", "V"),)
 G_LAST = 1
-G_FLUSH = 3
+G_FLUSH = 2
 S_SLOTS = 2
-E_SLOTS = 1
+E_SLOTS = 2
+ADD_SPLIT = 1
+T_BUFS = 3
+Y_BUFS = 3
+A_BUFS = 2
+RUNS = 1
+G_ORDER = 1
+V_POS = 0
+S_POS = 0
+S_SPLIT = 1
 
 FLOPS = 2 * B * D * H2 * F * L3
 
@@ -46,9 +55,9 @@ def tile_cin_pb_t_kernel(tc, h2, x0, W3_words, W3_scales, b3, out):
     with ExitStack() as ctx:
         const = ctx.enter_context(tc.tile_pool(name="const", bufs=1))
         work = ctx.enter_context(tc.tile_pool(name="work", bufs=3))
-        t_psum = ctx.enter_context(tc.psum_pool(name="t_psum", bufs=3))
-        y_psum = ctx.enter_context(tc.psum_pool(name="y_psum", bufs=3))
-        a_psum = ctx.enter_context(tc.psum_pool(name="a_psum", bufs=2))
+        t_psum = ctx.enter_context(tc.psum_pool(name="t_psum", bufs=T_BUFS))
+        y_psum = ctx.enter_context(tc.psum_pool(name="y_psum", bufs=Y_BUFS))
+        a_psum = ctx.enter_context(tc.psum_pool(name="a_psum", bufs=A_BUFS))
         ctx.enter_context(tc.manual_schedule())
 
         ntile = len(TILES)
@@ -67,7 +76,7 @@ def tile_cin_pb_t_kernel(tc, h2, x0, W3_words, W3_scales, b3, out):
                 row += park_rows[ti]
 
         def owner(c, ct):
-            who = OWNERS[CHUNKS[c][1] % 2][ct]
+            who = OWNERS[CHUNKS[c][1] % len(OWNERS)][ct]
             if who == "G" and c >= NCHUNK - G_LAST:
                 return "T" if c % 2 else "V"
             return who
@@ -135,15 +144,18 @@ def tile_cin_pb_t_kernel(tc, h2, x0, W3_words, W3_scales, b3, out):
 
         xs = []
         for ti in range(ntile):
-            xs_tile = const.tile([P, nunit[ti], P * US * 4], BF16, name="xs%d" % ti)
-            xs.append(xs_tile)
+            xs_units = []
+            for u in range(nunit[ti]):
+                xs_tile = const.tile([P, P * US * 4], BF16, name="xs%d_%d" % (ti, u))
+                xs_units.append(xs_tile)
+            xs.append(xs_units)
 
         def spread_x0(ti):
             for u in range(nunit[ti]):
                 for jh in range(2):
                     r = park0[ti, jh] + UROWS * u
                     nc.sync.dma_start(
-                        out=xs[ti][jh:P:2, u, :].bitcast(F32),
+                        out=xs[ti][u][jh:P:2, :].bitcast(F32),
                         in_=out[r : r + UROWS, :].rearrange("r c -> (r c)").partition_broadcast(P // 2),
                     )
 
@@ -300,7 +312,7 @@ def tile_cin_pb_t_kernel(tc, h2, x0, W3_words, W3_scales, b3, out):
                 in1=(
                     x_first[:].rearrange("p i r (tp e) -> p i r tp e", tp=2)
                     if c == 0
-                    else xs[ti][:, DC * k // US, :].rearrange("p (r d8 tp e) -> p d8 r tp e", d8=US, tp=2, e=2)[:, first : first + DC]
+                    else xs[ti][DC * k // US][:].rearrange("p (r d8 tp e) -> p d8 r tp e", d8=US, tp=2, e=2)[:, first : first + DC]
                 ),
                 op=ALU.mult,
             )
@@ -357,14 +369,18 @@ def tile_cin_pb_t_kernel(tc, h2, x0, W3_words, W3_scales, b3, out):
             elif owner(c, ct) == "G":
                 y_relu[c, ct] = work.tile([P, NCOL], F32, name="y_relu_g", bufs=6)
             else:
-                y_relu[c, ct] = work.tile([P, NCOL], F32, name="y_relu", bufs=4)
+                y_relu[c, ct] = work.tile([P, NCOL], F32, name="y_relu", bufs=8)
             nc.scalar.activation(out=y_relu[c, ct][:], in_=y[c, ct][:], func=RELU, bias=bias[:, ct : ct + 1], scale=1.0)
 
         def add_gpsimd(c):
             ti = CHUNKS[c][0]
             for ct in range(CT):
                 if owner(c, ct) == "G" and c != users(ti, "G", ct)[0]:
-                    nc.gpsimd.tensor_tensor(out=sums[ti, "G", ct][:], in0=sums[ti, "G", ct][:], in1=y_relu[c, ct][:], op=ALU.add)
+                    for a in range(ADD_SPLIT):
+                        cols = slice(NCOL * a // ADD_SPLIT, NCOL * (a + 1) // ADD_SPLIT)
+                        nc.gpsimd.tensor_tensor(
+                            out=sums[ti, "G", ct][:, cols], in0=sums[ti, "G", ct][:, cols], in1=y_relu[c, ct][:, cols], op=ALU.add
+                        )
 
         def n_adds(ti):
             return DC * (sum([len(users(ti, "T", ct)) for ct in range(CT)]) + len(SUMS[ti]))
@@ -402,65 +418,110 @@ def tile_cin_pb_t_kernel(tc, h2, x0, W3_words, W3_scales, b3, out):
         def live(c):
             return 0 <= c < NCHUNK
 
-        for s in range(-E_AHEAD, NCHUNK + 1 + G_FLUSH):
-            if s + Q_AHEAD == 0:
-                quantise(0)
-                turn_bias()
-                save_bias()
-                for ct in (0, 1):
-                    multiply_mx(0, ct)
-                    if owner(0, ct) != "V":
-                        relu_scalar(0, ct)
-            if live(s + M_AHEAD):
-                multiply(s + M_AHEAD, 0)
-            if s + Q_AHEAD == 0:
-                late_loads()
-            if s == 2:
-                fill_fold()
+        def st_adds(s):
             if live(s - 1):
                 add_gpsimd(s - 1)
+
+        def st_dbl(s):
             if live(s + E_AHEAD) and s + E_AHEAD > 0:
                 new_h2e(s + E_AHEAD)
                 for i in range(0, DC - S_SLOTS, E_SLOTS):
                     double_values(s + E_AHEAD, i, min(E_SLOTS, DC - S_SLOTS - i))
-            if live(s) and s > 0:
-                for ct in (0, 1):
+
+        def st_mx(s, cts):
+            if live(s):
+                for ct in cts:
                     multiply_mx(s, ct)
                     if owner(s, ct) != "V":
                         relu_scalar(s, ct)
+
+        def st_vrelu(s):
             if live(s - 1):
                 for ct in range(CT):
                     if owner(s - 1, ct) == "V":
                         relu_add_vector(s - 1, ct)
-            if live(s + Q_AHEAD) and s + Q_AHEAD > 0:
-                quantise(s + Q_AHEAD)
+
+        def st_words(s, part):
             if live(s + H_AHEAD) and s + H_AHEAD > 0:
-                new_h4(s + H_AHEAD)
-                for i in range(DC):
+                if part == 0:
+                    new_h4(s + H_AHEAD)
+                for i in ((0, 1, 2, 3) if S_SPLIT == 0 and part == 0 else () if S_SPLIT == 0 else (0, 1) if part == 0 else (2, 3)):
                     if i < DC - S_SLOTS:
                         double_words(s + H_AHEAD, i)
                     else:
                         fourfold_scalar(s + H_AHEAD, i)
-            for ti in range(ntile):
-                if s == finish_step(ti) + 1 and TILES[ti][1] < P:
-                    fold_sums(ti)
+
+        def st_acc(s, cts):
             if live(s - 1):
-                for ct in range(CT):
+                for ct in cts:
                     if owner(s - 1, ct) == "T":
                         add_up(CHUNKS[s - 1][0], ct, y_relu[s - 1, ct])
+
+        def st_flush(s):
             for ti in range(ntile):
                 for (who, ct) in SUMS[ti]:
                     if s == flush_step(ti, who, ct):
                         add_up(ti, ct, sums[ti, who, ct])
                 if s == finish_step(ti):
                     save_sums(ti)
+
+        def st_turn(s, g):
             if live(s + T_AHEAD):
-                for g in range(G):
-                    turn_h2(s + T_AHEAD, g)
+                turn_h2(s + T_AHEAD, g)
+
+        for s in range(-E_AHEAD, NCHUNK + 1 + G_FLUSH):
+            if s == -1:
+                quantise(0)
+                turn_bias()
+                save_bias()
+                st_mx(0, (0, 1))
             if live(s + M_AHEAD):
-                multiply(s + M_AHEAD, 1)
-            if live(s):
-                for ct in (2, 3):
-                    multiply_mx(s, ct)
-                    if owner(s, ct) != "V":
-                        relu_scalar(s, ct)
+                multiply(s + M_AHEAD, 0)
+            if s == -1:
+                late_loads()
+            if s == 2:
+                fill_fold()
+            if G_ORDER == 0:
+                st_adds(s)
+                st_dbl(s)
+            else:
+                st_dbl(s)
+                st_adds(s)
+            if S_POS == 0:
+                st_words(s, 0)
+            if s > 0:
+                st_mx(s, (0, 1))
+            if V_POS == 0:
+                st_vrelu(s)
+            if live(s + Q_AHEAD) and s + Q_AHEAD > 0:
+                quantise(s + Q_AHEAD)
+            if V_POS == 1:
+                st_vrelu(s)
+            if S_POS == 1:
+                st_words(s, 0)
+            for ti in range(ntile):
+                if s == finish_step(ti) + 1 and TILES[ti][1] < P:
+                    fold_sums(ti)
+            st_acc(s, (0, 1, 2, 3) if RUNS == 1 else (0, 1))
+            if RUNS == 1:
+                st_flush(s)
+                st_turn(s, 0)
+                st_turn(s, 1)
+                if live(s + M_AHEAD):
+                    multiply(s + M_AHEAD, 1)
+                if V_POS == 2:
+                    st_vrelu(s)
+                st_mx(s, (2, 3))
+            else:
+                st_turn(s, 0)
+                if live(s + M_AHEAD):
+                    multiply(s + M_AHEAD, 1)
+                if V_POS == 2:
+                    st_vrelu(s)
+                st_mx(s, (2, 3))
+                st_acc(s, (2, 3))
+                st_flush(s)
+                st_turn(s, 1)
+            st_words(s, 1)
+            if S_POS == 2:
+                st_words(s, 0)

@@ -35,13 +35,22 @@ Q_AHEAD = 1
 OWNERS = (("G", "T", "T", "V"),)
 G_LAST = 1
 G_FLUSH = 2
-S_SLOTS = 2
+S_SLOTS = (2,)
+V_SLOTS = 0
+XF = 1
+LAST = 0
+Z_BUFS = 3
+S_FIRST = 1
+X2_STEP = -2
+H2E_BUFS = 3
+H2_EARLY = 0
 E_SLOTS = 2
 ADD_SPLIT = 1
 T_BUFS = 3
 Y_BUFS = 3
 A_BUFS = 2
 RUNS = 1
+PE_ORDER = 0
 G_ORDER = 1
 V_POS = 0
 S_POS = 0
@@ -75,6 +84,9 @@ def tile_cin_pb_t_kernel(tc, h2, x0, W3_words, W3_scales, b3, out):
                 park0[ti, jh] = row
                 row += park_rows[ti]
 
+        def g_slots(c):
+            return DC - V_SLOTS - S_SLOTS[c % len(S_SLOTS)]
+
         def owner(c, ct):
             who = OWNERS[CHUNKS[c][1] % len(OWNERS)][ct]
             if who == "G" and c >= NCHUNK - G_LAST:
@@ -85,7 +97,7 @@ def tile_cin_pb_t_kernel(tc, h2, x0, W3_words, W3_scales, b3, out):
             return [c for c in range(NCHUNK) if CHUNKS[c][0] == ti and owner(c, ct) == who]
 
         def flush_step(ti, who, ct):
-            return users(ti, who, ct)[-1] + (1 if who == "V" else G_FLUSH)
+            return users(ti, who, ct)[-1] + ((2 if PE_ORDER else 1) if who == "V" else G_FLUSH)
 
         SUMS = {ti: [(who, ct) for who in "VG" for ct in range(CT) if users(ti, who, ct)] for ti in range(ntile)}
 
@@ -97,7 +109,8 @@ def tile_cin_pb_t_kernel(tc, h2, x0, W3_words, W3_scales, b3, out):
         def load_x0(ti):
             nc.sync.dma_start(out=x1[:, ti, :], in_=x0[row0[ti] : row0[ti] + P].rearrange("b j d -> b (j d)"))
 
-        load_x0(0)
+        for ti in range(ntile):
+            load_x0(ti)
         h2_sb = []
         for ti in range(ntile):
             h2_tile = const.tile([P, H2 * D + SHIFT], BF16, name="h2_tile%d" % ti)
@@ -107,6 +120,10 @@ def tile_cin_pb_t_kernel(tc, h2, x0, W3_words, W3_scales, b3, out):
                 out=h2_sb[0][:, SHIFT + FL * D * g : SHIFT + FL * D * (g + 1)],
                 in_=h2[0:P, FL * g : FL * (g + 1), :].rearrange("b f d -> b (f d)"),
             )
+
+        warm = const.tile([P, 1], F32, name="warm")
+        nc.vector.memset(warm[:], 0.0)
+        nc.scalar.activation(out=warm[:], in_=warm[:], func=RELU)
 
         def load_h2(ti):
             b0, nb = TILES[ti]
@@ -128,7 +145,11 @@ def tile_cin_pb_t_kernel(tc, h2, x0, W3_words, W3_scales, b3, out):
         x2 = const.tile([P, ntile, 2, D, 4], BF16, name="x2")
 
         def interleave_x0(ti):
-            nc.vector.tensor_copy(out=x2[:, ti], in_=x1[:, ti, :].rearrange("p (jh t d) -> p jh d t", jh=2, t=4))
+            src = x1[:, ti, :].rearrange("p (jh t d) -> p jh d t", jh=2, t=4)
+            if ti == 0:
+                nc.vector.tensor_copy(out=x2[:, ti], in_=src)
+            else:
+                nc.gpsimd.tensor_scalar(out=x2[:, ti], in0=src, scalar1=1.0, scalar2=0.0, op0=ALU.mult, op1=ALU.add)
 
         def park_x0(ti):
             nh = P // TILES[ti][1]
@@ -151,7 +172,10 @@ def tile_cin_pb_t_kernel(tc, h2, x0, W3_words, W3_scales, b3, out):
             xs.append(xs_units)
 
         def spread_x0(ti):
-            for u in range(nunit[ti]):
+            spread_units(ti, 0, nunit[ti])
+
+        def spread_units(ti, u0, u1):
+            for u in range(u0, u1):
                 for jh in range(2):
                     r = park0[ti, jh] + UROWS * u
                     nc.sync.dma_start(
@@ -159,8 +183,31 @@ def tile_cin_pb_t_kernel(tc, h2, x0, W3_words, W3_scales, b3, out):
                         in_=out[r : r + UROWS, :].rearrange("r c -> (r c)").partition_broadcast(P // 2),
                     )
 
+        b_rows_f = const.tile([P, P], F32)
+        b_cols = y_psum.tile([P, P], F32, tag="y", name="b_cols")
+        bias = const.tile([P, CT], F32)
+        neg_b = const.tile([P, CT], F32)
+        nv_b = {}
+        nv = {(ti, ct): len(users(ti, "V", ct)) for ti in range(ntile) for ct in range(CT)}
+
+        def turn_bias():
+            nc.scalar.copy(out=b_rows_f[:], in_=b_rows[:])
+            nc.tensor.transpose(b_cols[:], b_rows_f[:], ident[:])
+
+        def save_bias():
+            nc.scalar.copy(out=bias[:], in_=b_cols[:, 0:CT])
+            nc.scalar.mul(out=neg_b[:], in_=b_cols[:, 0:CT], mul=-1.0)
+            for n in sorted(set(nv.values()) - {0}):
+                nv_b[n] = const.tile([P, CT], F32, name="nv_b%d" % n)
+                nc.scalar.mul(out=nv_b[n][:], in_=b_cols[:, 0:CT], mul=float(n))
+
+        fold = const.tile([P, P], F32, name="fold")
+
         interleave_x0(0)
         park_x0(0)
+        nc.sync.dma_start(out=b_rows[0:CT, :], in_=b3.rearrange("(r c) -> r c", c=P))
+        nc.gpsimd.memset(fold[:], 0.0)
+        nc.gpsimd.tensor_tensor(out=fold[:, 0 : P // 2], in0=ident[:, 0 : P // 2], in1=ident[:, P // 2 : P], op=ALU.add)
 
         x_rows = const.tile([P, 2 * DC, P], F32, name="x_rows")
         nc.vector.tensor_copy(
@@ -178,37 +225,20 @@ def tile_cin_pb_t_kernel(tc, h2, x0, W3_words, W3_scales, b3, out):
                 out=w_scales[32 * quad : 32 * quad + 4].bitcast(I32),
                 in_=W3_scales[:, 4 * quad : 4 * quad + 4, :].bitcast(I32).rearrange("g r n -> r g n"),
             )
-        nc.sync.dma_start(out=b_rows[0:CT, :], in_=b3.rearrange("(r c) -> r c", c=P))
-        for ti in range(1, ntile):
-            load_x0(ti)
-        spread_x0(0)
-        load_h2(1)
+        if H2_EARLY:
+            spread_units(0, 0, H2_EARLY)
+            load_h2(1)
+            spread_units(0, H2_EARLY, nunit[0])
+        else:
+            spread_x0(0)
+            load_h2(1)
 
         def late_loads():
             for ti in range(1, ntile):
-                interleave_x0(ti)
                 park_x0(ti)
             spread_x0(1)
             load_h2(2)
             spread_x0(2)
-
-        b_rows_f = const.tile([P, P], F32)
-        b_cols = y_psum.tile([P, P], F32, tag="y", name="b_cols")
-        bias = const.tile([P, CT], F32)
-        neg_b = const.tile([P, CT], F32)
-        nv_b = {}
-        nv = {(ti, ct): len(users(ti, "V", ct)) for ti in range(ntile) for ct in range(CT)}
-
-        def turn_bias():
-            nc.vector.tensor_copy(out=b_rows_f[:], in_=b_rows[:])
-            nc.tensor.transpose(b_cols[:], b_rows_f[:], ident[:])
-
-        def save_bias():
-            nc.vector.tensor_copy(out=bias[:], in_=b_cols[:, 0:CT])
-            nc.vector.tensor_scalar(out=neg_b[:], in0=b_cols[:, 0:CT], scalar1=-1.0, scalar2=None, op0=ALU.mult)
-            for n in sorted(set(nv.values()) - {0}):
-                nv_b[n] = const.tile([P, CT], F32, name="nv_b%d" % n)
-                nc.vector.tensor_scalar(out=nv_b[n][:], in0=b_cols[:, 0:CT], scalar1=float(n), scalar2=None, op0=ALU.mult)
 
         h2e = {}
         h4 = {}
@@ -225,7 +255,10 @@ def tile_cin_pb_t_kernel(tc, h2, x0, W3_words, W3_scales, b3, out):
         def fourfold_first(g):
             nc.vector.tensor_copy(
                 out=h4[0][:, :, 4 * FL * g : 4 * FL * (g + 1)].rearrange("p i (f q) -> p i f q", q=4),
-                in_=h2_slots(0, 0, DC, FL * g, FL).unsqueeze(3).to_broadcast([P, DC, FL, 4]),
+                in_=h2_sb[0][:, SHIFT + FL * D * g : SHIFT + FL * D * (g + 1)]
+                .rearrange("p (f d) -> p d f", d=D)[:, 0:DC]
+                .unsqueeze(3)
+                .to_broadcast([P, DC, FL, 4]),
             )
 
         new_h4(0)
@@ -245,14 +278,9 @@ def tile_cin_pb_t_kernel(tc, h2, x0, W3_words, W3_scales, b3, out):
             )
 
         save_first(0, nc.scalar.copy)
-        save_first(1, nc.vector.tensor_copy)
+        save_first(1, nc.scalar.copy if XF else nc.vector.tensor_copy)
         fourfold_first(1)
 
-        fold = const.tile([P, P], F32, name="fold")
-
-        def fill_fold():
-            nc.vector.memset(fold[:].bitcast(I32), 0)
-            nc.vector.tensor_tensor(out=fold[:, 0 : P // 2], in0=ident[:, 0 : P // 2], in1=ident[:, P // 2 : P], op=ALU.add)
 
         h_t = {}
         z = {}
@@ -267,7 +295,7 @@ def tile_cin_pb_t_kernel(tc, h2, x0, W3_words, W3_scales, b3, out):
         folded = {}
 
         def new_h2e(c):
-            h2e[c] = work.tile([P, DC - S_SLOTS, 2 * H2], BF16, name="h2e", bufs=E_AHEAD - H_AHEAD + 2)
+            h2e[c] = work.tile([P, g_slots(c), 2 * H2], BF16, name="h2e%d" % g_slots(c), bufs=H2E_BUFS)
 
         def double_values(c, i0, n):
             nc.gpsimd.tensor_scalar(
@@ -285,6 +313,13 @@ def tile_cin_pb_t_kernel(tc, h2, x0, W3_words, W3_scales, b3, out):
                 in_=h2e[c][:, i, :].bitcast(F32).unsqueeze(2).to_broadcast([P, H2, 2]),
             )
 
+        def fourfold_vector(c, i):
+            n = DC - i
+            nc.vector.tensor_copy(
+                out=h4[c][:, i:DC, :].rearrange("p i (f q) -> p i f q", q=4),
+                in_=h2_slots(c, i, n, 0, H2).unsqueeze(3).to_broadcast([P, n, H2, 4]),
+            )
+
         def fourfold_scalar(c, i):
             nc.scalar.copy(
                 out=h4[c][:, i, :].rearrange("p (f q) -> p f q", q=4),
@@ -299,7 +334,7 @@ def tile_cin_pb_t_kernel(tc, h2, x0, W3_words, W3_scales, b3, out):
         def multiply(c, g):
             ti, k = CHUNKS[c]
             if g == 0:
-                z[c] = work.tile([P, G, NCOL, 4], BF16, name="z", bufs=3, align_bytes=64)
+                z[c] = work.tile([P, G, NCOL, 4], BF16, name="z", bufs=Z_BUFS, align_bytes=64)
             first = DC * k % US
             nc.vector.tensor_tensor(
                 out=z[c][:, g].rearrange("p (i r) (tp e) -> p i r tp e", i=DC, tp=2),
@@ -424,9 +459,11 @@ def tile_cin_pb_t_kernel(tc, h2, x0, W3_words, W3_scales, b3, out):
 
         def st_dbl(s):
             if live(s + E_AHEAD) and s + E_AHEAD > 0:
-                new_h2e(s + E_AHEAD)
-                for i in range(0, DC - S_SLOTS, E_SLOTS):
-                    double_values(s + E_AHEAD, i, min(E_SLOTS, DC - S_SLOTS - i))
+                if g_slots(s + E_AHEAD):
+                    new_h2e(s + E_AHEAD)
+                c = s + E_AHEAD
+                for i in range(0, g_slots(c), E_SLOTS):
+                    double_values(c, i, min(E_SLOTS, g_slots(c) - i))
 
         def st_mx(s, cts):
             if live(s):
@@ -445,10 +482,11 @@ def tile_cin_pb_t_kernel(tc, h2, x0, W3_words, W3_scales, b3, out):
             if live(s + H_AHEAD) and s + H_AHEAD > 0:
                 if part == 0:
                     new_h4(s + H_AHEAD)
-                for i in ((0, 1, 2, 3) if S_SPLIT == 0 and part == 0 else () if S_SPLIT == 0 else (0, 1) if part == 0 else (2, 3)):
-                    if i < DC - S_SLOTS:
+                order = (2, 3, 0, 1) if S_FIRST else (0, 1, 2, 3)
+                for i in (order if S_SPLIT == 0 and part == 0 else () if S_SPLIT == 0 else order[0:2] if part == 0 else order[2:4]):
+                    if i < g_slots(s + H_AHEAD):
                         double_words(s + H_AHEAD, i)
-                    else:
+                    elif i < DC - V_SLOTS:
                         fourfold_scalar(s + H_AHEAD, i)
 
         def st_acc(s, cts):
@@ -470,17 +508,20 @@ def tile_cin_pb_t_kernel(tc, h2, x0, W3_words, W3_scales, b3, out):
                 turn_h2(s + T_AHEAD, g)
 
         for s in range(-E_AHEAD, NCHUNK + 1 + G_FLUSH):
-            if s == -1:
-                quantise(0)
+            if s == X2_STEP:
+                for ti in range(1, ntile):
+                    interleave_x0(ti)
+            if s == -2:
                 turn_bias()
+            if s == -Q_AHEAD:
+                quantise(0)
                 save_bias()
+            if s == -1:
                 st_mx(0, (0, 1))
             if live(s + M_AHEAD):
                 multiply(s + M_AHEAD, 0)
-            if s == -1:
+            if s == -Q_AHEAD:
                 late_loads()
-            if s == 2:
-                fill_fold()
             if G_ORDER == 0:
                 st_adds(s)
                 st_dbl(s)
@@ -489,6 +530,17 @@ def tile_cin_pb_t_kernel(tc, h2, x0, W3_words, W3_scales, b3, out):
                 st_adds(s)
             if S_POS == 0:
                 st_words(s, 0)
+            if PE_ORDER:
+                if PE_ORDER == 1:
+                    st_turn(s, 0)
+                    st_turn(s, 1)
+                st_acc(s, (0, 1, 2, 3))
+                st_flush(s)
+                if PE_ORDER == 2:
+                    st_turn(s, 0)
+                    st_turn(s, 1)
+            if LAST and s == NCHUNK - 1:
+                st_acc(s, (0, 1, 2, 3))
             if s > 0:
                 st_mx(s, (0, 1))
             if V_POS == 0:
@@ -502,13 +554,24 @@ def tile_cin_pb_t_kernel(tc, h2, x0, W3_words, W3_scales, b3, out):
             for ti in range(ntile):
                 if s == finish_step(ti) + 1 and TILES[ti][1] < P:
                     fold_sums(ti)
-            st_acc(s, (0, 1, 2, 3) if RUNS == 1 else (0, 1))
-            if RUNS == 1:
+            if PE_ORDER == 0 and not (LAST and s == NCHUNK - 1):
+                st_acc(s, (0, 1, 2, 3) if RUNS == 1 else (0, 1))
+            if PE_ORDER:
+                if live(s + M_AHEAD):
+                    multiply(s + M_AHEAD, 1)
+                if V_SLOTS and live(s + H_AHEAD) and s + H_AHEAD > 0:
+                    fourfold_vector(s + H_AHEAD, DC - V_SLOTS)
+                if V_POS == 2:
+                    st_vrelu(s)
+                st_mx(s, (2, 3))
+            elif RUNS == 1:
                 st_flush(s)
                 st_turn(s, 0)
                 st_turn(s, 1)
                 if live(s + M_AHEAD):
                     multiply(s + M_AHEAD, 1)
+                if V_SLOTS and live(s + H_AHEAD) and s + H_AHEAD > 0:
+                    fourfold_vector(s + H_AHEAD, DC - V_SLOTS)
                 if V_POS == 2:
                     st_vrelu(s)
                 st_mx(s, (2, 3))
@@ -516,6 +579,8 @@ def tile_cin_pb_t_kernel(tc, h2, x0, W3_words, W3_scales, b3, out):
                 st_turn(s, 0)
                 if live(s + M_AHEAD):
                     multiply(s + M_AHEAD, 1)
+                if V_SLOTS and live(s + H_AHEAD) and s + H_AHEAD > 0:
+                    fourfold_vector(s + H_AHEAD, DC - V_SLOTS)
                 if V_POS == 2:
                     st_vrelu(s)
                 st_mx(s, (2, 3))

@@ -40,6 +40,9 @@ V_SLOTS = 0
 XF = 1
 LAST = 0
 Z_BUFS = 3
+MERGE = 1
+WARM = 6
+SPLIT_END = 0
 S_FIRST = 1
 X2_STEP = -2
 H2E_BUFS = 3
@@ -47,8 +50,8 @@ H2_EARLY = 0
 E_SLOTS = 2
 ADD_SPLIT = 1
 T_BUFS = 3
-Y_BUFS = 3
-A_BUFS = 2
+Y_BUFS = 4
+A_BUFS = 1
 RUNS = 1
 PE_ORDER = 0
 G_ORDER = 1
@@ -134,6 +137,12 @@ def tile_cin_pb_t_kernel(tc, h2, x0, W3_words, W3_scales, b3, out):
                 nc.sync.dma_start(out=h2_sb[ti][0:nb, SHIFT : SHIFT + H2 * D], in_=rows)
                 nc.sync.dma_start(out=h2_sb[ti][nb:P, 0 : H2 * D], in_=rows)
 
+        if WARM:
+            idle = const.tile([P, NCOL], BF16, name="idle")
+            nc.vector.memset(idle[:].bitcast(I32), 0)
+            idle_y = y_psum.tile([P, NCOL], F32, tag="y", name="idle_y")
+            for i in range(WARM):
+                nc.tensor.matmul(out=idle_y[:], lhsT=idle[:, 0:P], rhs=idle[:], start=True, stop=True)
         w_words = const.tile([P, G, 2 * L3], U8, align_bytes=64)
         w_scales = const.tile([P, G, L3], U8, align_bytes=64)
         nc.vector.memset(w_scales[:].bitcast(I32), 0)
@@ -320,6 +329,18 @@ def tile_cin_pb_t_kernel(tc, h2, x0, W3_words, W3_scales, b3, out):
                 in_=h2_slots(c, i, n, 0, H2).unsqueeze(3).to_broadcast([P, n, H2, 4]),
             )
 
+        def double_words_pair(c, i0, i1):
+            nc.scalar.copy(
+                out=h4[c][:, i0:i1, :].bitcast(F32).rearrange("p i (f r) -> p (i f) r", r=2),
+                in_=h2e[c][:, i0:i1, :].bitcast(F32).rearrange("p i f -> p (i f)").unsqueeze(2).to_broadcast([P, (i1 - i0) * H2, 2]),
+            )
+
+        def fourfold_pair(c, i0, i1):
+            nc.scalar.copy(
+                out=h4[c][:, i0:i1, :].rearrange("p i (f q) -> p i f q", q=4),
+                in_=h2_slots(c, i0, i1 - i0, 0, H2).unsqueeze(3).to_broadcast([P, i1 - i0, H2, 4]),
+            )
+
         def fourfold_scalar(c, i):
             nc.scalar.copy(
                 out=h4[c][:, i, :].rearrange("p (f q) -> p f q", q=4),
@@ -437,8 +458,15 @@ def tile_cin_pb_t_kernel(tc, h2, x0, W3_words, W3_scales, b3, out):
 
         def save_sums(ti):
             acc_sb[ti] = work.tile([P, L3], F32, name="acc_sb", bufs=2)
-            nc.scalar.copy(out=acc_sb[ti][:], in_=acc[ti][:].rearrange("p ct c -> p (ct c)"))
             b0, nb = TILES[ti]
+            if ti == ntile - 1 and SPLIT_END:
+                half = L3 // 2
+                nc.scalar.copy(out=acc_sb[ti][:, 0:half], in_=acc[ti][:, 0 : CT // 2].rearrange("p ct c -> p (ct c)"))
+                nc.vector.tensor_copy(out=acc_sb[ti][:, half:L3], in_=acc[ti][:, CT // 2 : CT].rearrange("p ct c -> p (ct c)"))
+                nc.sync.dma_start(out=out[b0 : b0 + nb, 0:half], in_=acc_sb[ti][:, 0:half])
+                nc.scalar.dma_start(out=out[b0 : b0 + nb, half:L3], in_=acc_sb[ti][:, half:L3])
+                return
+            nc.scalar.copy(out=acc_sb[ti][:], in_=acc[ti][:].rearrange("p ct c -> p (ct c)"))
             if nb == P:
                 nc.sync.dma_start(out=out[b0 : b0 + nb, :], in_=acc_sb[ti][:])
 
@@ -483,17 +511,30 @@ def tile_cin_pb_t_kernel(tc, h2, x0, W3_words, W3_scales, b3, out):
                 if part == 0:
                     new_h4(s + H_AHEAD)
                 order = (2, 3, 0, 1) if S_FIRST else (0, 1, 2, 3)
-                for i in (order if S_SPLIT == 0 and part == 0 else () if S_SPLIT == 0 else order[0:2] if part == 0 else order[2:4]):
+                if MERGE:
+                    c = s + H_AHEAD
+                    if part == 0 and g_slots(c) < DC:
+                        fourfold_pair(c, g_slots(c), DC)
+                    if part == 1 - (S_SPLIT == 0) and g_slots(c) > 0:
+                        double_words_pair(c, 0, g_slots(c))
+                    continue_ = False
+                else:
+                    continue_ = True
+                for i in () if not continue_ else (order if S_SPLIT == 0 and part == 0 else () if S_SPLIT == 0 else order[0:2] if part == 0 else order[2:4]):
                     if i < g_slots(s + H_AHEAD):
                         double_words(s + H_AHEAD, i)
                     elif i < DC - V_SLOTS:
                         fourfold_scalar(s + H_AHEAD, i)
 
+        def opens_bank(c):
+            return A_BUFS == 1 and 0 < c < NCHUNK and CHUNKS[c][1] == 0
+
         def st_acc(s, cts):
-            if live(s - 1):
-                for ct in cts:
-                    if owner(s - 1, ct) == "T":
-                        add_up(CHUNKS[s - 1][0], ct, y_relu[s - 1, ct])
+            for c in (s - 2, s - 1):
+                if live(c) and (opens_bank(c) if c == s - 2 else not opens_bank(c)):
+                    for ct in cts:
+                        if owner(c, ct) == "T":
+                            add_up(CHUNKS[c][0], ct, y_relu[c, ct])
 
         def st_flush(s):
             for ti in range(ntile):

@@ -32,16 +32,24 @@ T_AHEAD = 3
 M_AHEAD = 2
 Q_AHEAD = 1
 
-OWNERS = (("G", "T", "T", "V"),)
+OWN_NEW = ("G", "G", "T", "V")
+OWN_OLD = ("G", "T", "T", "V")
+OLD_MOD = 4
+OLD_AT = (3,)
 G_LAST = 1
 G_FLUSH = 2
 S_SLOTS = (2,)
 V_SLOTS = 0
 XF = 1
-LAST = 0
+LAST = 1
+V_FLUSH = 2
 Z_BUFS = 3
 MERGE = 1
-WARM = 6
+S_NEW = 2
+WARM = 2
+WARM2 = 0
+EARLY_WORDS = 1
+FOLD_G = 0
 SPLIT_END = 0
 S_FIRST = 1
 X2_STEP = -2
@@ -56,6 +64,7 @@ RUNS = 1
 PE_ORDER = 0
 G_ORDER = 1
 V_POS = 0
+V_LAG = 1
 S_POS = 0
 S_SPLIT = 1
 
@@ -88,19 +97,22 @@ def tile_cin_pb_t_kernel(tc, h2, x0, W3_words, W3_scales, b3, out):
                 row += park_rows[ti]
 
         def g_slots(c):
-            return DC - V_SLOTS - S_SLOTS[c % len(S_SLOTS)]
+            return 0 if by_matmul(c) else DC - V_SLOTS - S_SLOTS[c % len(S_SLOTS)]
+
+        def by_matmul(c):
+            return c % OLD_MOD not in OLD_AT
 
         def owner(c, ct):
-            who = OWNERS[CHUNKS[c][1] % len(OWNERS)][ct]
+            who = (OWN_NEW if by_matmul(c) else OWN_OLD)[ct]
             if who == "G" and c >= NCHUNK - G_LAST:
-                return "T" if c % 2 else "V"
+                return "T"
             return who
 
         def users(ti, who, ct):
             return [c for c in range(NCHUNK) if CHUNKS[c][0] == ti and owner(c, ct) == who]
 
         def flush_step(ti, who, ct):
-            return users(ti, who, ct)[-1] + ((2 if PE_ORDER else 1) if who == "V" else G_FLUSH)
+            return users(ti, who, ct)[-1] + ((1 if ti == len(TILES) - 1 else V_FLUSH) if who == "V" else G_FLUSH)
 
         SUMS = {ti: [(who, ct) for who in "VG" for ct in range(CT) if users(ti, who, ct)] for ti in range(ntile)}
 
@@ -151,6 +163,15 @@ def tile_cin_pb_t_kernel(tc, h2, x0, W3_words, W3_scales, b3, out):
         ident = const.tile([P, P], F32)
         make_identity(nc, ident[:])
 
+        twice = const.tile([P, 2 * P], BF16, name="twice")
+        nc.gpsimd.tensor_scalar(
+            out=twice[:].rearrange("p (m e) -> p m e", e=2),
+            in0=ident[:].unsqueeze(2).to_broadcast([P, P, 2]),
+            scalar1=1.0,
+            scalar2=0.0,
+            op0=ALU.mult,
+            op1=ALU.add,
+        )
         x2 = const.tile([P, ntile, 2, D, 4], BF16, name="x2")
 
         def interleave_x0(ti):
@@ -251,6 +272,10 @@ def tile_cin_pb_t_kernel(tc, h2, x0, W3_words, W3_scales, b3, out):
 
         h2e = {}
         h4 = {}
+        batch = {}
+        gsum = {}
+        GCTS = [ct for ct in range(CT) if OWN_NEW[ct] == "G"]
+        NG = len(GCTS)
 
         def h2_slots(c, i0, n, f0, nf):
             ti, k = CHUNKS[c]
@@ -261,17 +286,28 @@ def tile_cin_pb_t_kernel(tc, h2, x0, W3_words, W3_scales, b3, out):
         def new_h4(c):
             h4[c] = work.tile([P, DC, 4 * H2], BF16, name="h4", bufs=H_AHEAD - T_AHEAD + 2)
 
-        def fourfold_first(g):
+        def twofold_first(g):
             nc.vector.tensor_copy(
-                out=h4[0][:, :, 4 * FL * g : 4 * FL * (g + 1)].rearrange("p i (f q) -> p i f q", q=4),
+                out=h2r[0][:, :, P * g : P * (g + 1)].rearrange("p i (f r) -> p i f r", r=2),
                 in_=h2_sb[0][:, SHIFT + FL * D * g : SHIFT + FL * D * (g + 1)]
                 .rearrange("p (f d) -> p d f", d=D)[:, 0:DC]
                 .unsqueeze(3)
-                .to_broadcast([P, DC, FL, 4]),
+                .to_broadcast([P, DC, FL, 2]),
             )
 
-        new_h4(0)
-        fourfold_first(0)
+        h2r = {}
+
+        def new_h2r(c):
+            h2r[c] = work.tile([P, DC, 2 * H2], BF16, name="h2r", bufs=H_AHEAD - T_AHEAD + 2)
+
+        def twofold(c, i0, i1):
+            nc.scalar.copy(
+                out=h2r[c][:, i0:i1, :].rearrange("p i (f r) -> p i f r", r=2),
+                in_=h2_slots(c, i0, i1 - i0, 0, H2).unsqueeze(3).to_broadcast([P, i1 - i0, H2, 2]),
+            )
+
+        new_h2r(0)
+        twofold_first(0)
         x_first = const.tile([P, DC, P, 4], BF16, name="x_first")
         x_cols = []
         for h in range(2):
@@ -288,7 +324,7 @@ def tile_cin_pb_t_kernel(tc, h2, x0, W3_words, W3_scales, b3, out):
 
         save_first(0, nc.scalar.copy)
         save_first(1, nc.scalar.copy if XF else nc.vector.tensor_copy)
-        fourfold_first(1)
+        twofold_first(1)
 
 
         h_t = {}
@@ -348,6 +384,13 @@ def tile_cin_pb_t_kernel(tc, h2, x0, W3_words, W3_scales, b3, out):
             )
 
         def turn_h2(c, g):
+            if by_matmul(c):
+                h_t[c, g] = t_psum.tile([P, DC, 2 * P], BF16, name="h_t")
+                for i in range(DC):
+                    nc.tensor.matmul(
+                        out=h_t[c, g][:, i, :], lhsT=h2r[c][:, i, P * g : P * (g + 1)], rhs=twice[:], start=True, stop=True
+                    )
+                return
             h_t[c, g] = t_psum.tile([P, DC, P], F32, name="h_t")
             for i in range(DC):
                 nc.tensor.transpose(h_t[c, g][:, i, :], h4[c][:, i, 2 * H2 * g : 2 * H2 * (g + 1)].bitcast(F32), ident[:])
@@ -359,9 +402,7 @@ def tile_cin_pb_t_kernel(tc, h2, x0, W3_words, W3_scales, b3, out):
             first = DC * k % US
             nc.vector.tensor_tensor(
                 out=z[c][:, g].rearrange("p (i r) (tp e) -> p i r tp e", i=DC, tp=2),
-                in0=h_t[c, g][:]
-                .rearrange("p i r -> p (i r)")
-                .bitcast(BF16)
+                in0=(h_t[c, g][:].rearrange("p i r -> p (i r)") if by_matmul(c) else h_t[c, g][:].rearrange("p i r -> p (i r)").bitcast(BF16))
                 .rearrange("p (i r e) -> p i r e", i=DC, e=2)
                 .unsqueeze(3)
                 .to_broadcast([P, DC, P, 2, 2]),
@@ -419,24 +460,29 @@ def tile_cin_pb_t_kernel(tc, h2, x0, W3_words, W3_scales, b3, out):
 
         def relu_scalar(c, ct):
             ti = CHUNKS[c][0]
-            if owner(c, ct) == "G" and c == users(ti, "G", ct)[0]:
-                sums[ti, "G", ct] = work.tile([P, NCOL], F32, name="sum_g%d" % ct, bufs=2)
-                y_relu[c, ct] = sums[ti, "G", ct]
-            elif owner(c, ct) == "G":
-                y_relu[c, ct] = work.tile([P, NCOL], F32, name="y_relu_g", bufs=6)
+            if owner(c, ct) == "G":
+                if c not in batch:
+                    first_c = CHUNKS[c][1] == 0
+                    if first_c:
+                        sum_g = work.tile([P, NG, NCOL], F32, name="sum_g", bufs=2)
+                        batch[c] = sum_g
+                        for lane in range(NG):
+                            sums[ti, "G", GCTS[lane]] = batch[c][:, lane, :]
+                        gsum[ti] = batch[c]
+                    else:
+                        y_relu_g = work.tile([P, NG, NCOL], F32, name="y_relu_g", bufs=4)
+                        batch[c] = y_relu_g
+                y_relu[c, ct] = batch[c][:, GCTS.index(ct), :]
             else:
                 y_relu[c, ct] = work.tile([P, NCOL], F32, name="y_relu", bufs=8)
-            nc.scalar.activation(out=y_relu[c, ct][:], in_=y[c, ct][:], func=RELU, bias=bias[:, ct : ct + 1], scale=1.0)
+            nc.scalar.activation(out=y_relu[c, ct] if owner(c, ct) == "G" else y_relu[c, ct][:], in_=y[c, ct][:], func=RELU, bias=bias[:, ct : ct + 1], scale=1.0)
 
         def add_gpsimd(c):
             ti = CHUNKS[c][0]
-            for ct in range(CT):
-                if owner(c, ct) == "G" and c != users(ti, "G", ct)[0]:
-                    for a in range(ADD_SPLIT):
-                        cols = slice(NCOL * a // ADD_SPLIT, NCOL * (a + 1) // ADD_SPLIT)
-                        nc.gpsimd.tensor_tensor(
-                            out=sums[ti, "G", ct][:, cols], in0=sums[ti, "G", ct][:, cols], in1=y_relu[c, ct][:, cols], op=ALU.add
-                        )
+            n = len([ct for ct in range(CT) if owner(c, ct) == "G"])
+            if n and CHUNKS[c][1] > 0:
+                dst = gsum[ti][:, 0:n, :].rearrange("p l n -> p (l n)")
+                nc.gpsimd.tensor_tensor(out=dst, in0=dst, in1=batch[c][:, 0:n, :].rearrange("p l n -> p (l n)"), op=ALU.add)
 
         def n_adds(ti):
             return DC * (sum([len(users(ti, "T", ct)) for ct in range(CT)]) + len(SUMS[ti]))
@@ -470,7 +516,25 @@ def tile_cin_pb_t_kernel(tc, h2, x0, W3_words, W3_scales, b3, out):
             if nb == P:
                 nc.sync.dma_start(out=out[b0 : b0 + nb, :], in_=acc_sb[ti][:])
 
+        def fold_gpsimd(ti):
+            b0, nb = TILES[ti]
+            nc.sync.dma_start(out=out[b0 : b0 + nb, :], in_=acc_sb[ti][nb:P, :])
+            upper = work.tile([P, L3], F32, name="upper", bufs=1)
+            nc.sync.dma_start(out=upper[0:nb, :], in_=out[b0 : b0 + nb, :])
+            upper_of[ti] = upper
+
+        def fold_add(ti):
+            b0, nb = TILES[ti]
+            out_sb = work.tile([P, L3], F32, name="out_sb", bufs=1)
+            nc.gpsimd.tensor_tensor(out=out_sb[0:nb, :], in0=acc_sb[ti][0:nb, :], in1=upper_of[ti][0:nb, :], op=ALU.add)
+            nc.sync.dma_start(out=out[b0 : b0 + nb, :], in_=out_sb[0:nb, :])
+
+        upper_of = {}
+
         def fold_sums(ti):
+            if FOLD_G:
+                fold_gpsimd(ti)
+                return
             folded[ti] = y_psum.tile([P, L3], F32, name="folded", tag="y")
             nc.tensor.matmul(out=folded[ti][:], lhsT=fold[:], rhs=acc_sb[ti][:], start=True, stop=True)
             b0, nb = TILES[ti]
@@ -501,13 +565,23 @@ def tile_cin_pb_t_kernel(tc, h2, x0, W3_words, W3_scales, b3, out):
                         relu_scalar(s, ct)
 
         def st_vrelu(s):
-            if live(s - 1):
+            c = s - V_LAG
+            if live(c):
                 for ct in range(CT):
-                    if owner(s - 1, ct) == "V":
-                        relu_add_vector(s - 1, ct)
+                    if owner(c, ct) == "V":
+                        relu_add_vector(c, ct)
 
         def st_words(s, part):
             if live(s + H_AHEAD) and s + H_AHEAD > 0:
+                if by_matmul(s + H_AHEAD):
+                    if part == 0:
+                        new_h2r(s + H_AHEAD)
+                    if S_NEW == 1:
+                        if part == 0:
+                            twofold(s + H_AHEAD, 0, DC)
+                    else:
+                        twofold(s + H_AHEAD, 2 * part, 2 * part + 2)
+                    return
                 if part == 0:
                     new_h4(s + H_AHEAD)
                 order = (2, 3, 0, 1) if S_FIRST else (0, 1, 2, 3)
@@ -557,19 +631,29 @@ def tile_cin_pb_t_kernel(tc, h2, x0, W3_words, W3_scales, b3, out):
             if s == -Q_AHEAD:
                 quantise(0)
                 save_bias()
+            if s < 0 and EARLY_WORDS:
+                st_words(s, 0)
+                st_words(s, 1)
             if s == -1:
+                if WARM2:
+                    idle_y2 = y_psum.tile([P, NCOL], F32, tag="y", name="idle_y2")
+                    for i in range(WARM2):
+                        nc.tensor.matmul(out=idle_y2[:], lhsT=idle[:, 0:P], rhs=idle[:], start=True, stop=True)
                 st_mx(0, (0, 1))
             if live(s + M_AHEAD):
                 multiply(s + M_AHEAD, 0)
             if s == -Q_AHEAD:
                 late_loads()
+            for ti in range(ntile):
+                if FOLD_G and s == finish_step(ti) + 4 and TILES[ti][1] < P:
+                    fold_add(ti)
             if G_ORDER == 0:
                 st_adds(s)
                 st_dbl(s)
             else:
                 st_dbl(s)
                 st_adds(s)
-            if S_POS == 0:
+            if S_POS == 0 and not (s < 0 and EARLY_WORDS):
                 st_words(s, 0)
             if PE_ORDER:
                 if PE_ORDER == 1:
@@ -628,6 +712,7 @@ def tile_cin_pb_t_kernel(tc, h2, x0, W3_words, W3_scales, b3, out):
                 st_acc(s, (2, 3))
                 st_flush(s)
                 st_turn(s, 1)
-            st_words(s, 1)
+            if not (s < 0 and EARLY_WORDS):
+                st_words(s, 1)
             if S_POS == 2:
                 st_words(s, 0)

@@ -32,8 +32,7 @@ T_AHEAD = 3
 M_AHEAD = 2
 Q_AHEAD = 1
 
-OWN_NEW = ("G", "G", "T", "V")
-OWN_OLD = ("G", "T", "T", "V")
+OWN8 = (("G", "G", "T", "V"), ("G", "G", "T", "V"), ("G", "G", "T", "V"), ("G", "T", "T", "V"), ("G", "G", "T", "V"), ("G", "G", "T", "V"), ("G", "G", "T", "V"), ("G", "T", "T", "V"))
 OLD_MOD = 4
 OLD_AT = (3,)
 G_LAST = 1
@@ -46,10 +45,11 @@ V_FLUSH = 2
 Z_BUFS = 3
 MERGE = 1
 S_NEW = 2
-WARM = 2
+WARM = 3
 WARM2 = 0
 EARLY_WORDS = 1
-FOLD_G = 0
+FOLD_G = 1
+FOLD_AT = 20
 SPLIT_END = 0
 S_FIRST = 1
 X2_STEP = -2
@@ -103,7 +103,7 @@ def tile_cin_pb_t_kernel(tc, h2, x0, W3_words, W3_scales, b3, out):
             return c % OLD_MOD not in OLD_AT
 
         def owner(c, ct):
-            who = (OWN_NEW if by_matmul(c) else OWN_OLD)[ct]
+            who = OWN8[c % 8][ct]
             if who == "G" and c >= NCHUNK - G_LAST:
                 return "T"
             return who
@@ -274,7 +274,7 @@ def tile_cin_pb_t_kernel(tc, h2, x0, W3_words, W3_scales, b3, out):
         h4 = {}
         batch = {}
         gsum = {}
-        GCTS = [ct for ct in range(CT) if OWN_NEW[ct] == "G"]
+        GCTS = [ct for ct in range(CT) if any([o[ct] == "G" for o in OWN8])]
         NG = len(GCTS)
 
         def h2_slots(c, i0, n, f0, nf):
@@ -645,7 +645,7 @@ def tile_cin_pb_t_kernel(tc, h2, x0, W3_words, W3_scales, b3, out):
             if s == -Q_AHEAD:
                 late_loads()
             for ti in range(ntile):
-                if FOLD_G and s == finish_step(ti) + 4 and TILES[ti][1] < P:
+                if FOLD_G and s == (FOLD_AT if FOLD_AT else finish_step(ti) + 4) and TILES[ti][1] < P:
                     fold_add(ti)
             if G_ORDER == 0:
                 st_adds(s)

@@ -48,13 +48,13 @@ S_NEW = 2
 WARM = 3
 WARM2 = 0
 EARLY_WORDS = 1
+X1_LATE = 0
 FOLD_G = 1
 FOLD_AT = 20
 SPLIT_END = 0
 S_FIRST = 1
 X2_STEP = -2
 H2E_BUFS = 3
-H2_EARLY = 0
 E_SLOTS = 2
 ADD_SPLIT = 1
 T_BUFS = 3
@@ -83,18 +83,29 @@ def tile_cin_pb_t_kernel(tc, h2, x0, W3_words, W3_scales, b3, out):
 
         ntile = len(TILES)
         nchunk = [D * nb // NCOL for (b0, nb) in TILES]
-        nunit = [n * DC // US for n in nchunk]
         CHUNKS = [(ti, k) for ti in range(ntile) for k in range(nchunk[ti])]
         row0 = [b0 + nb - P for (b0, nb) in TILES]
         skip = [P - nb for (b0, nb) in TILES]
-        UROWS = P * US * 2 // L3
-        park_rows = [n * UROWS for n in nunit]
+        UNITS = [[(DC, DC)] if ti == 0 else [] for ti in range(ntile)]
+        for ti in range(ntile):
+            UNITS[ti].extend([(i0, US) for i0 in range(2 * DC if ti == 0 else 0, nchunk[ti] * DC, US)])
+
+        def unit_rows(n):
+            return P * n * 2 // L3
+
         park0 = {}
         row = PARK_ROW
         for ti in range(ntile):
             for jh in range(2):
-                park0[ti, jh] = row
-                row += park_rows[ti]
+                for u in range(len(UNITS[ti])):
+                    park0[ti, jh, u] = row
+                    row += unit_rows(UNITS[ti][u][1])
+
+        def unit_of(c):
+            ti, k = CHUNKS[c]
+            for u in range(len(UNITS[ti])):
+                if UNITS[ti][u][0] <= DC * k < UNITS[ti][u][0] + UNITS[ti][u][1]:
+                    return u, DC * k - UNITS[ti][u][0]
 
         def g_slots(c):
             return 0 if by_matmul(c) else DC - V_SLOTS - S_SLOTS[c % len(S_SLOTS)]
@@ -124,7 +135,7 @@ def tile_cin_pb_t_kernel(tc, h2, x0, W3_words, W3_scales, b3, out):
         def load_x0(ti):
             nc.sync.dma_start(out=x1[:, ti, :], in_=x0[row0[ti] : row0[ti] + P].rearrange("b j d -> b (j d)"))
 
-        for ti in range(ntile):
+        for ti in range(1 if X1_LATE else ntile):
             load_x0(ti)
         h2_sb = []
         for ti in range(ntile):
@@ -181,36 +192,37 @@ def tile_cin_pb_t_kernel(tc, h2, x0, W3_words, W3_scales, b3, out):
             else:
                 nc.gpsimd.tensor_scalar(out=x2[:, ti], in0=src, scalar1=1.0, scalar2=0.0, op0=ALU.mult, op1=ALU.add)
 
-        def park_x0(ti):
+        def park_x0(ti, u0, u1):
             nh = P // TILES[ti][1]
+            n = UNITS[ti][u0][1]
+            i0 = UNITS[ti][u0][0]
             for jh in range(2):
-                rows = out[park0[ti, jh] : park0[ti, jh] + park_rows[ti], :].rearrange("r c -> (r c)")
+                r = park0[ti, jh, u0]
+                rows = out[r : r + (u1 - u0) * unit_rows(n), :].rearrange("r c -> (r c)")
                 for dh in range(nh):
+                    d0 = D // nh * dh + i0
                     nc.sync.dma_start(
-                        out=rows.rearrange("(u dh b w) -> dh b u w", u=nunit[ti], dh=nh, w=2 * US)[dh],
-                        in_=x2[skip[ti] : P, ti, jh]
-                        .rearrange("p (dh u d8) t -> p dh u (d8 t)", dh=nh, u=nunit[ti])[:, dh]
+                        out=rows.rearrange("(u dh b w) -> dh b u w", u=u1 - u0, dh=nh, w=2 * n)[dh],
+                        in_=x2[skip[ti] : P, ti, jh, d0 : d0 + (u1 - u0) * n, :]
+                        .rearrange("p (u d) t -> p u (d t)", u=u1 - u0)
                         .bitcast(F32),
                     )
 
         xs = []
         for ti in range(ntile):
             xs_units = []
-            for u in range(nunit[ti]):
-                xs_tile = const.tile([P, P * US * 4], BF16, name="xs%d_%d" % (ti, u))
+            for u in range(len(UNITS[ti])):
+                xs_tile = const.tile([P, P * UNITS[ti][u][1] * 4], BF16, name="xs%d_%d" % (ti, u))
                 xs_units.append(xs_tile)
             xs.append(xs_units)
 
-        def spread_x0(ti):
-            spread_units(ti, 0, nunit[ti])
-
-        def spread_units(ti, u0, u1):
+        def spread_x0(ti, u0, u1):
             for u in range(u0, u1):
                 for jh in range(2):
-                    r = park0[ti, jh] + UROWS * u
+                    r = park0[ti, jh, u]
                     nc.sync.dma_start(
                         out=xs[ti][u][jh:P:2, :].bitcast(F32),
-                        in_=out[r : r + UROWS, :].rearrange("r c -> (r c)").partition_broadcast(P // 2),
+                        in_=out[r : r + unit_rows(UNITS[ti][u][1]), :].rearrange("r c -> (r c)").partition_broadcast(P // 2),
                     )
 
         b_rows_f = const.tile([P, P], F32)
@@ -234,7 +246,8 @@ def tile_cin_pb_t_kernel(tc, h2, x0, W3_words, W3_scales, b3, out):
         fold = const.tile([P, P], F32, name="fold")
 
         interleave_x0(0)
-        park_x0(0)
+        park_x0(0, 0, 1)
+        park_x0(0, 1, len(UNITS[0]))
         nc.sync.dma_start(out=b_rows[0:CT, :], in_=b3.rearrange("(r c) -> r c", c=P))
         nc.gpsimd.memset(fold[:], 0.0)
         nc.gpsimd.tensor_tensor(out=fold[:, 0 : P // 2], in0=ident[:, 0 : P // 2], in1=ident[:, P // 2 : P], op=ALU.add)
@@ -255,20 +268,19 @@ def tile_cin_pb_t_kernel(tc, h2, x0, W3_words, W3_scales, b3, out):
                 out=w_scales[32 * quad : 32 * quad + 4].bitcast(I32),
                 in_=W3_scales[:, 4 * quad : 4 * quad + 4, :].bitcast(I32).rearrange("g r n -> r g n"),
             )
-        if H2_EARLY:
-            spread_units(0, 0, H2_EARLY)
-            load_h2(1)
-            spread_units(0, H2_EARLY, nunit[0])
-        else:
-            spread_x0(0)
-            load_h2(1)
+        spread_x0(0, 0, 1)
+        if X1_LATE:
+            for ti in range(1, ntile):
+                load_x0(ti)
+        spread_x0(0, 1, len(UNITS[0]))
+        load_h2(1)
 
         def late_loads():
             for ti in range(1, ntile):
-                park_x0(ti)
-            spread_x0(1)
+                park_x0(ti, 0, len(UNITS[ti]))
+            spread_x0(1, 0, len(UNITS[1]))
             load_h2(2)
-            spread_x0(2)
+            spread_x0(2, 0, len(UNITS[2]))
 
         h2e = {}
         h4 = {}
@@ -385,10 +397,14 @@ def tile_cin_pb_t_kernel(tc, h2, x0, W3_words, W3_scales, b3, out):
 
         def turn_h2(c, g):
             if by_matmul(c):
-                h_t[c, g] = t_psum.tile([P, DC, 2 * P], BF16, name="h_t")
+                h_t[c, g] = t_psum.tile([P, P, DC, 2], BF16, name="h_t")
                 for i in range(DC):
                     nc.tensor.matmul(
-                        out=h_t[c, g][:, i, :], lhsT=h2r[c][:, i, P * g : P * (g + 1)], rhs=twice[:], start=True, stop=True
+                        out=h_t[c, g][:, :, i, :],
+                        lhsT=h2r[c][:, i, P * g : P * (g + 1)],
+                        rhs=twice[:].rearrange("p (m e) -> p m e", e=2),
+                        start=True,
+                        stop=True,
                     )
                 return
             h_t[c, g] = t_psum.tile([P, DC, P], F32, name="h_t")
@@ -399,17 +415,29 @@ def tile_cin_pb_t_kernel(tc, h2, x0, W3_words, W3_scales, b3, out):
             ti, k = CHUNKS[c]
             if g == 0:
                 z[c] = work.tile([P, G, NCOL, 4], BF16, name="z", bufs=Z_BUFS, align_bytes=64)
-            first = DC * k % US
+            u, first = unit_of(c) if c > 0 else (0, 0)
+            if by_matmul(c):
+                nc.vector.tensor_tensor(
+                    out=z[c][:, g].rearrange("p (r i) (tp e) -> p r i tp e", i=DC, tp=2),
+                    in0=h_t[c, g][:].unsqueeze(3).to_broadcast([P, P, DC, 2, 2]),
+                    in1=(
+                        x_first[:].rearrange("p i r (tp e) -> p r i tp e", tp=2)
+                        if c == 0
+                        else xs[ti][u][:].rearrange("p (r d tp e) -> p r d tp e", d=UNITS[ti][u][1], tp=2, e=2)[:, :, first : first + DC]
+                    ),
+                    op=ALU.mult,
+                )
+                return
             nc.vector.tensor_tensor(
                 out=z[c][:, g].rearrange("p (i r) (tp e) -> p i r tp e", i=DC, tp=2),
-                in0=(h_t[c, g][:].rearrange("p i r -> p (i r)") if by_matmul(c) else h_t[c, g][:].rearrange("p i r -> p (i r)").bitcast(BF16))
+                in0=h_t[c, g][:].rearrange("p i r -> p (i r)").bitcast(BF16)
                 .rearrange("p (i r e) -> p i r e", i=DC, e=2)
                 .unsqueeze(3)
                 .to_broadcast([P, DC, P, 2, 2]),
                 in1=(
                     x_first[:].rearrange("p i r (tp e) -> p i r tp e", tp=2)
                     if c == 0
-                    else xs[ti][DC * k // US][:].rearrange("p (r d8 tp e) -> p d8 r tp e", d8=US, tp=2, e=2)[:, first : first + DC]
+                    else xs[ti][u][:].rearrange("p (r d tp e) -> p d r tp e", d=UNITS[ti][u][1], tp=2, e=2)[:, first : first + DC]
                 ),
                 op=ALU.mult,
             )
@@ -436,13 +464,18 @@ def tile_cin_pb_t_kernel(tc, h2, x0, W3_words, W3_scales, b3, out):
                     stop=(g == G - 1),
                 )
 
+        def by_slot(c, columns):
+            if by_matmul(c):
+                return columns.rearrange("p (r i) -> p i r", i=DC)
+            return columns.rearrange("p (i r) -> p i r", i=DC)
+
         def relu_add_vector(c, ct):
             ti = CHUNKS[c][0]
             if c == users(ti, "V", ct)[0]:
                 sums[ti, "V", ct] = work.tile([P, NCOL], F32, name="sum_v%d" % ct, bufs=2)
                 nc.vector.tensor_scalar(
-                    out=sums[ti, "V", ct][:],
-                    in0=y[c, ct][:],
+                    out=sums[ti, "V", ct][:].rearrange("p (i r) -> p i r", i=DC),
+                    in0=by_slot(c, y[c, ct][:]),
                     scalar1=neg_b[:, ct : ct + 1],
                     scalar2=nv_b[nv[ti, ct]][:, ct : ct + 1],
                     op0=ALU.max,
@@ -450,10 +483,10 @@ def tile_cin_pb_t_kernel(tc, h2, x0, W3_words, W3_scales, b3, out):
                 )
             else:
                 nc.vector.scalar_tensor_tensor(
-                    out=sums[ti, "V", ct][:],
-                    in0=y[c, ct][:],
+                    out=sums[ti, "V", ct][:].rearrange("p (i r) -> p i r", i=DC),
+                    in0=by_slot(c, y[c, ct][:]),
                     scalar=neg_b[:, ct : ct + 1],
-                    in1=sums[ti, "V", ct][:],
+                    in1=sums[ti, "V", ct][:].rearrange("p (i r) -> p i r", i=DC),
                     op0=ALU.max,
                     op1=ALU.add,
                 )
@@ -475,7 +508,8 @@ def tile_cin_pb_t_kernel(tc, h2, x0, W3_words, W3_scales, b3, out):
                 y_relu[c, ct] = batch[c][:, GCTS.index(ct), :]
             else:
                 y_relu[c, ct] = work.tile([P, NCOL], F32, name="y_relu", bufs=8)
-            nc.scalar.activation(out=y_relu[c, ct] if owner(c, ct) == "G" else y_relu[c, ct][:], in_=y[c, ct][:], func=RELU, bias=bias[:, ct : ct + 1], scale=1.0)
+            columns = y_relu[c, ct] if owner(c, ct) == "G" else y_relu[c, ct][:]
+            nc.scalar.activation(out=columns.rearrange("p (i r) -> p i r", i=DC), in_=by_slot(c, y[c, ct][:]), func=RELU, bias=bias[:, ct : ct + 1], scale=1.0)
 
         def add_gpsimd(c):
             ti = CHUNKS[c][0]

from contextlib import ExitStack

import concourse.mybir as mybir
from concourse.masks import make_identity

BF16 = mybir.dt.bfloat16
F32 = mybir.dt.float32
I32 = mybir.dt.int32
U8 = mybir.dt.uint8
U32 = mybir.dt.uint32
FP8X4 = mybir.dt.float8_e4m3fn_x4
FP4X4 = mybir.dt.float4_e2m1fn_x4
ALU = mybir.AluOpType
RELU = mybir.ActivationFunctionType.Relu

B, H2, F, D, L3 = 320, 128, 8, 32, 512
P = 128
G = 2
FL = H2 // G
NCOL = 512
DC = NCOL // P
CT = L3 // P
US = 8
TILES = ((0, 128), (256, 64), (128, 128))
NCHUNK = B * D // NCOL
PARK_ROW = 128
SHIFT = D // 2

E_AHEAD = 5
H_AHEAD = 4
T_AHEAD = 3
M_AHEAD = 2
Q_AHEAD = 1

OWN8 = (("G", "G", "T", "V"), ("G", "G", "T", "V"), ("G", "G", "T", "V"), ("G", "T", "T", "V"), ("G", "G", "T", "V"), ("G", "G", "T", "V"), ("G", "G", "T", "V"), ("G", "T", "T", "V"))
OLD_MOD = 4
OLD_AT = (3,)
G_LAST = 1
G_FLUSH = 2
S_SLOTS = (2,)
V_SLOTS = 0
XF = 1
LAST = 1
V_FLUSH = 2
Z_BUFS = 3
MERGE = 1
S_NEW = 2
WARM = 3
WARM2 = 0
EARLY_WORDS = 1
X1_LATE = 0
FOLD_G = 1
FOLD_AT = 20
SPLIT_END = 0
S_FIRST = 1
X2_STEP = -2
H2E_BUFS = 3
E_SLOTS = 2
ADD_SPLIT = 1
T_BUFS = 3
Y_BUFS = 4
A_BUFS = 1
RUNS = 1
PE_ORDER = 0
G_ORDER = 1
V_POS = 0
V_LAG = 1
S_POS = 0
S_SPLIT = 1

FLOPS = 2 * B * D * H2 * F * L3


def tile_cin_pb_t_kernel(tc, h2, x0, W3_words, W3_scales, b3, out):
    nc = tc.nc
    with ExitStack() as ctx:
        const = ctx.enter_context(tc.tile_pool(name="const", bufs=1))
        work = ctx.enter_context(tc.tile_pool(name="work", bufs=3))
        t_psum = ctx.enter_context(tc.psum_pool(name="t_psum", bufs=T_BUFS))
        y_psum = ctx.enter_context(tc.psum_pool(name="y_psum", bufs=Y_BUFS))
        a_psum = ctx.enter_context(tc.psum_pool(name="a_psum", bufs=A_BUFS))
        ctx.enter_context(tc.manual_schedule())

        ntile = len(TILES)
        nchunk = [D * nb // NCOL for (b0, nb) in TILES]
        CHUNKS = [(ti, k) for ti in range(ntile) for k in range(nchunk[ti])]
        row0 = [b0 + nb - P for (b0, nb) in TILES]
        skip = [P - nb for (b0, nb) in TILES]
        UNITS = [[(DC, DC)] if ti == 0 else [] for ti in range(ntile)]
        for ti in range(ntile):
            UNITS[ti].extend([(i0, US) for i0 in range(2 * DC if ti == 0 else 0, nchunk[ti] * DC, US)])

        def unit_rows(n):
            return P * n * 2 // L3

        park0 = {}
        row = PARK_ROW
        for ti in range(ntile):
            for jh in range(2):
                for u in range(len(UNITS[ti])):
                    park0[ti, jh, u] = row
                    row += unit_rows(UNITS[ti][u][1])

        def unit_of(c):
            ti, k = CHUNKS[c]
            for u in range(len(UNITS[ti])):
                if UNITS[ti][u][0] <= DC * k < UNITS[ti][u][0] + UNITS[ti][u][1]:
                    return u, DC * k - UNITS[ti][u][0]

        def g_slots(c):
            return 0 if by_matmul(c) else DC - V_SLOTS - S_SLOTS[c % len(S_SLOTS)]

        def by_matmul(c):
            return c % OLD_MOD not in OLD_AT

        def owner(c, ct):
            who = OWN8[c % 8][ct]
            if who == "G" and c >= NCHUNK - G_LAST:
                return "T"
            return who

        def users(ti, who, ct):
            return [c for c in range(NCHUNK) if CHUNKS[c][0] == ti and owner(c, ct) == who]

        def flush_step(ti, who, ct):
            return users(ti, who, ct)[-1] + ((1 if ti == len(TILES) - 1 else V_FLUSH) if who == "V" else G_FLUSH)

        SUMS = {ti: [(who, ct) for who in "VG" for ct in range(CT) if users(ti, who, ct)] for ti in range(ntile)}

        def finish_step(ti):
            return max([CHUNKS.index((ti, nchunk[ti] - 1)) + 1] + [flush_step(ti, who, ct) for (who, ct) in SUMS[ti]])

        x1 = const.tile([P, ntile, F * D], BF16, name="x1")

        def load_x0(ti):
            nc.sync.dma_start(out=x1[:, ti, :], in_=x0[row0[ti] : row0[ti] + P].rearrange("b j d -> b (j d)"))

        for ti in range(1 if X1_LATE else ntile):
            load_x0(ti)
        h2_sb = []
        for ti in range(ntile):
            h2_tile = const.tile([P, H2 * D + SHIFT], BF16, name="h2_tile%d" % ti)
            h2_sb.append(h2_tile)
        for g in range(G):
            nc.scalar.dma_start(
                out=h2_sb[0][:, SHIFT + FL * D * g : SHIFT + FL * D * (g + 1)],
                in_=h2[0:P, FL * g : FL * (g + 1), :].rearrange("b f d -> b (f d)"),
            )

        warm = const.tile([P, 1], F32, name="warm")
        nc.vector.memset(warm[:], 0.0)
        nc.scalar.activation(out=warm[:], in_=warm[:], func=RELU)

        def load_h2(ti):
            b0, nb = TILES[ti]
            rows = h2[b0 : b0 + nb].rearrange("b f d -> b (f d)")
            if nb == P:
                nc.sync.dma_start(out=h2_sb[ti][:, SHIFT : SHIFT + H2 * D], in_=rows)
            else:
                nc.sync.dma_start(out=h2_sb[ti][0:nb, SHIFT : SHIFT + H2 * D], in_=rows)
                nc.sync.dma_start(out=h2_sb[ti][nb:P, 0 : H2 * D], in_=rows)

        if WARM:
            idle = const.tile([P, NCOL], BF16, name="idle")
            nc.vector.memset(idle[:].bitcast(I32), 0)
            idle_y = y_psum.tile([P, NCOL], F32, tag="y", name="idle_y")
            for i in range(WARM):
                nc.tensor.matmul(out=idle_y[:], lhsT=idle[:, 0:P], rhs=idle[:], start=True, stop=True)
        w_words = const.tile([P, G, 2 * L3], U8, align_bytes=64)
        w_scales = const.tile([P, G, L3], U8, align_bytes=64)
        nc.vector.memset(w_scales[:].bitcast(I32), 0)
        b_rows = const.tile([P, P], BF16)
        nc.vector.memset(b_rows[:].bitcast(I32), 0)
        ident = const.tile([P, P], F32)
        make_identity(nc, ident[:])

        twice = const.tile([P, 2 * P], BF16, name="twice")
        nc.gpsimd.tensor_scalar(
            out=twice[:].rearrange("p (m e) -> p m e", e=2),
            in0=ident[:].unsqueeze(2).to_broadcast([P, P, 2]),
            scalar1=1.0,
            scalar2=0.0,
            op0=ALU.mult,
            op1=ALU.add,
        )
        x2 = const.tile([P, ntile, 2, D, 4], BF16, name="x2")

        def interleave_x0(ti):
            src = x1[:, ti, :].rearrange("p (jh t d) -> p jh d t", jh=2, t=4)
            if ti == 0:
                nc.vector.tensor_copy(out=x2[:, ti], in_=src)
            else:
                nc.gpsimd.tensor_scalar(out=x2[:, ti], in0=src, scalar1=1.0, scalar2=0.0, op0=ALU.mult, op1=ALU.add)

        def park_x0(ti, u0, u1):
            nh = P // TILES[ti][1]
            n = UNITS[ti][u0][1]
            i0 = UNITS[ti][u0][0]
            for jh in range(2):
                r = park0[ti, jh, u0]
                rows = out[r : r + (u1 - u0) * unit_rows(n), :].rearrange("r c -> (r c)")
                for dh in range(nh):
                    d0 = D // nh * dh + i0
                    nc.sync.dma_start(
                        out=rows.rearrange("(u dh b w) -> dh b u w", u=u1 - u0, dh=nh, w=2 * n)[dh],
                        in_=x2[skip[ti] : P, ti, jh, d0 : d0 + (u1 - u0) * n, :]
                        .rearrange("p (u d) t -> p u (d t)", u=u1 - u0)
                        .bitcast(F32),
                    )

        xs = []
        for ti in range(ntile):
            xs_units = []
            for u in range(len(UNITS[ti])):
                xs_tile = const.tile([P, P * UNITS[ti][u][1] * 4], BF16, name="xs%d_%d" % (ti, u))
                xs_units.append(xs_tile)
            xs.append(xs_units)

        def spread_x0(ti, u0, u1):
            for u in range(u0, u1):
                for jh in range(2):
                    r = park0[ti, jh, u]
                    nc.sync.dma_start(
                        out=xs[ti][u][jh:P:2, :].bitcast(F32),
                        in_=out[r : r + unit_rows(UNITS[ti][u][1]), :].rearrange("r c -> (r c)").partition_broadcast(P // 2),
                    )

        b_rows_f = const.tile([P, P], F32)
        b_cols = y_psum.tile([P, P], F32, tag="y", name="b_cols")
        bias = const.tile([P, CT], F32)
        neg_b = const.tile([P, CT], F32)
        nv_b = {}
        nv = {(ti, ct): len(users(ti, "V", ct)) for ti in range(ntile) for ct in range(CT)}

        def turn_bias():
            nc.scalar.copy(out=b_rows_f[:], in_=b_rows[:])
            nc.tensor.transpose(b_cols[:], b_rows_f[:], ident[:])

        def save_bias():
            nc.scalar.copy(out=bias[:], in_=b_cols[:, 0:CT])
            nc.scalar.mul(out=neg_b[:], in_=b_cols[:, 0:CT], mul=-1.0)
            for n in sorted(set(nv.values()) - {0}):
                nv_b[n] = const.tile([P, CT], F32, name="nv_b%d" % n)
                nc.scalar.mul(out=nv_b[n][:], in_=b_cols[:, 0:CT], mul=float(n))

        fold = const.tile([P, P], F32, name="fold")

        interleave_x0(0)
        park_x0(0, 0, 1)
        park_x0(0, 1, len(UNITS[0]))
        nc.sync.dma_start(out=b_rows[0:CT, :], in_=b3.rearrange("(r c) -> r c", c=P))
        nc.gpsimd.memset(fold[:], 0.0)
        nc.gpsimd.tensor_tensor(out=fold[:, 0 : P // 2], in0=ident[:, 0 : P // 2], in1=ident[:, P // 2 : P], op=ALU.add)

        x_rows = const.tile([P, 2 * DC, P], F32, name="x_rows")
        nc.vector.tensor_copy(
            out=x_rows[:].rearrange("p a (fl jh) -> p a fl jh", jh=2),
            in_=x2[:, 0]
            .rearrange("p jh d t -> p jh (d t)")
            .bitcast(F32)[:, :, 0 : 2 * DC]
            .rearrange("p jh a -> p a jh")
            .unsqueeze(2)
            .to_broadcast([P, 2 * DC, P // 2, 2]),
        )
        nc.sync.dma_start(out=w_words[:].bitcast(I32), in_=W3_words.bitcast(I32).rearrange("g p n -> p g n"))
        for quad in range(4):
            nc.sync.dma_start(
                out=w_scales[32 * quad : 32 * quad + 4].bitcast(I32),
                in_=W3_scales[:, 4 * quad : 4 * quad + 4, :].bitcast(I32).rearrange("g r n -> r g n"),
            )
        spread_x0(0, 0, 1)
        if X1_LATE:
            for ti in range(1, ntile):
                load_x0(ti)
        spread_x0(0, 1, len(UNITS[0]))
        load_h2(1)

        def late_loads():
            for ti in range(1, ntile):
                park_x0(ti, 0, len(UNITS[ti]))
            spread_x0(1, 0, len(UNITS[1]))
            load_h2(2)
            spread_x0(2, 0, len(UNITS[2]))

        h2e = {}
        h4 = {}
        batch = {}
        gsum = {}
        GCTS = [ct for ct in range(CT) if any([o[ct] == "G" for o in OWN8])]
        NG = len(GCTS)

        def h2_slots(c, i0, n, f0, nf):
            ti, k = CHUNKS[c]
            return h2_sb[ti][:, SHIFT : SHIFT + H2 * D].rearrange("p (f d) -> p d f", d=D)[
                :, DC * k + i0 : DC * k + i0 + n, f0 : f0 + nf
            ]

        def new_h4(c):
            h4[c] = work.tile([P, DC, 4 * H2], BF16, name="h4", bufs=H_AHEAD - T_AHEAD + 2)

        def twofold_first(g):
            nc.vector.tensor_copy(
                out=h2r[0][:, :, P * g : P * (g + 1)].rearrange("p i (f r) -> p i f r", r=2),
                in_=h2_sb[0][:, SHIFT + FL * D * g : SHIFT + FL * D * (g + 1)]
                .rearrange("p (f d) -> p d f", d=D)[:, 0:DC]
                .unsqueeze(3)
                .to_broadcast([P, DC, FL, 2]),
            )

        h2r = {}

        def new_h2r(c):
            h2r[c] = work.tile([P, DC, 2 * H2], BF16, name="h2r", bufs=H_AHEAD - T_AHEAD + 2)

        def twofold(c, i0, i1):
            nc.scalar.copy(
                out=h2r[c][:, i0:i1, :].rearrange("p i (f r) -> p i f r", r=2),
                in_=h2_slots(c, i0, i1 - i0, 0, H2).unsqueeze(3).to_broadcast([P, i1 - i0, H2, 2]),
            )

        new_h2r(0)
        twofold_first(0)
        x_first = const.tile([P, DC, P, 4], BF16, name="x_first")
        x_cols = []
        for h in range(2):
            x_cols_h = y_psum.tile([P, DC, P], F32, tag="y", name="x_cols%d" % h)
            x_cols.append(x_cols_h)
            for a in range(DC):
                nc.tensor.transpose(x_cols_h[:, a, :], x_rows[:, DC * h + a, :], ident[:])

        def save_first(h, copy):
            copy(
                out=x_first[:, 2 * h : 2 * h + 2].rearrange("p i r t -> p i (r t)").bitcast(F32).rearrange("p i (r tp) -> p i r tp", tp=2),
                in_=x_cols[h][:].rearrange("p (i tp) r -> p i r tp", tp=2),
            )

        save_first(0, nc.scalar.copy)
        save_first(1, nc.scalar.copy if XF else nc.vector.tensor_copy)
        twofold_first(1)


        h_t = {}
        z = {}
        z_codes = {}
        z_scales = {}
        y = {}
        y_relu = {}
        acc = {}
        sums = {}
        acc_sb = {}
        done = {}
        folded = {}

        def new_h2e(c):
            h2e[c] = work.tile([P, g_slots(c), 2 * H2], BF16, name="h2e%d" % g_slots(c), bufs=H2E_BUFS)

        def double_values(c, i0, n):
            nc.gpsimd.tensor_scalar(
                out=h2e[c][:, i0 : i0 + n, :].rearrange("p i (f e) -> p i f e", e=2),
                in0=h2_slots(c, i0, n, 0, H2).unsqueeze(3).to_broadcast([P, n, H2, 2]),
                scalar1=1.0,
                scalar2=0.0,
                op0=ALU.mult,
                op1=ALU.add,
            )

        def double_words(c, i):
            nc.scalar.copy(
                out=h4[c][:, i, :].bitcast(F32).rearrange("p (f r) -> p f r", r=2),
                in_=h2e[c][:, i, :].bitcast(F32).unsqueeze(2).to_broadcast([P, H2, 2]),
            )

        def fourfold_vector(c, i):
            n = DC - i
            nc.vector.tensor_copy(
                out=h4[c][:, i:DC, :].rearrange("p i (f q) -> p i f q", q=4),
                in_=h2_slots(c, i, n, 0, H2).unsqueeze(3).to_broadcast([P, n, H2, 4]),
            )

        def double_words_pair(c, i0, i1):
            nc.scalar.copy(
                out=h4[c][:, i0:i1, :].bitcast(F32).rearrange("p i (f r) -> p (i f) r", r=2),
                in_=h2e[c][:, i0:i1, :].bitcast(F32).rearrange("p i f -> p (i f)").unsqueeze(2).to_broadcast([P, (i1 - i0) * H2, 2]),
            )

        def fourfold_pair(c, i0, i1):
            nc.scalar.copy(
                out=h4[c][:, i0:i1, :].rearrange("p i (f q) -> p i f q", q=4),
                in_=h2_slots(c, i0, i1 - i0, 0, H2).unsqueeze(3).to_broadcast([P, i1 - i0, H2, 4]),
            )

        def fourfold_scalar(c, i):
            nc.scalar.copy(
                out=h4[c][:, i, :].rearrange("p (f q) -> p f q", q=4),
                in_=h2_slots(c, i, 1, 0, H2).rearrange("p i f -> p (i f)").unsqueeze(2).to_broadcast([P, H2, 4]),
            )

        def turn_h2(c, g):
            if by_matmul(c):
                h_t[c, g] = t_psum.tile([P, P, DC, 2], BF16, name="h_t")
                for i in range(DC):
                    nc.tensor.matmul(
                        out=h_t[c, g][:, :, i, :],
                        lhsT=h2r[c][:, i, P * g : P * (g + 1)],
                        rhs=twice[:].rearrange("p (m e) -> p m e", e=2),
                        start=True,
                        stop=True,
                    )
                return
            h_t[c, g] = t_psum.tile([P, DC, P], F32, name="h_t")
            for i in range(DC):
                nc.tensor.transpose(h_t[c, g][:, i, :], h4[c][:, i, 2 * H2 * g : 2 * H2 * (g + 1)].bitcast(F32), ident[:])

        def multiply(c, g):
            ti, k = CHUNKS[c]
            if g == 0:
                z[c] = work.tile([P, G, NCOL, 4], BF16, name="z", bufs=Z_BUFS, align_bytes=64)
            u, first = unit_of(c) if c > 0 else (0, 0)
            if by_matmul(c):
                nc.vector.tensor_tensor(
                    out=z[c][:, g].rearrange("p (r i) (tp e) -> p r i tp e", i=DC, tp=2),
                    in0=h_t[c, g][:].unsqueeze(3).to_broadcast([P, P, DC, 2, 2]),
                    in1=(
                        x_first[:].rearrange("p i r (tp e) -> p r i tp e", tp=2)
                        if c == 0
                        else xs[ti][u][:].rearrange("p (r d tp e) -> p r d tp e", d=UNITS[ti][u][1], tp=2, e=2)[:, :, first : first + DC]
                    ),
                    op=ALU.mult,
                )
                return
            nc.vector.tensor_tensor(
                out=z[c][:, g].rearrange("p (i r) (tp e) -> p i r tp e", i=DC, tp=2),
                in0=h_t[c, g][:].rearrange("p i r -> p (i r)").bitcast(BF16)
                .rearrange("p (i r e) -> p i r e", i=DC, e=2)
                .unsqueeze(3)
                .to_broadcast([P, DC, P, 2, 2]),
                in1=(
                    x_first[:].rearrange("p i r (tp e) -> p i r tp e", tp=2)
                    if c == 0
                    else xs[ti][u][:].rearrange("p (r d tp e) -> p d r tp e", d=UNITS[ti][u][1], tp=2, e=2)[:, first : first + DC]
                ),
                op=ALU.mult,
            )

        def quantise(c):
            z_codes[c] = work.tile([P, G, NCOL], U32, name="z_codes", bufs=3, align_bytes=64)
            z_scales[c] = work.tile([P, G, NCOL], U8, name="z_scales", bufs=3, align_bytes=64)
            nc.vector.quantize_mx(
                out=z_codes[c][:].rearrange("p g n -> p (g n)").bitcast(FP8X4),
                scales=z_scales[c][:].rearrange("p g n -> p (g n)"),
                in_=z[c][:].rearrange("p g n t -> p (g n t)"),
            )

        def multiply_mx(c, ct):
            y[c, ct] = y_psum.tile([P, NCOL], F32, name="y", tag="y")
            for g in range(G):
                nc.tensor.matmul_mx(
                    out=y[c, ct][:],
                    lhsT=w_words[:, g, 2 * P * ct : 2 * P * (ct + 1)].bitcast(FP4X4),
                    lhsT_scale=w_scales[:, g, P * ct : P * (ct + 1)],
                    rhs=z_codes[c][:, g, :].bitcast(FP8X4),
                    rhs_scale=z_scales[c][:, g, :],
                    start=(g == 0),
                    stop=(g == G - 1),
                )

        def by_slot(c, columns):
            if by_matmul(c):
                return columns.rearrange("p (r i) -> p i r", i=DC)
            return columns.rearrange("p (i r) -> p i r", i=DC)

        def relu_add_vector(c, ct):
            ti = CHUNKS[c][0]
            if c == users(ti, "V", ct)[0]:
                sums[ti, "V", ct] = work.tile([P, NCOL], F32, name="sum_v%d" % ct, bufs=2)
                nc.vector.tensor_scalar(
                    out=sums[ti, "V", ct][:].rearrange("p (i r) -> p i r", i=DC),
                    in0=by_slot(c, y[c, ct][:]),
                    scalar1=neg_b[:, ct : ct + 1],
                    scalar2=nv_b[nv[ti, ct]][:, ct : ct + 1],
                    op0=ALU.max,
                    op1=ALU.add,
                )
            else:
                nc.vector.scalar_tensor_tensor(
                    out=sums[ti, "V", ct][:].rearrange("p (i r) -> p i r", i=DC),
                    in0=by_slot(c, y[c, ct][:]),
                    scalar=neg_b[:, ct : ct + 1],
                    in1=sums[ti, "V", ct][:].rearrange("p (i r) -> p i r", i=DC),
                    op0=ALU.max,
                    op1=ALU.add,
                )

        def relu_scalar(c, ct):
            ti = CHUNKS[c][0]
            if owner(c, ct) == "G":
                if c not in batch:
                    first_c = CHUNKS[c][1] == 0
                    if first_c:
                        sum_g = work.tile([P, NG, NCOL], F32, name="sum_g", bufs=2)
                        batch[c] = sum_g
                        for lane in range(NG):
                            sums[ti, "G", GCTS[lane]] = batch[c][:, lane, :]
                        gsum[ti] = batch[c]
                    else:
                        y_relu_g = work.tile([P, NG, NCOL], F32, name="y_relu_g", bufs=4)
                        batch[c] = y_relu_g
                y_relu[c, ct] = batch[c][:, GCTS.index(ct), :]
            else:
                y_relu[c, ct] = work.tile([P, NCOL], F32, name="y_relu", bufs=8)
            columns = y_relu[c, ct] if owner(c, ct) == "G" else y_relu[c, ct][:]
            nc.scalar.activation(out=columns.rearrange("p (i r) -> p i r", i=DC), in_=by_slot(c, y[c, ct][:]), func=RELU, bias=bias[:, ct : ct + 1], scale=1.0)

        def add_gpsimd(c):
            ti = CHUNKS[c][0]
            n = len([ct for ct in range(CT) if owner(c, ct) == "G"])
            if n and CHUNKS[c][1] > 0:
                dst = gsum[ti][:, 0:n, :].rearrange("p l n -> p (l n)")
                nc.gpsimd.tensor_tensor(out=dst, in0=dst, in1=batch[c][:, 0:n, :].rearrange("p l n -> p (l n)"), op=ALU.add)

        def n_adds(ti):
            return DC * (sum([len(users(ti, "T", ct)) for ct in range(CT)]) + len(SUMS[ti]))

        def add_up(ti, ct, columns):
            if ti not in acc:
                acc[ti] = a_psum.tile([P, CT, P], F32, name="acc")
                done[ti] = 0
            for i in range(DC):
                nc.tensor.matmul(
                    out=acc[ti][:, ct, :],
                    lhsT=columns[:, i * P : (i + 1) * P],
                    rhs=ident[:],
                    is_transpose=True,
                    start=(done[ti] == 0),
                    stop=(done[ti] == n_adds(ti) - 1),
                )
                done[ti] += 1

        def save_sums(ti):
            acc_sb[ti] = work.tile([P, L3], F32, name="acc_sb", bufs=2)
            b0, nb = TILES[ti]
            if ti == ntile - 1 and SPLIT_END:
                half = L3 // 2
                nc.scalar.copy(out=acc_sb[ti][:, 0:half], in_=acc[ti][:, 0 : CT // 2].rearrange("p ct c -> p (ct c)"))
                nc.vector.tensor_copy(out=acc_sb[ti][:, half:L3], in_=acc[ti][:, CT // 2 : CT].rearrange("p ct c -> p (ct c)"))
                nc.sync.dma_start(out=out[b0 : b0 + nb, 0:half], in_=acc_sb[ti][:, 0:half])
                nc.scalar.dma_start(out=out[b0 : b0 + nb, half:L3], in_=acc_sb[ti][:, half:L3])
                return
            nc.scalar.copy(out=acc_sb[ti][:], in_=acc[ti][:].rearrange("p ct c -> p (ct c)"))
            if nb == P:
                nc.sync.dma_start(out=out[b0 : b0 + nb, :], in_=acc_sb[ti][:])

        def fold_gpsimd(ti):
            b0, nb = TILES[ti]
            nc.sync.dma_start(out=out[b0 : b0 + nb, :], in_=acc_sb[ti][nb:P, :])
            upper = work.tile([P, L3], F32, name="upper", bufs=1)
            nc.sync.dma_start(out=upper[0:nb, :], in_=out[b0 : b0 + nb, :])
            upper_of[ti] = upper

        def fold_add(ti):
            b0, nb = TILES[ti]
            out_sb = work.tile([P, L3], F32, name="out_sb", bufs=1)
            nc.gpsimd.tensor_tensor(out=out_sb[0:nb, :], in0=acc_sb[ti][0:nb, :], in1=upper_of[ti][0:nb, :], op=ALU.add)
            nc.sync.dma_start(out=out[b0 : b0 + nb, :], in_=out_sb[0:nb, :])

        upper_of = {}

        def fold_sums(ti):
            if FOLD_G:
                fold_gpsimd(ti)
                return
            folded[ti] = y_psum.tile([P, L3], F32, name="folded", tag="y")
            nc.tensor.matmul(out=folded[ti][:], lhsT=fold[:], rhs=acc_sb[ti][:], start=True, stop=True)
            b0, nb = TILES[ti]
            out_sb = work.tile([P, L3], F32, name="out_sb", bufs=1)
            nc.scalar.copy(out=out_sb[:], in_=folded[ti][:])
            nc.sync.dma_start(out=out[b0 : b0 + nb, :], in_=out_sb[0:nb, :])

        def live(c):
            return 0 <= c < NCHUNK

        def st_adds(s):
            if live(s - 1):
                add_gpsimd(s - 1)

        def st_dbl(s):
            if live(s + E_AHEAD) and s + E_AHEAD > 0:
                if g_slots(s + E_AHEAD):
                    new_h2e(s + E_AHEAD)
                c = s + E_AHEAD
                for i in range(0, g_slots(c), E_SLOTS):
                    double_values(c, i, min(E_SLOTS, g_slots(c) - i))

        def st_mx(s, cts):
            if live(s):
                for ct in cts:
                    multiply_mx(s, ct)
                    if owner(s, ct) != "V":
                        relu_scalar(s, ct)

        def st_vrelu(s):
            c = s - V_LAG
            if live(c):
                for ct in range(CT):
                    if owner(c, ct) == "V":
                        relu_add_vector(c, ct)

        def st_words(s, part):
            if live(s + H_AHEAD) and s + H_AHEAD > 0:
                if by_matmul(s + H_AHEAD):
                    if part == 0:
                        new_h2r(s + H_AHEAD)
                    if S_NEW == 1:
                        if part == 0:
                            twofold(s + H_AHEAD, 0, DC)
                    else:
                        twofold(s + H_AHEAD, 2 * part, 2 * part + 2)
                    return
                if part == 0:
                    new_h4(s + H_AHEAD)
                order = (2, 3, 0, 1) if S_FIRST else (0, 1, 2, 3)
                if MERGE:
                    c = s + H_AHEAD
                    if part == 0 and g_slots(c) < DC:
                        fourfold_pair(c, g_slots(c), DC)
                    if part == 1 - (S_SPLIT == 0) and g_slots(c) > 0:
                        double_words_pair(c, 0, g_slots(c))
                    continue_ = False
                else:
                    continue_ = True
                for i in () if not continue_ else (order if S_SPLIT == 0 and part == 0 else () if S_SPLIT == 0 else order[0:2] if part == 0 else order[2:4]):
                    if i < g_slots(s + H_AHEAD):
                        double_words(s + H_AHEAD, i)
                    elif i < DC - V_SLOTS:
                        fourfold_scalar(s + H_AHEAD, i)

        def opens_bank(c):
            return A_BUFS == 1 and 0 < c < NCHUNK and CHUNKS[c][1] == 0

        def st_acc(s, cts):
            for c in (s - 2, s - 1):
                if live(c) and (opens_bank(c) if c == s - 2 else not opens_bank(c)):
                    for ct in cts:
                        if owner(c, ct) == "T":
                            add_up(CHUNKS[c][0], ct, y_relu[c, ct])

        def st_flush(s):
            for ti in range(ntile):
                for (who, ct) in SUMS[ti]:
                    if s == flush_step(ti, who, ct):
                        add_up(ti, ct, sums[ti, who, ct])
                if s == finish_step(ti):
                    save_sums(ti)

        def st_turn(s, g):
            if live(s + T_AHEAD):
                turn_h2(s + T_AHEAD, g)

        for s in range(-E_AHEAD, NCHUNK + 1 + G_FLUSH):
            if s == X2_STEP:
                for ti in range(1, ntile):
                    interleave_x0(ti)
            if s == -2:
                turn_bias()
            if s == -Q_AHEAD:
                quantise(0)
                save_bias()
            if s < 0 and EARLY_WORDS:
                st_words(s, 0)
                st_words(s, 1)
            if s == -1:
                if WARM2:
                    idle_y2 = y_psum.tile([P, NCOL], F32, tag="y", name="idle_y2")
                    for i in range(WARM2):
                        nc.tensor.matmul(out=idle_y2[:], lhsT=idle[:, 0:P], rhs=idle[:], start=True, stop=True)
                st_mx(0, (0, 1))
            if live(s + M_AHEAD):
                multiply(s + M_AHEAD, 0)
            if s == -Q_AHEAD:
                late_loads()
            for ti in range(ntile):
                if FOLD_G and s == (FOLD_AT if FOLD_AT else finish_step(ti) + 4) and TILES[ti][1] < P:
                    fold_add(ti)
            if G_ORDER == 0:
                st_adds(s)
                st_dbl(s)
            else:
                st_dbl(s)
                st_adds(s)
            if S_POS == 0 and not (s < 0 and EARLY_WORDS):
                st_words(s, 0)
            if PE_ORDER:
                if PE_ORDER == 1:
                    st_turn(s, 0)
                    st_turn(s, 1)
                st_acc(s, (0, 1, 2, 3))
                st_flush(s)
                if PE_ORDER == 2:
                    st_turn(s, 0)
                    st_turn(s, 1)
            if LAST and s == NCHUNK - 1:
                st_acc(s, (0, 1, 2, 3))
            if s > 0:
                st_mx(s, (0, 1))
            if V_POS == 0:
                st_vrelu(s)
            if live(s + Q_AHEAD) and s + Q_AHEAD > 0:
                quantise(s + Q_AHEAD)
            if V_POS == 1:
                st_vrelu(s)
            if S_POS == 1:
                st_words(s, 0)
            for ti in range(ntile):
                if s == finish_step(ti) + 1 and TILES[ti][1] < P:
                    fold_sums(ti)
            if PE_ORDER == 0 and not (LAST and s == NCHUNK - 1):
                st_acc(s, (0, 1, 2, 3) if RUNS == 1 else (0, 1))
            if PE_ORDER:
                if live(s + M_AHEAD):
                    multiply(s + M_AHEAD, 1)
                if V_SLOTS and live(s + H_AHEAD) and s + H_AHEAD > 0:
                    fourfold_vector(s + H_AHEAD, DC - V_SLOTS)
                if V_POS == 2:
                    st_vrelu(s)
                st_mx(s, (2, 3))
            elif RUNS == 1:
                st_flush(s)
                st_turn(s, 0)
                st_turn(s, 1)
                if live(s + M_AHEAD):
                    multiply(s + M_AHEAD, 1)
                if V_SLOTS and live(s + H_AHEAD) and s + H_AHEAD > 0:
                    fourfold_vector(s + H_AHEAD, DC - V_SLOTS)
                if V_POS == 2:
                    st_vrelu(s)
                st_mx(s, (2, 3))
            else:
                st_turn(s, 0)
                if live(s + M_AHEAD):
                    multiply(s + M_AHEAD, 1)
                if V_SLOTS and live(s + H_AHEAD) and s + H_AHEAD > 0:
                    fourfold_vector(s + H_AHEAD, DC - V_SLOTS)
                if V_POS == 2:
                    st_vrelu(s)
                st_mx(s, (2, 3))
                st_acc(s, (2, 3))
                st_flush(s)
                st_turn(s, 1)
            if not (s < 0 and EARLY_WORDS):
                st_words(s, 1)
            if S_POS == 2:
                st_words(s, 0)
